import numpy as np
import ml_dtypes


def mxq(x, axis, fmt="e4m3"):
    dtype, down = {"e4m3": (ml_dtypes.float8_e4m3fn, 7), "e5m2": (ml_dtypes.float8_e5m2, 14)}[fmt]
    v = np.moveaxis(np.asarray(x, np.float32).astype(ml_dtypes.bfloat16).astype(np.float64), axis, -1)
    blocks = v.reshape(v.shape[:-1] + (-1, 32))
    amax = np.abs(blocks).max(-1, keepdims=True)
    byte = np.maximum(np.where(amax > 0, np.frexp(amax)[1] - 1 + 127, 0) - down, 1)
    scale = np.exp2(byte - 127.0)
    codes = (blocks / scale).astype(np.float32).astype(dtype).astype(np.float64)
    return np.moveaxis((codes * scale).reshape(v.shape), -1, axis)


WIDE = False


def mx_kscale(k):
    if not WIDE:
        return np.ones(k)
    levels = np.array([10, -10, 5, -5, 0])
    a = np.random.permutation(np.resize(levels, k // 512 * 4)).reshape(k // 512, 4)
    idx = np.arange(k)
    return np.exp2(a[idx // 512, idx % 128 // 32])


BF16 = ml_dtypes.bfloat16


def bf(x):
    return np.asarray(x, np.float32).astype(BF16)


def f64(x):
    return np.asarray(x).astype(np.float64)


B, S, HID, H, HKV, D, NU = 1, 1024, 1024, 4, 2, 256, 3
G = H // HKV
F = D * 2 * NU
EPS = 1e-8


def dpfp(x):
    x = np.concatenate([np.maximum(x, 0.0), np.maximum(-x, 0.0)], axis=-1)
    rolled = np.concatenate([np.roll(x, j, axis=-1) for j in range(1, NU + 1)], axis=-1)
    rep = np.concatenate([x] * NU, axis=-1)
    return rep * rolled


def l2_normalize(x):
    n = np.sqrt(np.sum(x * x, axis=-1, keepdims=True))
    return x / np.maximum(n, 1e-12)


def sigmoid(a):
    return 1.0 / (1.0 + np.exp(-a))


def setup_inputs():
    s = mx_kscale(HID)
    lev = np.linspace(0.8, 1.3, H)[:, None]
    return {"hidden_states": bf(np.random.standard_normal((S, HID)) * s),
            "k": bf(np.random.standard_normal((HKV, S, D))),
            "Wv": bf(np.random.standard_normal((HKV * D, HID)) / np.sqrt(HID) / s[None, :]),
            "bv": bf(np.random.standard_normal(HKV * D) * 0.1),
            "Wmb": bf(np.random.standard_normal((HID, HID)) / np.sqrt(HID) / s[None, :]),
            "bmb": bf(np.random.standard_normal(HID) * 0.3),
            "memory": bf(np.random.standard_normal((H, F, D)) * 0.5),
            "norm": bf(np.random.random((H, F)) * lev * 2.0 * np.pi / np.sqrt(F))}


def reference(hidden_states, k, Wv, bv, Wmb, bmb, memory, norm):
    mem, nrm = f64(memory), f64(norm)
    mk = l2_normalize(dpfp(f64(k)))
    num = mxq(mk, 2, "e4m3")[:, None] @ mxq(mem, 1, "e4m3").reshape(HKV, G, F, D)
    denom = np.sum(mk[:, None] * nrm.reshape(HKV, G, F)[:, :, None, :], axis=-1, keepdims=True) + EPS
    prev_v = num / denom
    hq = mxq(f64(hidden_states), 1, "e4m3")
    v = ((hq @ mxq(f64(Wv), 1, "e4m3").T) + f64(bv)).reshape(S, HKV, D).transpose(1, 0, 2)
    mb = sigmoid((hq @ mxq(f64(Wmb), 1, "e4m3").T) + f64(bmb))
    mb = mb.reshape(S, HKV, G, D).transpose(1, 2, 0, 3)
    wmv = (v[:, None] - prev_v) * mb
    delta_memory = mxq(mk, 1, "e4m3").transpose(0, 2, 1)[:, None] @ mxq(wmv, 2, "e4m3")
    return mem + delta_memory.reshape(H, F, D)

@@ -1,0 +1,380 @@
+from contextlib import ExitStack
+
+import concourse.mybir as mybir
+from concourse.masks import make_identity
+
+F32 = mybir.dt.float32
+BF16 = mybir.dt.bfloat16
+U32 = mybir.dt.uint32
+U8 = mybir.dt.uint8
+FP8X4 = mybir.dt.float8_e4m3fn_x4
+ACT = mybir.ActivationFunctionType
+ALU = mybir.AluOpType
+
+P = 128
+PACK = 4
+K_PASS = P * PACK
+BANK = 512
+
+S = 1024
+HID = 1024
+D = 256
+H = 4
+HKV = 2
+PAIR = H // HKV
+NU = 3
+X2 = 2 * D
+F = NU * X2
+EPS = 1e-8
+TINY = 1e-12
+
+S_TILES = S // P
+S_PASSES = S // K_PASS
+HID_PASSES = HID // K_PASS
+F_PASSES = F // K_PASS
+W_ROWS = HKV * D + HID
+ROW_UNIT = 256
+
+FLOPS = 2 * S * HID * W_ROWS + 2 * 2 * H * S * F * D
+
+
+def quantise(nc, grouped, codes, scales):
+    nc.vector.quantize_mx(
+        out=codes.bitcast(FP8X4),
+        scales=scales,
+        in_=grouped.rearrange("p c t -> p (c t)"),
+    )
+
+
+def mx_group(nc, bank, passes, lhs_codes, lhs_scales, rhs_codes, rhs_scales):
+    for g in range(passes):
+        nc.tensor.matmul_mx(
+            out=bank,
+            lhsT=lhs_codes(g).bitcast(FP8X4),
+            lhsT_scale=lhs_scales(g),
+            rhs=rhs_codes(g).bitcast(FP8X4),
+            rhs_scale=rhs_scales(g),
+            start=(g == 0),
+            stop=(g == passes - 1),
+        )
+
+
+def tile_armtapproach_pa_kernel(
+    tc, hidden_states, k, Wv, bv, Wmb, bmb, memory, norm, out
+):
+    nc = tc.nc
+    with ExitStack() as whole:
+        keep = whole.enter_context(tc.tile_pool(name="keep", bufs=1))
+
+        ident = keep.tile([P, P], F32)
+        make_identity(nc, ident[:])
+
+        bias_v = keep.tile([P, HKV * D], BF16)
+        nc.scalar.dma_start(out=bias_v[:], in_=bv.partition_broadcast(P))
+        bias_mb = keep.tile([P, HID], BF16)
+        nc.scalar.dma_start(out=bias_mb[:], in_=bmb.partition_broadcast(P))
+
+        hs_codes = keep.tile([P, HID_PASSES, S], U32, align_bytes=64)
+        hs_scales = keep.tile([P, HID_PASSES, S], U8, align_bytes=64)
+        w_codes = keep.tile([P, HID_PASSES, W_ROWS], U32, align_bytes=64)
+        w_scales = keep.tile([P, HID_PASSES, W_ROWS], U8, align_bytes=64)
+        mem_codes = keep.tile([P, HKV, F_PASSES, PAIR * D], U32, align_bytes=64)
+        mem_scales = keep.tile([P, HKV, F_PASSES, PAIR * D], U8, align_bytes=64)
+        mkT_codes = keep.tile([P, HKV, F_PASSES, S], U32, align_bytes=64)
+        mkT_scales = keep.tile([P, HKV, F_PASSES, S], U8, align_bytes=64)
+        mkS_codes = keep.tile([P, HKV, S_PASSES, F], U32, align_bytes=64)
+        mkS_scales = keep.tile([P, HKV, S_PASSES, F], U8, align_bytes=64)
+        neg_inv_denom = keep.tile([P, HKV, S_TILES, PAIR], F32)
+
+        with tc.tile_pool(name="feat", bufs=2) as feat, tc.tile_pool(
+            name="stage", bufs=2
+        ) as stage, tc.psum_pool(name="flip_banks", bufs=6) as flip_banks:
+            norm_rows = feat.tile([P, H, F], BF16, bufs=1)
+            nc.scalar.dma_start(
+                out=norm_rows[:].rearrange("p h f -> p (h f)"),
+                in_=norm.rearrange("h f -> (h f)").partition_broadcast(P),
+            )
+
+            for c in range(HKV):
+                for sg in range(S_PASSES):
+                    k_rows = feat.tile([P, PACK, D], BF16)
+                    nc.sync.dma_start(
+                        out=k_rows[:],
+                        in_=k[c, sg * K_PASS : (sg + 1) * K_PASS, :].rearrange(
+                            "(t p) d -> p t d", p=P
+                        ),
+                    )
+                    mk_planes = feat.tile([P, PACK, F], BF16)
+                    for a in range(PACK // 2):
+                        x = k_rows[:, 2 * a : 2 * a + 2, :]
+                        x2 = feat.tile([P, 2, NU + X2 + 1], BF16)
+                        nc.scalar.activation(out=x2[:, :, NU : NU + D], in_=x, func=ACT.Relu)
+                        nc.scalar.activation(
+                            out=x2[:, :, NU + D : NU + X2], in_=x, func=ACT.Relu, scale=-1.0
+                        )
+                        nc.scalar.activation(
+                            out=x2[:, :, 0:NU], in_=x[:, :, D - NU : D], func=ACT.Relu, scale=-1.0
+                        )
+                        phi = feat.tile([P, 2, F], F32)
+                        for j in range(1, NU + 1):
+                            nc.vector.tensor_tensor(
+                                out=phi[:, :, (j - 1) * X2 : j * X2],
+                                in0=x2[:, :, NU : NU + X2],
+                                in1=x2[:, :, NU - j : NU - j + X2],
+                                op=ALU.mult,
+                            )
+                        sum_sq = feat.tile([P, 2], F32)
+                        dots = feat.tile([P, 2, PAIR], F32)
+                        for b in range(2):
+                            squares = feat.tile([P, F], BF16)
+                            nc.scalar.activation(
+                                out=squares[:],
+                                in_=phi[:, b, :],
+                                func=ACT.Square,
+                                accum_out=sum_sq[:, b : b + 1],
+                            )
+                            for h2 in range(PAIR):
+                                weighted = feat.tile([P, F], F32)
+                                nc.vector.scalar_tensor_tensor(
+                                    out=weighted[:],
+                                    in0=phi[:, b, :],
+                                    scalar=1.0,
+                                    in1=norm_rows[:, PAIR * c + h2, :],
+                                    op0=ALU.mult,
+                                    op1=ALU.mult,
+                                    accum_out=dots[:, b, h2 : h2 + 1],
+                                )
+                        nc.vector.tensor_scalar_max(
+                            out=sum_sq[:], in0=sum_sq[:], scalar1=TINY * TINY
+                        )
+                        length = feat.tile([P, 2], F32)
+                        nc.scalar.activation(out=length[:], in_=sum_sq[:], func=ACT.Sqrt)
+                        inv_norm = feat.tile([P, 2], F32)
+                        nc.vector.reciprocal(out=inv_norm[:], in_=length[:])
+                        denom = feat.tile([P, 2, PAIR], F32)
+                        nc.vector.tensor_tensor(
+                            out=denom[:],
+                            in0=dots[:],
+                            in1=inv_norm[:].unsqueeze(2).to_broadcast([P, 2, PAIR]),
+                            op=ALU.mult,
+                        )
+                        nc.vector.tensor_scalar(
+                            out=denom[:],
+                            in0=denom[:],
+                            scalar1=-1.0,
+                            scalar2=-EPS,
+                            op0=ALU.mult,
+                            op1=ALU.add,
+                        )
+                        st0 = PACK * sg + 2 * a
+                        nc.vector.reciprocal(out=neg_inv_denom[:, c, st0 : st0 + 2, :], in_=denom[:])
+                        for b in range(2):
+                            nc.scalar.activation(
+                                out=mk_planes[:, 2 * a + b, :],
+                                in_=phi[:, b, :],
+                                func=ACT.Copy,
+                                scale=inv_norm[:, b : b + 1],
+                            )
+
+                    mkS_grouped = feat.tile([P, F, PACK], BF16, bufs=1, align_bytes=64)
+                    for g in range(F_PASSES):
+                        f_cols = slice(g * X2, (g + 1) * X2)
+                        nc.vector.tensor_copy(
+                            out=mkS_grouped[:, f_cols, :],
+                            in_=mk_planes[:, :, f_cols].rearrange("p t f -> p f t"),
+                        )
+                    for g in range(F_PASSES):
+                        f_cols = slice(g * X2, (g + 1) * X2)
+                        quantise(
+                            nc,
+                            mkS_grouped[:, f_cols, :],
+                            mkS_codes[:, c, sg, f_cols],
+                            mkS_scales[:, c, sg, f_cols],
+                        )
+
+                    for g in range(F_PASSES):
+                        mkT_grouped = feat.tile([P, K_PASS, PACK], BF16, align_bytes=64)
+                        mkT_words = mkT_grouped[:].bitcast(F32)
+                        for a in range(PACK // 2):
+                            flipped = flip_banks.tile([P, 2, 2, P], F32, tag="bank")
+                            for b in range(2):
+                                plane_words = mk_planes[:, 2 * a + b, :].bitcast(F32)
+                                for u in range(2):
+                                    w0 = (2 * g + u) * P
+                                    nc.tensor.transpose(
+                                        flipped[:, b, u, :], plane_words[:, w0 : w0 + P], ident[:]
+                                    )
+                            nc.scalar.copy(
+                                out=mkT_words[:, 2 * a * P : (2 * a + 2) * P, :].rearrange(
+                                    "q (b r) u -> q b r u", b=2
+                                ),
+                                in_=flipped[:].rearrange("q b u r -> q b r u"),
+                            )
+                        s_cols = slice(sg * K_PASS, (sg + 1) * K_PASS)
+                        quantise(
+                            nc, mkT_grouped[:], mkT_codes[:, c, g, s_cols], mkT_scales[:, c, g, s_cols]
+                        )
+
+            def stage_rows(rows, codes, scales):
+                grouped = stage.tile([P, HID_PASSES, ROW_UNIT, PACK], BF16, align_bytes=64)
+                grouped_words = grouped[:].bitcast(F32)
+                for rt in range(ROW_UNIT // P):
+                    raw = stage.tile([P, HID], BF16)
+                    nc.sync.dma_start(out=raw[:], in_=rows[rt * P : (rt + 1) * P, :])
+                    raw_words = raw[:].bitcast(F32)
+                    flipped = flip_banks.tile([P, HID_PASSES, 2, P], F32, tag="bank")
+                    for g in range(HID_PASSES):
+                        for u in range(2):
+                            w0 = (2 * g + u) * P
+                            nc.tensor.transpose(
+                                flipped[:, g, u, :], raw_words[:, w0 : w0 + P], ident[:]
+                            )
+                    nc.scalar.copy(
+                        out=grouped_words[:, :, rt * P : (rt + 1) * P, :],
+                        in_=flipped[:].rearrange("q g u r -> q g r u"),
+                    )
+                for g in range(HID_PASSES):
+                    quantise(nc, grouped[:, g], codes[:, g, :], scales[:, g, :])
+
+            for r0 in range(0, S, ROW_UNIT):
+                stage_rows(
+                    hidden_states[r0 : r0 + ROW_UNIT, :],
+                    hs_codes[:, :, r0 : r0 + ROW_UNIT],
+                    hs_scales[:, :, r0 : r0 + ROW_UNIT],
+                )
+            for r0 in range(0, HKV * D, ROW_UNIT):
+                stage_rows(
+                    Wv[r0 : r0 + ROW_UNIT, :],
+                    w_codes[:, :, r0 : r0 + ROW_UNIT],
+                    w_scales[:, :, r0 : r0 + ROW_UNIT],
+                )
+            for r0 in range(0, HID, ROW_UNIT):
+                o0 = HKV * D + r0
+                stage_rows(
+                    Wmb[r0 : r0 + ROW_UNIT, :],
+                    w_codes[:, :, o0 : o0 + ROW_UNIT],
+                    w_scales[:, :, o0 : o0 + ROW_UNIT],
+                )
+
+            for c in range(HKV):
+                for g in range(F_PASSES):
+                    mem_raw = stage.tile([P, PAIR, PACK, D], BF16, bufs=1)
+                    for h2 in range(PAIR):
+                        nc.sync.dma_start(
+                            out=mem_raw[:, h2].rearrange("q (u e) d -> q u (e d)", u=2),
+                            in_=memory[PAIR * c + h2, g * K_PASS : (g + 1) * K_PASS, :].rearrange(
+                                "(u q e) d -> q u (e d)", u=2, e=2
+                            ),
+                        )
+                    mem_grouped = stage.tile([P, PAIR * D, PACK], BF16, bufs=1, align_bytes=64)
+                    nc.scalar.copy(
+                        out=mem_grouped[:].rearrange("q (h d) t -> q h d t", h=PAIR),
+                        in_=mem_raw[:].rearrange("q h t d -> q h d t"),
+                    )
+                    quantise(nc, mem_grouped[:], mem_codes[:, c, g, :], mem_scales[:, c, g, :])
+
+        with tc.tile_pool(name="late", bufs=2) as late, tc.psum_pool(
+            name="sum_banks", bufs=2
+        ) as sum_banks:
+            wmv_codes = late.tile([P, S_PASSES, H * D], U32, bufs=1, align_bytes=64)
+            wmv_scales = late.tile([P, S_PASSES, H * D], U8, bufs=1, align_bytes=64)
+
+            old = late.tile([P, HKV, F // P, PAIR, D], BF16, bufs=1)
+            for c in range(HKV):
+                for ft in range(F // P):
+                    nc.scalar.dma_start(
+                        out=old[:, c, ft],
+                        in_=memory[PAIR * c : PAIR * (c + 1), ft * P : (ft + 1) * P, :].rearrange(
+                            "h f d -> f h d"
+                        ),
+                    )
+
+            for c in range(HKV):
+                c_cols = slice(c * BANK, (c + 1) * BANK)
+
+                for sg in range(S_PASSES):
+                    wmv_planes = late.tile([P, PACK, BANK], BF16)
+                    for t in range(PACK):
+                        st = PACK * sg + t
+                        s_cols = slice(st * P, (st + 1) * P)
+
+                        def project(bank, o0, width):
+                            mx_group(
+                                nc,
+                                bank,
+                                HID_PASSES,
+                                lambda g: hs_codes[:, g, s_cols],
+                                lambda g: hs_scales[:, g, s_cols],
+                                lambda g: w_codes[:, g, o0 : o0 + width],
+                                lambda g: w_scales[:, g, o0 : o0 + width],
+                            )
+
+                        v_bank = sum_banks.tile([P, D], F32)
+                        project(v_bank[:], c * D, D)
+                        mb_bank = sum_banks.tile([P, BANK], F32)
+                        project(mb_bank[:], HKV * D + c * BANK, BANK)
+                        num_bank = sum_banks.tile([P, BANK], F32)
+                        mx_group(
+                            nc,
+                            num_bank[:],
+                            F_PASSES,
+                            lambda g: mkT_codes[:, c, g, s_cols],
+                            lambda g: mkT_scales[:, c, g, s_cols],
+                            lambda g: mem_codes[:, c, g, :],
+                            lambda g: mem_scales[:, c, g, :],
+                        )
+                        gate = late.tile([P, BANK], F32)
+                        nc.vector.tensor_tensor(
+                            out=gate[:], in0=mb_bank[:], in1=bias_mb[:, c_cols], op=ALU.add
+                        )
+                        nc.scalar.activation(out=gate[:], in_=gate[:], func=ACT.Sigmoid)
+                        v_biased = late.tile([P, D], F32)
+                        nc.vector.tensor_tensor(
+                            out=v_biased[:],
+                            in0=v_bank[:],
+                            in1=bias_v[:, c * D : (c + 1) * D],
+                            op=ALU.add,
+                        )
+                        diff = late.tile([P, BANK], F32)
+                        for h2 in range(PAIR):
+                            h_cols = slice(h2 * D, (h2 + 1) * D)
+                            nc.vector.scalar_tensor_tensor(
+                                out=diff[:, h_cols],
+                                in0=num_bank[:, h_cols],
+                                scalar=neg_inv_denom[:, c, st, h2 : h2 + 1],
+                                in1=v_biased[:],
+                                op0=ALU.mult,
+                                op1=ALU.add,
+                            )
+                        nc.gpsimd.tensor_tensor(
+                            out=wmv_planes[:, t, :], in0=diff[:], in1=gate[:], op=ALU.mult
+                        )
+                    wmv_grouped = late.tile([P, BANK, PACK], BF16, align_bytes=64)
+                    nc.vector.tensor_copy(
+                        out=wmv_grouped[:], in_=wmv_planes[:].rearrange("p t n -> p n t")
+                    )
+                    quantise(nc, wmv_grouped[:], wmv_codes[:, sg, c_cols], wmv_scales[:, sg, c_cols])
+
+                for ft in range(F // P):
+                    f_cols = slice(ft * P, (ft + 1) * P)
+                    delta = sum_banks.tile([P, BANK], F32)
+                    mx_group(
+                        nc,
+                        delta[:],
+                        S_PASSES,
+                        lambda g: mkS_codes[:, c, g, f_cols],
+                        lambda g: mkS_scales[:, c, g, f_cols],
+                        lambda g: wmv_codes[:, g, c_cols],
+                        lambda g: wmv_scales[:, g, c_cols],
+                    )
+                    new = late.tile([P, PAIR, D], F32, bufs=4)
+                    nc.vector.tensor_tensor(
+                        out=new[:].rearrange("f h d -> f (h d)"),
+                        in0=delta[:],
+                        in1=old[:, c, ft].rearrange("f h d -> f (h d)"),
+                        op=ALU.add,
+                    )
+                    nc.sync.dma_start(
+                        out=out[PAIR * c : PAIR * (c + 1), f_cols, :].rearrange("h f d -> f h d"),
+                        in_=new[:],
+                    )

@@ -34,6 +34,7 @@ HID_PASSES = HID // K_PASS
 F_PASSES = F // K_PASS
 W_ROWS = HKV * D + HID
 ROW_UNIT = 256
+NORM_PITCH = X2 + 32
 
 FLOPS = 2 * S * HID * W_ROWS + 2 * 2 * H * S * F * D
 
@@ -68,11 +69,11 @@ def tile_armtapproach_pa_kernel(
 
         ident = keep.tile([P, P], F32)
         make_identity(nc, ident[:])
+        ident_bf = keep.tile([P, P], BF16)
+        make_identity(nc, ident_bf[:])
 
         bias_v = keep.tile([P, HKV * D], BF16)
-        nc.scalar.dma_start(out=bias_v[:], in_=bv.partition_broadcast(P))
         bias_mb = keep.tile([P, HID], BF16)
-        nc.scalar.dma_start(out=bias_mb[:], in_=bmb.partition_broadcast(P))
 
         hs_codes = keep.tile([P, HID_PASSES, S], U32, align_bytes=64)
         hs_scales = keep.tile([P, HID_PASSES, S], U8, align_bytes=64)
@@ -82,202 +83,347 @@ def tile_armtapproach_pa_kernel(
         mem_scales = keep.tile([P, HKV, F_PASSES, PAIR * D], U8, align_bytes=64)
         mkT_codes = keep.tile([P, HKV, F_PASSES, S], U32, align_bytes=64)
         mkT_scales = keep.tile([P, HKV, F_PASSES, S], U8, align_bytes=64)
-        mkS_codes = keep.tile([P, HKV, S_PASSES, F], U32, align_bytes=64)
-        mkS_scales = keep.tile([P, HKV, S_PASSES, F], U8, align_bytes=64)
         neg_inv_denom = keep.tile([P, HKV, S_TILES, PAIR], F32)
+        mk_planes = keep.tile([P, HKV, S_PASSES, PACK, F], BF16)
 
         with tc.tile_pool(name="feat", bufs=2) as feat, tc.tile_pool(
             name="stage", bufs=2
-        ) as stage, tc.psum_pool(name="flip_banks", bufs=6) as flip_banks:
-            norm_rows = feat.tile([P, H, F], BF16, bufs=1)
-            nc.scalar.dma_start(
-                out=norm_rows[:].rearrange("p h f -> p (h f)"),
-                in_=norm.rearrange("h f -> (h f)").partition_broadcast(P),
+        ) as stage, tc.psum_pool(name="flip_banks", bufs=3) as flip_banks, tc.psum_pool(
+            name="dot_banks", bufs=1
+        ) as dot_banks:
+            norm_w = feat.tile(
+                [P, H, NU, NORM_PITCH], BF16, bufs=1, align_bytes=64, tag="mkT_grouped"
             )
+            diagonals = feat.tile([P, NU, P], BF16, bufs=1)
+            edge_w = feat.tile([P, H, NU - 1, X2 // P, 2], BF16, bufs=1)
+            band = feat.tile([P, H, X2 // P, P], BF16, bufs=1)
 
-            for c in range(HKV):
-                for sg in range(S_PASSES):
-                    k_rows = feat.tile([P, PACK, D], BF16)
-                    nc.sync.dma_start(
-                        out=k_rows[:],
-                        in_=k[c, sg * K_PASS : (sg + 1) * K_PASS, :].rearrange(
-                            "(t p) d -> p t d", p=P
-                        ),
+            def load_norm():
+                for h in range(H):
+                    for j in range(NU):
+                        nc.sync.dma_start(
+                            out=norm_w[:, h, j, 1 : 1 + X2],
+                            in_=norm[h, j * X2 : (j + 1) * X2].partition_broadcast(P),
+                        )
+
+            def build_band():
+                nc.gpsimd.memset(diagonals[:], 0.0)
+                for j in range(NU):
+                    nc.gpsimd.tensor_copy(out=diagonals[:, j, j:P], in_=ident_bf[:, 0 : P - j])
+                nc.gpsimd.tensor_copy(
+                    out=norm_w[:, :, :, 1 + X2 : 2 + X2], in_=norm_w[:, :, :, 1:2]
+                )
+                for j in range(1, NU):
+                    nc.gpsimd.tensor_copy(
+                        out=edge_w[:, :, j - 1],
+                        in_=norm_w[:, :, j, 1 : 1 + X2].rearrange("p h (m n) -> p h m n", n=P)[
+                            :, :, :, 1:3
+                        ],
                     )
-                    mk_planes = feat.tile([P, PACK, F], BF16)
-                    for a in range(PACK // 2):
-                        x = k_rows[:, 2 * a : 2 * a + 2, :]
-                        x2 = feat.tile([P, 2, NU + X2 + 1], BF16)
-                        nc.scalar.activation(out=x2[:, :, NU : NU + D], in_=x, func=ACT.Relu)
-                        nc.scalar.activation(
-                            out=x2[:, :, NU + D : NU + X2], in_=x, func=ACT.Relu, scale=-1.0
+                nc.gpsimd.memset(edge_w[:, :, 0, :, 1:2], 0.0)
+                for j in range(NU):
+                    window = norm_w[:, :, j, 2 : 2 + X2].rearrange("p h (m n) -> p h m n", n=P)
+                    diagonal = (
+                        diagonals[:, j, :].unsqueeze(1).unsqueeze(1).to_broadcast([P, H, X2 // P, P])
+                    )
+                    if j == 0:
+                        nc.vector.tensor_tensor(out=band[:], in0=window, in1=diagonal, op=ALU.mult)
+                    else:
+                        term = feat.tile([P, H, X2 // P, P], BF16, bufs=1)
+                        nc.vector.tensor_tensor(out=term[:], in0=window, in1=diagonal, op=ALU.mult)
+                        nc.vector.tensor_tensor(out=band[:], in0=band[:], in1=term[:], op=ALU.add)
+
+            k_rows, x2, phi, inv_norm, x2T, inner_sums, mkT_grouped = {}, {}, {}, {}, {}, {}, {}
+
+            def load_keys(grp):
+                c, sg = divmod(grp, S_PASSES)
+                k_rows[grp] = feat.tile([P, PACK, D], BF16, name="k_rows")
+                nc.sync.dma_start(
+                    out=k_rows[grp][:],
+                    in_=k[c, sg * K_PASS : (sg + 1) * K_PASS, :].rearrange("(t p) d -> p t d", p=P),
+                )
+
+            def relu_halves(pair):
+                grp, a = divmod(pair, 2)
+                x = k_rows[grp][:, 2 * a : 2 * a + 2, :]
+                x2[pair] = feat.tile([P, 2, NU + X2 + 1], BF16, bufs=3, name="x2")
+                nc.scalar.activation(
+                    out=x2[pair][:, :, NU + X2 : NU + X2 + 1], in_=x[:, :, 0:1], func=ACT.Relu
+                )
+                nc.scalar.activation(out=x2[pair][:, :, NU : NU + D], in_=x, func=ACT.Relu)
+                nc.scalar.activation(
+                    out=x2[pair][:, :, NU + D : NU + X2], in_=x, func=ACT.Relu, scale=-1.0
+                )
+                nc.scalar.activation(
+                    out=x2[pair][:, :, 0:NU], in_=x[:, :, D - NU : D], func=ACT.Relu, scale=-1.0
+                )
+
+            def products(pair):
+                phi[pair] = feat.tile([P, 2, F], F32, bufs=3, name="phi")
+                for j in range(1, NU + 1):
+                    nc.vector.tensor_tensor(
+                        out=phi[pair][:, :, (j - 1) * X2 : j * X2],
+                        in0=x2[pair][:, :, NU : NU + X2],
+                        in1=x2[pair][:, :, NU - j : NU - j + X2],
+                        op=ALU.mult,
+                    )
+
+            def inverse_norms(pair):
+                sum_sq = feat.tile([P, 2], F32)
+                for b in range(2):
+                    squares = feat.tile([P, F], BF16)
+                    nc.scalar.activation(
+                        out=squares[:],
+                        in_=phi[pair][:, b, :],
+                        func=ACT.Square,
+                        accum_out=sum_sq[:, b : b + 1],
+                    )
+                nc.scalar.activation(
+                    out=sum_sq[:], in_=sum_sq[:], func=ACT.Relu, bias=-(TINY * TINY)
+                )
+                inv_norm[pair] = feat.tile([P, 2], F32, name="inv_norm")
+                nc.scalar.activation(
+                    out=inv_norm[pair][:],
+                    in_=sum_sq[:],
+                    func=ACT.Abs_reciprocal_sqrt,
+                    bias=TINY * TINY,
+                )
+
+            def flip_x2(pair):
+                x2T_bank = dot_banks.tile([P, 2, X2 // P, P], BF16)
+                for b in range(2):
+                    for m in range(X2 // P):
+                        nc.tensor.transpose(
+                            x2T_bank[:, b, m, :],
+                            x2[pair][:, b, NU + m * P : NU + (m + 1) * P],
+                            ident_bf[:],
                         )
-                        nc.scalar.activation(
-                            out=x2[:, :, 0:NU], in_=x[:, :, D - NU : D], func=ACT.Relu, scale=-1.0
-                        )
-                        phi = feat.tile([P, 2, F], F32)
-                        for j in range(1, NU + 1):
-                            nc.vector.tensor_tensor(
-                                out=phi[:, :, (j - 1) * X2 : j * X2],
-                                in0=x2[:, :, NU : NU + X2],
-                                in1=x2[:, :, NU - j : NU - j + X2],
-                                op=ALU.mult,
+                x2T[pair] = feat.tile([P, 2, X2 // P, P], BF16, name="x2T")
+                nc.scalar.copy(out=x2T[pair][:], in_=x2T_bank[:])
+
+            def band_products(pair):
+                c = pair // (2 * S_PASSES)
+                for b in range(2):
+                    for h2 in range(PAIR):
+                        sums = dot_banks.tile([P, X2], F32, bufs=2 * PAIR, name="inner_sums")
+                        for m in range(X2 // P):
+                            nc.tensor.matmul(
+                                out=sums[:, m * P : (m + 1) * P],
+                                lhsT=x2T[pair][:, b, m, :],
+                                rhs=band[:, PAIR * c + h2, m, :],
+                                start=True,
+                                stop=True,
                             )
-                        sum_sq = feat.tile([P, 2], F32)
-                        dots = feat.tile([P, 2, PAIR], F32)
-                        for b in range(2):
-                            squares = feat.tile([P, F], BF16)
-                            nc.scalar.activation(
-                                out=squares[:],
-                                in_=phi[:, b, :],
-                                func=ACT.Square,
-                                accum_out=sum_sq[:, b : b + 1],
-                            )
-                            for h2 in range(PAIR):
-                                weighted = feat.tile([P, F], F32)
-                                nc.vector.scalar_tensor_tensor(
-                                    out=weighted[:],
-                                    in0=phi[:, b, :],
-                                    scalar=1.0,
-                                    in1=norm_rows[:, PAIR * c + h2, :],
-                                    op0=ALU.mult,
-                                    op1=ALU.mult,
-                                    accum_out=dots[:, b, h2 : h2 + 1],
-                                )
-                        nc.vector.tensor_scalar_max(
-                            out=sum_sq[:], in0=sum_sq[:], scalar1=TINY * TINY
-                        )
-                        length = feat.tile([P, 2], F32)
-                        nc.scalar.activation(out=length[:], in_=sum_sq[:], func=ACT.Sqrt)
-                        inv_norm = feat.tile([P, 2], F32)
-                        nc.vector.reciprocal(out=inv_norm[:], in_=length[:])
-                        denom = feat.tile([P, 2, PAIR], F32)
-                        nc.vector.tensor_tensor(
-                            out=denom[:],
-                            in0=dots[:],
-                            in1=inv_norm[:].unsqueeze(2).to_broadcast([P, 2, PAIR]),
-                            op=ALU.mult,
-                        )
-                        nc.vector.tensor_scalar(
-                            out=denom[:],
-                            in0=denom[:],
-                            scalar1=-1.0,
-                            scalar2=-EPS,
+                        inner_sums[(pair, b, h2)] = sums
+
+            def denominators(pair):
+                grp, a = divmod(pair, 2)
+                c, sg = divmod(grp, S_PASSES)
+                dots = feat.tile([P, 2, PAIR], F32)
+                for b in range(2):
+                    for h2 in range(PAIR):
+                        weighted = feat.tile([P, X2], F32)
+                        nc.vector.scalar_tensor_tensor(
+                            out=weighted[:],
+                            in0=inner_sums[(pair, b, h2)][:],
+                            scalar=1.0,
+                            in1=x2[pair][:, b, NU + 1 : NU + 1 + X2],
                             op0=ALU.mult,
-                            op1=ALU.add,
+                            op1=ALU.mult,
+                            accum_out=dots[:, b, h2 : h2 + 1],
                         )
-                        st0 = PACK * sg + 2 * a
-                        nc.vector.reciprocal(out=neg_inv_denom[:, c, st0 : st0 + 2, :], in_=denom[:])
-                        for b in range(2):
-                            nc.scalar.activation(
-                                out=mk_planes[:, 2 * a + b, :],
-                                in_=phi[:, b, :],
-                                func=ACT.Copy,
-                                scale=inv_norm[:, b : b + 1],
-                            )
-
-                    mkS_grouped = feat.tile([P, F, PACK], BF16, bufs=1, align_bytes=64)
-                    for g in range(F_PASSES):
-                        f_cols = slice(g * X2, (g + 1) * X2)
-                        nc.vector.tensor_copy(
-                            out=mkS_grouped[:, f_cols, :],
-                            in_=mk_planes[:, :, f_cols].rearrange("p t f -> p f t"),
-                        )
-                    for g in range(F_PASSES):
-                        f_cols = slice(g * X2, (g + 1) * X2)
-                        quantise(
-                            nc,
-                            mkS_grouped[:, f_cols, :],
-                            mkS_codes[:, c, sg, f_cols],
-                            mkS_scales[:, c, sg, f_cols],
-                        )
-
-                    for g in range(F_PASSES):
-                        mkT_grouped = feat.tile([P, K_PASS, PACK], BF16, align_bytes=64)
-                        mkT_words = mkT_grouped[:].bitcast(F32)
-                        for a in range(PACK // 2):
-                            flipped = flip_banks.tile([P, 2, 2, P], F32, tag="bank")
-                            for b in range(2):
-                                plane_words = mk_planes[:, 2 * a + b, :].bitcast(F32)
-                                for u in range(2):
-                                    w0 = (2 * g + u) * P
-                                    nc.tensor.transpose(
-                                        flipped[:, b, u, :], plane_words[:, w0 : w0 + P], ident[:]
-                                    )
-                            nc.scalar.copy(
-                                out=mkT_words[:, 2 * a * P : (2 * a + 2) * P, :].rearrange(
-                                    "q (b r) u -> q b r u", b=2
-                                ),
-                                in_=flipped[:].rearrange("q b u r -> q b r u"),
-                            )
-                        s_cols = slice(sg * K_PASS, (sg + 1) * K_PASS)
-                        quantise(
-                            nc, mkT_grouped[:], mkT_codes[:, c, g, s_cols], mkT_scales[:, c, g, s_cols]
-                        )
-
-            def stage_rows(rows, codes, scales):
-                grouped = stage.tile([P, HID_PASSES, ROW_UNIT, PACK], BF16, align_bytes=64)
-                grouped_words = grouped[:].bitcast(F32)
-                for rt in range(ROW_UNIT // P):
-                    raw = stage.tile([P, HID], BF16)
-                    nc.sync.dma_start(out=raw[:], in_=rows[rt * P : (rt + 1) * P, :])
-                    raw_words = raw[:].bitcast(F32)
-                    flipped = flip_banks.tile([P, HID_PASSES, 2, P], F32, tag="bank")
-                    for g in range(HID_PASSES):
-                        for u in range(2):
-                            w0 = (2 * g + u) * P
-                            nc.tensor.transpose(
-                                flipped[:, g, u, :], raw_words[:, w0 : w0 + P], ident[:]
-                            )
-                    nc.scalar.copy(
-                        out=grouped_words[:, :, rt * P : (rt + 1) * P, :],
-                        in_=flipped[:].rearrange("q g u r -> q g r u"),
+                edge_terms = feat.tile([P, 2, PAIR, 2 * (NU - 1) * (X2 // P)], F32)
+                for h2 in range(PAIR):
+                    nc.vector.tensor_tensor(
+                        out=edge_terms[:, :, h2, :].rearrange("p b (m n) -> p b m n", n=2),
+                        in0=phi[pair][:, :, X2:F].rearrange("p b (m n) -> p b m n", n=P)[:, :, :, 1:3],
+                        in1=edge_w[:, PAIR * c + h2]
+                        .rearrange("p j m n -> p (j m) n")
+                        .unsqueeze(1)
+                        .to_broadcast([P, 2, (NU - 1) * (X2 // P), 2]),
+                        op=ALU.mult,
                     )
-                for g in range(HID_PASSES):
-                    quantise(nc, grouped[:, g], codes[:, g, :], scales[:, g, :])
+                edge_sums = feat.tile([P, 2, PAIR], F32)
+                nc.vector.tensor_reduce(
+                    out=edge_sums[:], in_=edge_terms[:], axis=mybir.AxisListType.X, op=ALU.add
+                )
+                for b in range(2):
+                    nc.vector.tensor_scalar_mul(
+                        out=mk_planes[:, c, sg, 2 * a + b, :],
+                        in0=phi[pair][:, b, :],
+                        scalar1=inv_norm[pair][:, b : b + 1],
+                    )
+                nc.vector.tensor_tensor(out=dots[:], in0=dots[:], in1=edge_sums[:], op=ALU.add)
+                nc.vector.tensor_tensor(
+                    out=dots[:],
+                    in0=dots[:],
+                    in1=inv_norm[pair][:].unsqueeze(2).to_broadcast([P, 2, PAIR]),
+                    op=ALU.mult,
+                )
+                nc.vector.tensor_scalar(
+                    out=dots[:], in0=dots[:], scalar1=-1.0, scalar2=-EPS, op0=ALU.mult, op1=ALU.add
+                )
+                st0 = PACK * sg + 2 * a
+                nc.vector.reciprocal(out=neg_inv_denom[:, c, st0 : st0 + 2, :], in_=dots[:])
 
+            def transpose_features(grp):
+                mkT_grouped[grp] = feat.tile(
+                    [P, F_PASSES, K_PASS, PACK], BF16, bufs=1, align_bytes=64, name="mkT_grouped"
+                )
+                mkT_words = mkT_grouped[grp][:].bitcast(F32)
+                c, sg = divmod(grp, S_PASSES)
+                for g in range(F_PASSES):
+                    for a in range(PACK // 2):
+                        flipped = flip_banks.tile([P, 2, 2, P], F32, tag="bank")
+                        for b in range(2):
+                            plane_words = mk_planes[:, c, sg, 2 * a + b, :].bitcast(F32)
+                            for u in range(2):
+                                w0 = (2 * g + u) * P
+                                nc.tensor.transpose(
+                                    flipped[:, b, u, :], plane_words[:, w0 : w0 + P], ident[:]
+                                )
+                        nc.scalar.copy(
+                            out=mkT_words[:, g, 2 * a * P : (2 * a + 2) * P, :].rearrange(
+                                "q (b r) u -> q b r u", b=2
+                            ),
+                            in_=flipped[:].rearrange("q b u r -> q b r u"),
+                        )
+
+            def quantise_features(grp):
+                c, sg = divmod(grp, S_PASSES)
+                s_cols = slice(sg * K_PASS, (sg + 1) * K_PASS)
+                for g in range(F_PASSES):
+                    quantise(
+                        nc,
+                        mkT_grouped[grp][:, g],
+                        mkT_codes[:, c, g, s_cols],
+                        mkT_scales[:, c, g, s_cols],
+                    )
+
+            units = []
             for r0 in range(0, S, ROW_UNIT):
-                stage_rows(
-                    hidden_states[r0 : r0 + ROW_UNIT, :],
-                    hs_codes[:, :, r0 : r0 + ROW_UNIT],
-                    hs_scales[:, :, r0 : r0 + ROW_UNIT],
-                )
+                r_cols = slice(r0, r0 + ROW_UNIT)
+                units.append((hidden_states[r_cols, :], hs_codes[:, :, r_cols], hs_scales[:, :, r_cols]))
             for r0 in range(0, HKV * D, ROW_UNIT):
-                stage_rows(
-                    Wv[r0 : r0 + ROW_UNIT, :],
-                    w_codes[:, :, r0 : r0 + ROW_UNIT],
-                    w_scales[:, :, r0 : r0 + ROW_UNIT],
-                )
+                r_cols = slice(r0, r0 + ROW_UNIT)
+                units.append((Wv[r_cols, :], w_codes[:, :, r_cols], w_scales[:, :, r_cols]))
             for r0 in range(0, HID, ROW_UNIT):
-                o0 = HKV * D + r0
-                stage_rows(
-                    Wmb[r0 : r0 + ROW_UNIT, :],
-                    w_codes[:, :, o0 : o0 + ROW_UNIT],
-                    w_scales[:, :, o0 : o0 + ROW_UNIT],
-                )
-
+                o_cols = slice(HKV * D + r0, HKV * D + r0 + ROW_UNIT)
+                units.append((Wmb[r0 : r0 + ROW_UNIT, :], w_codes[:, :, o_cols], w_scales[:, :, o_cols]))
+            row_units = len(units)
             for c in range(HKV):
                 for g in range(F_PASSES):
-                    mem_raw = stage.tile([P, PAIR, PACK, D], BF16, bufs=1)
+                    units.append(
+                        (
+                            memory[PAIR * c : PAIR * (c + 1), g * K_PASS : (g + 1) * K_PASS, :],
+                            mem_codes[:, c, g, :],
+                            mem_scales[:, c, g, :],
+                        )
+                    )
+            raw, grouped = {}, {}
+
+            def load_unit(n):
+                if n < row_units:
+                    raw[n] = stage.tile([P, ROW_UNIT // P, HID], BF16, name="raw")
+                    nc.sync.dma_start(
+                        out=raw[n][:], in_=units[n][0].rearrange("(rt p) k -> p rt k", p=P)
+                    )
+                else:
+                    raw[n] = stage.tile([P, PAIR, PACK, D], BF16, name="raw")
                     for h2 in range(PAIR):
                         nc.sync.dma_start(
-                            out=mem_raw[:, h2].rearrange("q (u e) d -> q u (e d)", u=2),
-                            in_=memory[PAIR * c + h2, g * K_PASS : (g + 1) * K_PASS, :].rearrange(
-                                "(u q e) d -> q u (e d)", u=2, e=2
-                            ),
+                            out=raw[n][:, h2].rearrange("q (u e) d -> q u (e d)", u=2),
+                            in_=units[n][0][h2].rearrange("(u q e) d -> q u (e d)", u=2, e=2),
                         )
-                    mem_grouped = stage.tile([P, PAIR * D, PACK], BF16, bufs=1, align_bytes=64)
-                    nc.scalar.copy(
-                        out=mem_grouped[:].rearrange("q (h d) t -> q h d t", h=PAIR),
-                        in_=mem_raw[:].rearrange("q h t d -> q h d t"),
+
+            def lay_out_unit(n):
+                if n < row_units:
+                    grouped[n] = stage.tile(
+                        [P, HID_PASSES, ROW_UNIT, PACK], BF16, align_bytes=64, name="grouped"
                     )
-                    quantise(nc, mem_grouped[:], mem_codes[:, c, g, :], mem_scales[:, c, g, :])
+                    grouped_words = grouped[n][:].bitcast(F32)
+                    for rt in range(ROW_UNIT // P):
+                        raw_words = raw[n][:, rt, :].bitcast(F32)
+                        flipped = flip_banks.tile([P, HID_PASSES, 2, P], F32, tag="bank")
+                        for g in range(HID_PASSES):
+                            for u in range(2):
+                                w0 = (2 * g + u) * P
+                                nc.tensor.transpose(
+                                    flipped[:, g, u, :], raw_words[:, w0 : w0 + P], ident[:]
+                                )
+                        nc.scalar.copy(
+                            out=grouped_words[:, :, rt * P : (rt + 1) * P, :],
+                            in_=flipped[:].rearrange("q g u r -> q g r u"),
+                        )
+                else:
+                    grouped[n] = stage.tile([P, PAIR, D, PACK], BF16, align_bytes=64, name="grouped")
+                    for h2 in range(PAIR):
+                        nc.scalar.copy(
+                            out=grouped[n][:, h2].rearrange("q (n i) t -> q n t i", i=4),
+                            in_=raw[n][:, h2].rearrange("q t (n i) -> q n t i", i=4),
+                        )
+
+            def quantise_unit(n):
+                if n < row_units:
+                    for g in range(HID_PASSES):
+                        quantise(nc, grouped[n][:, g], units[n][1][:, g, :], units[n][2][:, g, :])
+                else:
+                    quantise(
+                        nc, grouped[n][:].rearrange("q h d t -> q (h d) t"), units[n][1], units[n][2]
+                    )
+
+            pairs = 2 * HKV * S_PASSES
+            share = len(units) // pairs
+            with tc.manual_schedule():
+                load_keys(0)
+                load_norm()
+                load_keys(1)
+                for n in range(share):
+                    load_unit(n)
+                relu_halves(0)
+                relu_halves(1)
+                products(0)
+                flip_x2(0)
+                build_band()
+                band_products(0)
+                for step in range(pairs + 1):
+                    done_grp = step // 2 - 1
+                    if step < pairs:
+                        inverse_norms(step)
+                    if step + 1 < pairs:
+                        flip_x2(step + 1)
+                    if step % 2 == 0 and step + 4 < pairs:
+                        load_keys(step // 2 + 2)
+                    if step + 2 < pairs:
+                        relu_halves(step + 2)
+                    if step % 2 == 0 and done_grp >= 0:
+                        quantise_features(done_grp)
+                    for n in range((step - 1) * share, step * share):
+                        if n >= 0:
+                            quantise_unit(n)
+                    if step < pairs:
+                        denominators(step)
+                    if step + 1 < pairs:
+                        products(step + 1)
+                    if step < pairs:
+                        for n in range(step * share, (step + 1) * share):
+                            lay_out_unit(n)
+                    if step % 2 == 1:
+                        transpose_features(step // 2)
+                    if step + 1 < pairs:
+                        band_products(step + 1)
+                        for n in range((step + 1) * share, (step + 2) * share):
+                            load_unit(n)
 
         with tc.tile_pool(name="late", bufs=2) as late, tc.psum_pool(
             name="sum_banks", bufs=2
         ) as sum_banks:
             wmv_codes = late.tile([P, S_PASSES, H * D], U32, bufs=1, align_bytes=64)
             wmv_scales = late.tile([P, S_PASSES, H * D], U8, bufs=1, align_bytes=64)
+            mkS_codes = late.tile([P, HKV, S_PASSES, F], U32, bufs=1, align_bytes=64)
+            mkS_scales = late.tile([P, HKV, S_PASSES, F], U8, bufs=1, align_bytes=64)
+            nc.sync.dma_start(out=bias_mb[:], in_=bmb.partition_broadcast(P))
+            nc.sync.dma_start(out=bias_v[:], in_=bv.partition_broadcast(P))
 
             old = late.tile([P, HKV, F // P, PAIR, D], BF16, bufs=1)
             for c in range(HKV):
@@ -349,11 +495,24 @@ def tile_armtapproach_pa_kernel(
                         nc.gpsimd.tensor_tensor(
                             out=wmv_planes[:, t, :], in0=diff[:], in1=gate[:], op=ALU.mult
                         )
-                    wmv_grouped = late.tile([P, BANK, PACK], BF16, align_bytes=64)
+                    wmv_grouped = late.tile([P, BANK, PACK], BF16, bufs=1, align_bytes=64)
                     nc.vector.tensor_copy(
-                        out=wmv_grouped[:], in_=wmv_planes[:].rearrange("p t n -> p n t")
+                        out=wmv_grouped[:].rearrange("p (n i) t -> p n t i", i=4),
+                        in_=wmv_planes[:].rearrange("p t (n i) -> p n t i", i=4),
                     )
                     quantise(nc, wmv_grouped[:], wmv_codes[:, sg, c_cols], wmv_scales[:, sg, c_cols])
+
+                for sg in range(S_PASSES):
+                    for g in range(F_PASSES):
+                        f_cols = slice(g * X2, (g + 1) * X2)
+                        mkS_grouped = late.tile([P, X2, PACK], BF16, bufs=3, align_bytes=64)
+                        nc.scalar.copy(
+                            out=mkS_grouped[:].rearrange("p (n i) t -> p n t i", i=4),
+                            in_=mk_planes[:, c, sg, :, f_cols].rearrange("p t (n i) -> p n t i", i=4),
+                        )
+                        quantise(
+                            nc, mkS_grouped[:], mkS_codes[:, c, sg, f_cols], mkS_scales[:, c, sg, f_cols]
+                        )
 
                 for ft in range(F // P):
                     f_cols = slice(ft * P, (ft + 1) * P)

@@ -99,12 +99,10 @@ def tile_armtapproach_pa_kernel(
             band = feat.tile([P, H, X2 // P, P], BF16, bufs=1)
 
             def load_norm():
-                for h in range(H):
-                    for j in range(NU):
-                        nc.sync.dma_start(
-                            out=norm_w[:, h, j, 1 : 1 + X2],
-                            in_=norm[h, j * X2 : (j + 1) * X2].partition_broadcast(P),
-                        )
+                nc.sync.dma_start(
+                    out=norm_w[:, :, :, 1 : 1 + X2].rearrange("p h j i -> p (h j) i"),
+                    in_=norm.rearrange("h (j i) -> (h j) i", j=NU).partition_broadcast(P),
+                )
 
             def build_band():
                 nc.gpsimd.memset(diagonals[:], 0.0)
@@ -146,7 +144,7 @@ def tile_armtapproach_pa_kernel(
             def relu_halves(pair):
                 grp, a = divmod(pair, 2)
                 x = k_rows[grp][:, 2 * a : 2 * a + 2, :]
-                x2[pair] = feat.tile([P, 2, NU + X2 + 1], BF16, bufs=3, name="x2")
+                x2[pair] = feat.tile([P, 2, NU + X2 + 1], BF16, bufs=4, name="x2")
                 nc.scalar.activation(
                     out=x2[pair][:, :, NU + X2 : NU + X2 + 1], in_=x[:, :, 0:1], func=ACT.Relu
                 )
@@ -376,59 +374,59 @@ def tile_armtapproach_pa_kernel(
             share = len(units) // pairs
             with tc.manual_schedule():
                 load_keys(0)
-                load_norm()
                 load_keys(1)
+                load_norm()
                 for n in range(share):
                     load_unit(n)
-                relu_halves(0)
-                relu_halves(1)
-                products(0)
+                nc.sync.dma_start(out=bias_mb[:], in_=bmb.partition_broadcast(P))
+                nc.sync.dma_start(out=bias_v[:], in_=bv.partition_broadcast(P))
+                for pair in range(3):
+                    relu_halves(pair)
+                for pair in range(2):
+                    products(pair)
                 flip_x2(0)
                 build_band()
                 band_products(0)
+                inverse_norms(0)
                 for step in range(pairs + 1):
-                    done_grp = step // 2 - 1
-                    if step < pairs:
-                        inverse_norms(step)
                     if step + 1 < pairs:
+                        inverse_norms(step + 1)
                         flip_x2(step + 1)
                     if step % 2 == 0 and step + 4 < pairs:
                         load_keys(step // 2 + 2)
-                    if step + 2 < pairs:
-                        relu_halves(step + 2)
-                    if step % 2 == 0 and done_grp >= 0:
-                        quantise_features(done_grp)
-                    for n in range((step - 1) * share, step * share):
-                        if n >= 0:
-                            quantise_unit(n)
+                    if step + 3 < pairs:
+                        relu_halves(step + 3)
+                    if step % 2 == 0 and step >= 2:
+                        quantise_features(step // 2 - 1)
+                    for n in range(max(step - 1, 0) * share, step * share):
+                        quantise_unit(n)
                     if step < pairs:
                         denominators(step)
-                    if step + 1 < pairs:
-                        products(step + 1)
+                    if step + 2 < pairs:
+                        products(step + 2)
                     if step < pairs:
                         for n in range(step * share, (step + 1) * share):
                             lay_out_unit(n)
+                    if step + 1 < pairs:
+                        band_products(step + 1)
                     if step % 2 == 1:
                         transpose_features(step // 2)
                     if step + 1 < pairs:
-                        band_products(step + 1)
                         for n in range((step + 1) * share, (step + 2) * share):
                             load_unit(n)
 
-        with tc.tile_pool(name="late", bufs=2) as late, tc.psum_pool(
-            name="sum_banks", bufs=2
+        with tc.tile_pool(name="late", bufs=2, reuse_waits="tile") as late, tc.psum_pool(
+            name="sum_banks", bufs=2, reuse_waits="tile"
         ) as sum_banks:
             wmv_codes = late.tile([P, S_PASSES, H * D], U32, bufs=1, align_bytes=64)
             wmv_scales = late.tile([P, S_PASSES, H * D], U8, bufs=1, align_bytes=64)
             mkS_codes = late.tile([P, HKV, S_PASSES, F], U32, bufs=1, align_bytes=64)
             mkS_scales = late.tile([P, HKV, S_PASSES, F], U8, bufs=1, align_bytes=64)
-            nc.sync.dma_start(out=bias_mb[:], in_=bmb.partition_broadcast(P))
-            nc.sync.dma_start(out=bias_v[:], in_=bv.partition_broadcast(P))
 
             old = late.tile([P, HKV, F // P, PAIR, D], BF16, bufs=1)
             for c in range(HKV):
                 for ft in range(F // P):
-                    nc.scalar.dma_start(
+                    nc.sync.dma_start(
                         out=old[:, c, ft],
                         in_=memory[PAIR * c : PAIR * (c + 1), ft * P : (ft + 1) * P, :].rearrange(
                             "h f d -> f h d"
@@ -527,12 +525,22 @@ def tile_armtapproach_pa_kernel(
                         lambda g: wmv_scales[:, g, c_cols],
                     )
                     new = late.tile([P, PAIR, D], F32, bufs=4)
-                    nc.vector.tensor_tensor(
-                        out=new[:].rearrange("f h d -> f (h d)"),
-                        in0=delta[:],
-                        in1=old[:, c, ft].rearrange("f h d -> f (h d)"),
-                        op=ALU.add,
-                    )
+                    if ft % 2 == 0:
+                        nc.vector.tensor_tensor(
+                            out=new[:].rearrange("f h d -> f (h d)"),
+                            in0=delta[:],
+                            in1=old[:, c, ft].rearrange("f h d -> f (h d)"),
+                            op=ALU.add,
+                        )
+                    else:
+                        delta_sb = late.tile([P, BANK], F32)
+                        nc.scalar.copy(out=delta_sb[:], in_=delta[:])
+                        nc.gpsimd.tensor_tensor(
+                            out=new[:].rearrange("f h d -> f (h d)"),
+                            in0=delta_sb[:],
+                            in1=old[:, c, ft].rearrange("f h d -> f (h d)"),
+                            op=ALU.add,
+                        )
                     nc.sync.dma_start(
                         out=out[PAIR * c : PAIR * (c + 1), f_cols, :].rearrange("h f d -> f h d"),
                         in_=new[:],

@@ -32,9 +32,11 @@ S_TILES = S // P
 S_PASSES = S // K_PASS
 HID_PASSES = HID // K_PASS
 F_PASSES = F // K_PASS
+X2_TILES = X2 // P
 W_ROWS = HKV * D + HID
 ROW_UNIT = 256
 NORM_PITCH = X2 + 32
+EDGES = 2 * (NU - 1) * X2_TILES
 
 FLOPS = 2 * S * HID * W_ROWS + 2 * 2 * H * S * F * D
 
@@ -58,6 +60,13 @@ def mx_group(nc, bank, passes, lhs_codes, lhs_scales, rhs_codes, rhs_scales):
             start=(g == 0),
             stop=(g == passes - 1),
         )
+
+
+def interleave(engine_copy, grouped, planes):
+    engine_copy(
+        out=grouped.rearrange("p (n i) t -> p n t i", i=4),
+        in_=planes.rearrange("p t (n i) -> p n t i", i=4),
+    )
 
 
 def tile_armtapproach_pa_kernel(
@@ -84,7 +93,7 @@ def tile_armtapproach_pa_kernel(
         mkT_codes = keep.tile([P, HKV, F_PASSES, S], U32, align_bytes=64)
         mkT_scales = keep.tile([P, HKV, F_PASSES, S], U8, align_bytes=64)
         neg_inv_denom = keep.tile([P, HKV, S_TILES, PAIR], F32)
-        mk_planes = keep.tile([P, HKV, S_PASSES, PACK, F], BF16)
+        mk_planes = keep.tile([P, HKV, S_TILES, F], BF16)
 
         with tc.tile_pool(name="feat", bufs=2) as feat, tc.tile_pool(
             name="stage", bufs=2
@@ -95,8 +104,8 @@ def tile_armtapproach_pa_kernel(
                 [P, H, NU, NORM_PITCH], BF16, bufs=1, align_bytes=64, tag="mkT_grouped"
             )
             diagonals = feat.tile([P, NU, P], BF16, bufs=1)
-            edge_w = feat.tile([P, H, NU - 1, X2 // P, 2], BF16, bufs=1)
-            band = feat.tile([P, H, X2 // P, P], BF16, bufs=1)
+            band = feat.tile([P, H, X2_TILES, P], BF16, bufs=1)
+            edge_w = feat.tile([P, H, NU - 1, X2_TILES, 2], BF16, bufs=1)
 
             def load_norm():
                 nc.sync.dma_start(
@@ -122,16 +131,23 @@ def tile_armtapproach_pa_kernel(
                 for j in range(NU):
                     window = norm_w[:, :, j, 2 : 2 + X2].rearrange("p h (m n) -> p h m n", n=P)
                     diagonal = (
-                        diagonals[:, j, :].unsqueeze(1).unsqueeze(1).to_broadcast([P, H, X2 // P, P])
+                        diagonals[:, j, :].unsqueeze(1).unsqueeze(1).to_broadcast([P, H, X2_TILES, P])
                     )
                     if j == 0:
                         nc.vector.tensor_tensor(out=band[:], in0=window, in1=diagonal, op=ALU.mult)
                     else:
-                        term = feat.tile([P, H, X2 // P, P], BF16, bufs=1)
+                        term = feat.tile([P, H, X2_TILES, P], BF16, bufs=1)
                         nc.vector.tensor_tensor(out=term[:], in0=window, in1=diagonal, op=ALU.mult)
                         nc.vector.tensor_tensor(out=band[:], in0=band[:], in1=term[:], op=ALU.add)
 
-            k_rows, x2, phi, inv_norm, x2T, inner_sums, mkT_grouped = {}, {}, {}, {}, {}, {}, {}
+            k_rows, x2, phi, x2T, inner_sums, mkT_grouped = {}, {}, {}, {}, {}, {}
+            inv_norm = feat.tile([P, HKV, S_TILES], F32, bufs=1)
+            dots = feat.tile([P, HKV, S_TILES, PAIR], F32, bufs=1)
+            edge_terms = feat.tile([P, HKV, S_TILES, PAIR, EDGES], F32, bufs=1)
+
+            def planes_of(pair):
+                c, half = divmod(pair, S_TILES // 2)
+                return c, 2 * half
 
             def load_keys(grp):
                 c, sg = divmod(grp, S_PASSES)
@@ -167,6 +183,7 @@ def tile_armtapproach_pa_kernel(
                     )
 
             def inverse_norms(pair):
+                c, st0 = planes_of(pair)
                 sum_sq = feat.tile([P, 2], F32)
                 for b in range(2):
                     squares = feat.tile([P, F], BF16)
@@ -179,32 +196,31 @@ def tile_armtapproach_pa_kernel(
                 nc.scalar.activation(
                     out=sum_sq[:], in_=sum_sq[:], func=ACT.Relu, bias=-(TINY * TINY)
                 )
-                inv_norm[pair] = feat.tile([P, 2], F32, name="inv_norm")
                 nc.scalar.activation(
-                    out=inv_norm[pair][:],
+                    out=inv_norm[:, c, st0 : st0 + 2],
                     in_=sum_sq[:],
                     func=ACT.Abs_reciprocal_sqrt,
                     bias=TINY * TINY,
                 )
 
             def flip_x2(pair):
-                x2T_bank = dot_banks.tile([P, 2, X2 // P, P], BF16)
+                x2T_bank = dot_banks.tile([P, 2, X2_TILES, P], BF16)
                 for b in range(2):
-                    for m in range(X2 // P):
+                    for m in range(X2_TILES):
                         nc.tensor.transpose(
                             x2T_bank[:, b, m, :],
                             x2[pair][:, b, NU + m * P : NU + (m + 1) * P],
                             ident_bf[:],
                         )
-                x2T[pair] = feat.tile([P, 2, X2 // P, P], BF16, name="x2T")
-                nc.scalar.copy(out=x2T[pair][:], in_=x2T_bank[:])
+                x2T[pair] = feat.tile([P, 2, X2_TILES, P], BF16, name="x2T")
+                nc.vector.tensor_copy(out=x2T[pair][:], in_=x2T_bank[:])
 
             def band_products(pair):
-                c = pair // (2 * S_PASSES)
+                c, st0 = planes_of(pair)
                 for b in range(2):
                     for h2 in range(PAIR):
                         sums = dot_banks.tile([P, X2], F32, bufs=2 * PAIR, name="inner_sums")
-                        for m in range(X2 // P):
+                        for m in range(X2_TILES):
                             nc.tensor.matmul(
                                 out=sums[:, m * P : (m + 1) * P],
                                 lhsT=x2T[pair][:, b, m, :],
@@ -214,10 +230,8 @@ def tile_armtapproach_pa_kernel(
                             )
                         inner_sums[(pair, b, h2)] = sums
 
-            def denominators(pair):
-                grp, a = divmod(pair, 2)
-                c, sg = divmod(grp, S_PASSES)
-                dots = feat.tile([P, 2, PAIR], F32)
+            def dot_products(pair):
+                c, st0 = planes_of(pair)
                 for b in range(2):
                     for h2 in range(PAIR):
                         weighted = feat.tile([P, X2], F32)
@@ -228,53 +242,58 @@ def tile_armtapproach_pa_kernel(
                             in1=x2[pair][:, b, NU + 1 : NU + 1 + X2],
                             op0=ALU.mult,
                             op1=ALU.mult,
-                            accum_out=dots[:, b, h2 : h2 + 1],
+                            accum_out=dots[:, c, st0 + b, h2 : h2 + 1],
                         )
-                edge_terms = feat.tile([P, 2, PAIR, 2 * (NU - 1) * (X2 // P)], F32)
                 for h2 in range(PAIR):
                     nc.vector.tensor_tensor(
-                        out=edge_terms[:, :, h2, :].rearrange("p b (m n) -> p b m n", n=2),
+                        out=edge_terms[:, c, st0 : st0 + 2, h2, :].rearrange(
+                            "p b (m n) -> p b m n", n=2
+                        ),
                         in0=phi[pair][:, :, X2:F].rearrange("p b (m n) -> p b m n", n=P)[:, :, :, 1:3],
                         in1=edge_w[:, PAIR * c + h2]
                         .rearrange("p j m n -> p (j m) n")
                         .unsqueeze(1)
-                        .to_broadcast([P, 2, (NU - 1) * (X2 // P), 2]),
+                        .to_broadcast([P, 2, EDGES // 2, 2]),
                         op=ALU.mult,
                     )
-                edge_sums = feat.tile([P, 2, PAIR], F32)
+
+            def round_planes(pair):
+                c, st0 = planes_of(pair)
+                for b in range(2):
+                    nc.vector.tensor_scalar_mul(
+                        out=mk_planes[:, c, st0 + b, :],
+                        in0=phi[pair][:, b, :],
+                        scalar1=inv_norm[:, c, st0 + b : st0 + b + 1],
+                    )
+
+            def finish_denominators():
+                edge_sums = feat.tile([P, HKV, S_TILES, PAIR], F32, bufs=1)
                 nc.vector.tensor_reduce(
                     out=edge_sums[:], in_=edge_terms[:], axis=mybir.AxisListType.X, op=ALU.add
                 )
-                for b in range(2):
-                    nc.vector.tensor_scalar_mul(
-                        out=mk_planes[:, c, sg, 2 * a + b, :],
-                        in0=phi[pair][:, b, :],
-                        scalar1=inv_norm[pair][:, b : b + 1],
-                    )
                 nc.vector.tensor_tensor(out=dots[:], in0=dots[:], in1=edge_sums[:], op=ALU.add)
                 nc.vector.tensor_tensor(
                     out=dots[:],
                     in0=dots[:],
-                    in1=inv_norm[pair][:].unsqueeze(2).to_broadcast([P, 2, PAIR]),
+                    in1=inv_norm[:].unsqueeze(3).to_broadcast([P, HKV, S_TILES, PAIR]),
                     op=ALU.mult,
                 )
                 nc.vector.tensor_scalar(
                     out=dots[:], in0=dots[:], scalar1=-1.0, scalar2=-EPS, op0=ALU.mult, op1=ALU.add
                 )
-                st0 = PACK * sg + 2 * a
-                nc.vector.reciprocal(out=neg_inv_denom[:, c, st0 : st0 + 2, :], in_=dots[:])
+                nc.vector.reciprocal(out=neg_inv_denom[:], in_=dots[:])
 
             def transpose_features(grp):
+                c, sg = divmod(grp, S_PASSES)
                 mkT_grouped[grp] = feat.tile(
                     [P, F_PASSES, K_PASS, PACK], BF16, bufs=1, align_bytes=64, name="mkT_grouped"
                 )
                 mkT_words = mkT_grouped[grp][:].bitcast(F32)
-                c, sg = divmod(grp, S_PASSES)
                 for g in range(F_PASSES):
                     for a in range(PACK // 2):
                         flipped = flip_banks.tile([P, 2, 2, P], F32, tag="bank")
                         for b in range(2):
-                            plane_words = mk_planes[:, c, sg, 2 * a + b, :].bitcast(F32)
+                            plane_words = mk_planes[:, c, PACK * sg + 2 * a + b, :].bitcast(F32)
                             for u in range(2):
                                 w0 = (2 * g + u) * P
                                 nc.tensor.transpose(
@@ -298,44 +317,56 @@ def tile_armtapproach_pa_kernel(
                         mkT_scales[:, c, g, s_cols],
                     )
 
-            units = []
+            row_units = []
             for r0 in range(0, S, ROW_UNIT):
                 r_cols = slice(r0, r0 + ROW_UNIT)
-                units.append((hidden_states[r_cols, :], hs_codes[:, :, r_cols], hs_scales[:, :, r_cols]))
+                row_units.append(
+                    (True, hidden_states[r_cols, :], hs_codes[:, :, r_cols], hs_scales[:, :, r_cols])
+                )
             for r0 in range(0, HKV * D, ROW_UNIT):
                 r_cols = slice(r0, r0 + ROW_UNIT)
-                units.append((Wv[r_cols, :], w_codes[:, :, r_cols], w_scales[:, :, r_cols]))
+                row_units.append((True, Wv[r_cols, :], w_codes[:, :, r_cols], w_scales[:, :, r_cols]))
             for r0 in range(0, HID, ROW_UNIT):
                 o_cols = slice(HKV * D + r0, HKV * D + r0 + ROW_UNIT)
-                units.append((Wmb[r0 : r0 + ROW_UNIT, :], w_codes[:, :, o_cols], w_scales[:, :, o_cols]))
-            row_units = len(units)
+                row_units.append(
+                    (True, Wmb[r0 : r0 + ROW_UNIT, :], w_codes[:, :, o_cols], w_scales[:, :, o_cols])
+                )
+            mem_units = []
             for c in range(HKV):
                 for g in range(F_PASSES):
-                    units.append(
+                    mem_units.append(
                         (
+                            False,
                             memory[PAIR * c : PAIR * (c + 1), g * K_PASS : (g + 1) * K_PASS, :],
                             mem_codes[:, c, g, :],
                             mem_scales[:, c, g, :],
                         )
                     )
+            pairs = HKV * S_TILES // 2
+            share = (len(row_units) + len(mem_units)) // pairs
+            units = []
+            for step in range(pairs):
+                source = mem_units if step % 2 == 0 and len(mem_units) > 0 else row_units
+                units.extend(source[:share])
+                source[:share] = []
             raw, grouped = {}, {}
 
             def load_unit(n):
-                if n < row_units:
+                if units[n][0]:
                     raw[n] = stage.tile([P, ROW_UNIT // P, HID], BF16, name="raw")
                     nc.sync.dma_start(
-                        out=raw[n][:], in_=units[n][0].rearrange("(rt p) k -> p rt k", p=P)
+                        out=raw[n][:], in_=units[n][1].rearrange("(rt p) k -> p rt k", p=P)
                     )
                 else:
                     raw[n] = stage.tile([P, PAIR, PACK, D], BF16, name="raw")
                     for h2 in range(PAIR):
                         nc.sync.dma_start(
                             out=raw[n][:, h2].rearrange("q (u e) d -> q u (e d)", u=2),
-                            in_=units[n][0][h2].rearrange("(u q e) d -> q u (e d)", u=2, e=2),
+                            in_=units[n][1][h2].rearrange("(u q e) d -> q u (e d)", u=2, e=2),
                         )
 
             def lay_out_unit(n):
-                if n < row_units:
+                if units[n][0]:
                     grouped[n] = stage.tile(
                         [P, HID_PASSES, ROW_UNIT, PACK], BF16, align_bytes=64, name="grouped"
                     )
@@ -356,22 +387,17 @@ def tile_armtapproach_pa_kernel(
                 else:
                     grouped[n] = stage.tile([P, PAIR, D, PACK], BF16, align_bytes=64, name="grouped")
                     for h2 in range(PAIR):
-                        nc.scalar.copy(
-                            out=grouped[n][:, h2].rearrange("q (n i) t -> q n t i", i=4),
-                            in_=raw[n][:, h2].rearrange("q t (n i) -> q n t i", i=4),
-                        )
+                        interleave(nc.scalar.copy, grouped[n][:, h2], raw[n][:, h2])
 
             def quantise_unit(n):
-                if n < row_units:
+                if units[n][0]:
                     for g in range(HID_PASSES):
-                        quantise(nc, grouped[n][:, g], units[n][1][:, g, :], units[n][2][:, g, :])
+                        quantise(nc, grouped[n][:, g], units[n][2][:, g, :], units[n][3][:, g, :])
                 else:
                     quantise(
-                        nc, grouped[n][:].rearrange("q h d t -> q (h d) t"), units[n][1], units[n][2]
+                        nc, grouped[n][:].rearrange("q h d t -> q (h d) t"), units[n][2], units[n][3]
                     )
 
-            pairs = 2 * HKV * S_PASSES
-            share = len(units) // pairs
             with tc.manual_schedule():
                 load_keys(0)
                 load_keys(1)
@@ -388,7 +414,7 @@ def tile_armtapproach_pa_kernel(
                 build_band()
                 band_products(0)
                 inverse_norms(0)
-                for step in range(pairs + 1):
+                for step in range(pairs + 2):
                     if step + 1 < pairs:
                         inverse_norms(step + 1)
                         flip_x2(step + 1)
@@ -396,12 +422,13 @@ def tile_armtapproach_pa_kernel(
                         load_keys(step // 2 + 2)
                     if step + 3 < pairs:
                         relu_halves(step + 3)
-                    if step % 2 == 0 and step >= 2:
-                        quantise_features(step // 2 - 1)
-                    for n in range(max(step - 1, 0) * share, step * share):
+                    if step % 2 == 1 and step >= 3:
+                        quantise_features((step - 3) // 2)
+                    for n in range(max(step - 1, 0) * share, min(step, pairs) * share):
                         quantise_unit(n)
                     if step < pairs:
-                        denominators(step)
+                        dot_products(step)
+                        round_planes(step)
                     if step + 2 < pairs:
                         products(step + 2)
                     if step < pairs:
@@ -409,11 +436,12 @@ def tile_armtapproach_pa_kernel(
                             lay_out_unit(n)
                     if step + 1 < pairs:
                         band_products(step + 1)
-                    if step % 2 == 1:
+                    if step % 2 == 1 and step < pairs:
                         transpose_features(step // 2)
                     if step + 1 < pairs:
                         for n in range((step + 1) * share, (step + 2) * share):
                             load_unit(n)
+                finish_denominators()
 
         with tc.tile_pool(name="late", bufs=2, reuse_waits="tile") as late, tc.psum_pool(
             name="sum_banks", bufs=2, reuse_waits="tile"
@@ -494,19 +522,17 @@ def tile_armtapproach_pa_kernel(
                             out=wmv_planes[:, t, :], in0=diff[:], in1=gate[:], op=ALU.mult
                         )
                     wmv_grouped = late.tile([P, BANK, PACK], BF16, bufs=1, align_bytes=64)
-                    nc.vector.tensor_copy(
-                        out=wmv_grouped[:].rearrange("p (n i) t -> p n t i", i=4),
-                        in_=wmv_planes[:].rearrange("p t (n i) -> p n t i", i=4),
-                    )
+                    interleave(nc.vector.tensor_copy, wmv_grouped[:], wmv_planes[:])
                     quantise(nc, wmv_grouped[:], wmv_codes[:, sg, c_cols], wmv_scales[:, sg, c_cols])
 
                 for sg in range(S_PASSES):
                     for g in range(F_PASSES):
                         f_cols = slice(g * X2, (g + 1) * X2)
                         mkS_grouped = late.tile([P, X2, PACK], BF16, bufs=3, align_bytes=64)
-                        nc.scalar.copy(
-                            out=mkS_grouped[:].rearrange("p (n i) t -> p n t i", i=4),
-                            in_=mk_planes[:, c, sg, :, f_cols].rearrange("p t (n i) -> p n t i", i=4),
+                        interleave(
+                            nc.scalar.copy,
+                            mkS_grouped[:],
+                            mk_planes[:, c, PACK * sg : PACK * (sg + 1), f_cols],
                         )
                         quantise(
                             nc, mkS_grouped[:], mkS_codes[:, c, sg, f_cols], mkS_scales[:, c, sg, f_cols]
@@ -525,7 +551,7 @@ def tile_armtapproach_pa_kernel(
                         lambda g: wmv_scales[:, g, c_cols],
                     )
                     new = late.tile([P, PAIR, D], F32, bufs=4)
-                    if ft % 2 == 0:
+                    if c == HKV - 1:
                         nc.vector.tensor_tensor(
                             out=new[:].rearrange("f h d -> f (h d)"),
                             in0=delta[:],

@@ -213,10 +213,10 @@ def tile_armtapproach_pa_kernel(
                             ident_bf[:],
                         )
                 x2T[pair] = feat.tile([P, 2, X2_TILES, P], BF16, name="x2T")
-                nc.vector.tensor_copy(out=x2T[pair][:], in_=x2T_bank[:])
+                nc.scalar.copy(out=x2T[pair][:], in_=x2T_bank[:])
 
             def band_products(pair):
-                c, st0 = planes_of(pair)
+                c = planes_of(pair)[0]
                 for b in range(2):
                     for h2 in range(PAIR):
                         sums = dot_banks.tile([P, X2], F32, bufs=2 * PAIR, name="inner_sums")
@@ -551,7 +551,7 @@ def tile_armtapproach_pa_kernel(
                         lambda g: wmv_scales[:, g, c_cols],
                     )
                     new = late.tile([P, PAIR, D], F32, bufs=4)
-                    if c == HKV - 1:
+                    if ft % 2 == 1:
                         nc.vector.tensor_tensor(
                             out=new[:].rearrange("f h d -> f (h d)"),
                             in0=delta[:],

@@ -32,11 +32,16 @@ S_TILES = S // P
 S_PASSES = S // K_PASS
 HID_PASSES = HID // K_PASS
 F_PASSES = F // K_PASS
-X2_TILES = X2 // P
+REACH = P - NU
+FULL_TILES = X2 // REACH
+REST = X2 - FULL_TILES * REACH
+X2_TILES = FULL_TILES + 1
 W_ROWS = HKV * D + HID
+W_TILES = W_ROWS // P
+V_TILES = HKV * D // P
 ROW_UNIT = 256
-NORM_PITCH = X2 + 32
-EDGES = 2 * (NU - 1) * X2_TILES
+KEY_FRONT = 16
+KEY_PITCH = KEY_FRONT + D
 
 FLOPS = 2 * S * HID * W_ROWS + 2 * 2 * H * S * F * D
 
@@ -75,14 +80,17 @@ def tile_armtapproach_pa_kernel(
     nc = tc.nc
     with ExitStack() as whole:
         keep = whole.enter_context(tc.tile_pool(name="keep", bufs=1))
+        feat = whole.enter_context(tc.tile_pool(name="feat", bufs=2))
+        stage = whole.enter_context(tc.tile_pool(name="stage", bufs=2))
+        late = whole.enter_context(tc.tile_pool(name="late", bufs=2))
+        banks = whole.enter_context(tc.psum_pool(name="banks", bufs=3))
 
         ident = keep.tile([P, P], F32)
         make_identity(nc, ident[:])
         ident_bf = keep.tile([P, P], BF16)
         make_identity(nc, ident_bf[:])
 
-        bias_v = keep.tile([P, HKV * D], BF16)
-        bias_mb = keep.tile([P, HID], BF16)
+        biases = keep.tile([P, W_TILES], F32)
 
         hs_codes = keep.tile([P, HID_PASSES, S], U32, align_bytes=64)
         hs_scales = keep.tile([P, HID_PASSES, S], U8, align_bytes=64)
@@ -90,484 +98,697 @@ def tile_armtapproach_pa_kernel(
         w_scales = keep.tile([P, HID_PASSES, W_ROWS], U8, align_bytes=64)
         mem_codes = keep.tile([P, HKV, F_PASSES, PAIR * D], U32, align_bytes=64)
         mem_scales = keep.tile([P, HKV, F_PASSES, PAIR * D], U8, align_bytes=64)
-        mkT_codes = keep.tile([P, HKV, F_PASSES, S], U32, align_bytes=64)
-        mkT_scales = keep.tile([P, HKV, F_PASSES, S], U8, align_bytes=64)
-        neg_inv_denom = keep.tile([P, HKV, S_TILES, PAIR], F32)
-        mk_planes = keep.tile([P, HKV, S_TILES, F], BF16)
+        mkS_codes = keep.tile([P, HKV, S_PASSES, F], U32, align_bytes=64)
+        mkS_scales = keep.tile([P, HKV, S_PASSES, F], U8, align_bytes=64)
+        wmv_codes = keep.tile([P, S_PASSES, H * D], U32, align_bytes=64)
+        wmv_scales = keep.tile([P, S_PASSES, H * D], U8, align_bytes=64)
 
-        with tc.tile_pool(name="feat", bufs=2) as feat, tc.tile_pool(
-            name="stage", bufs=2
-        ) as stage, tc.psum_pool(name="flip_banks", bufs=3) as flip_banks, tc.psum_pool(
-            name="dot_banks", bufs=1
-        ) as dot_banks:
-            norm_w = feat.tile(
-                [P, H, NU, NORM_PITCH], BF16, bufs=1, align_bytes=64, tag="mkT_grouped"
+        band = keep.tile([P, H, FULL_TILES, REACH], BF16)
+        band_rest = keep.tile([P, H, REST], BF16)
+        norm_w = {}
+
+        def load_norm(c):
+            norm_w[c] = late.tile(
+                [P, PAIR, NU, X2], BF16, bufs=1, align_bytes=64, name="norm_w", tag="wmv_grouped"
             )
-            diagonals = feat.tile([P, NU, P], BF16, bufs=1)
-            band = feat.tile([P, H, X2_TILES, P], BF16, bufs=1)
-            edge_w = feat.tile([P, H, NU - 1, X2_TILES, 2], BF16, bufs=1)
+            nc.sync.dma_start(
+                out=norm_w[c][:].rearrange("p h j i -> p (h j) i"),
+                in_=norm[PAIR * c : PAIR * (c + 1), :]
+                .rearrange("h (j i) -> (h j) i", j=NU)
+                .partition_broadcast(P),
+            )
 
-            def load_norm():
-                nc.sync.dma_start(
-                    out=norm_w[:, :, :, 1 : 1 + X2].rearrange("p h j i -> p (h j) i"),
-                    in_=norm.rearrange("h (j i) -> (h j) i", j=NU).partition_broadcast(P),
+        def build_band(c):
+            heads = slice(PAIR * c, PAIR * (c + 1))
+            for j in range(1, NU + 1):
+                full = norm_w[c][:, :, j - 1, 0 : X2 - REST].rearrange(
+                    "p h (m n) -> p h m n", n=REACH
                 )
-
-            def build_band():
-                nc.gpsimd.memset(diagonals[:], 0.0)
-                for j in range(NU):
-                    nc.gpsimd.tensor_copy(out=diagonals[:, j, j:P], in_=ident_bf[:, 0 : P - j])
-                nc.gpsimd.tensor_copy(
-                    out=norm_w[:, :, :, 1 + X2 : 2 + X2], in_=norm_w[:, :, :, 1:2]
+                full_diagonal = (
+                    ident_bf[:, NU - j : NU - j + REACH]
+                    .unsqueeze(1)
+                    .unsqueeze(1)
+                    .to_broadcast([P, PAIR, FULL_TILES, REACH])
                 )
-                for j in range(1, NU):
-                    nc.gpsimd.tensor_copy(
-                        out=edge_w[:, :, j - 1],
-                        in_=norm_w[:, :, j, 1 : 1 + X2].rearrange("p h (m n) -> p h m n", n=P)[
-                            :, :, :, 1:3
-                        ],
-                    )
-                nc.gpsimd.memset(edge_w[:, :, 0, :, 1:2], 0.0)
-                for j in range(NU):
-                    window = norm_w[:, :, j, 2 : 2 + X2].rearrange("p h (m n) -> p h m n", n=P)
-                    diagonal = (
-                        diagonals[:, j, :].unsqueeze(1).unsqueeze(1).to_broadcast([P, H, X2_TILES, P])
-                    )
-                    if j == 0:
-                        nc.vector.tensor_tensor(out=band[:], in0=window, in1=diagonal, op=ALU.mult)
-                    else:
-                        term = feat.tile([P, H, X2_TILES, P], BF16, bufs=1)
-                        nc.vector.tensor_tensor(out=term[:], in0=window, in1=diagonal, op=ALU.mult)
-                        nc.vector.tensor_tensor(out=band[:], in0=band[:], in1=term[:], op=ALU.add)
-
-            k_rows, x2, phi, x2T, inner_sums, mkT_grouped = {}, {}, {}, {}, {}, {}
-            inv_norm = feat.tile([P, HKV, S_TILES], F32, bufs=1)
-            dots = feat.tile([P, HKV, S_TILES, PAIR], F32, bufs=1)
-            edge_terms = feat.tile([P, HKV, S_TILES, PAIR, EDGES], F32, bufs=1)
-
-            def planes_of(pair):
-                c, half = divmod(pair, S_TILES // 2)
-                return c, 2 * half
-
-            def load_keys(grp):
-                c, sg = divmod(grp, S_PASSES)
-                k_rows[grp] = feat.tile([P, PACK, D], BF16, name="k_rows")
-                nc.sync.dma_start(
-                    out=k_rows[grp][:],
-                    in_=k[c, sg * K_PASS : (sg + 1) * K_PASS, :].rearrange("(t p) d -> p t d", p=P),
+                rest = norm_w[c][:, :, j - 1, X2 - REST : X2]
+                rest_diagonal = (
+                    ident_bf[:, P - REST - j : P - j].unsqueeze(1).to_broadcast([P, PAIR, REST])
                 )
-
-            def relu_halves(pair):
-                grp, a = divmod(pair, 2)
-                x = k_rows[grp][:, 2 * a : 2 * a + 2, :]
-                x2[pair] = feat.tile([P, 2, NU + X2 + 1], BF16, bufs=4, name="x2")
-                nc.scalar.activation(
-                    out=x2[pair][:, :, NU + X2 : NU + X2 + 1], in_=x[:, :, 0:1], func=ACT.Relu
-                )
-                nc.scalar.activation(out=x2[pair][:, :, NU : NU + D], in_=x, func=ACT.Relu)
-                nc.scalar.activation(
-                    out=x2[pair][:, :, NU + D : NU + X2], in_=x, func=ACT.Relu, scale=-1.0
-                )
-                nc.scalar.activation(
-                    out=x2[pair][:, :, 0:NU], in_=x[:, :, D - NU : D], func=ACT.Relu, scale=-1.0
-                )
-
-            def products(pair):
-                phi[pair] = feat.tile([P, 2, F], F32, bufs=3, name="phi")
-                for j in range(1, NU + 1):
+                if j == 1:
                     nc.vector.tensor_tensor(
-                        out=phi[pair][:, :, (j - 1) * X2 : j * X2],
-                        in0=x2[pair][:, :, NU : NU + X2],
-                        in1=x2[pair][:, :, NU - j : NU - j + X2],
-                        op=ALU.mult,
+                        out=band[:, heads], in0=full, in1=full_diagonal, op=ALU.mult
                     )
-
-            def inverse_norms(pair):
-                c, st0 = planes_of(pair)
-                sum_sq = feat.tile([P, 2], F32)
-                for b in range(2):
-                    squares = feat.tile([P, F], BF16)
-                    nc.scalar.activation(
-                        out=squares[:],
-                        in_=phi[pair][:, b, :],
-                        func=ACT.Square,
-                        accum_out=sum_sq[:, b : b + 1],
+                    nc.gpsimd.tensor_tensor(
+                        out=band_rest[:, heads], in0=rest, in1=rest_diagonal, op=ALU.mult
                     )
-                nc.scalar.activation(
-                    out=sum_sq[:], in_=sum_sq[:], func=ACT.Relu, bias=-(TINY * TINY)
-                )
-                nc.scalar.activation(
-                    out=inv_norm[:, c, st0 : st0 + 2],
-                    in_=sum_sq[:],
-                    func=ACT.Abs_reciprocal_sqrt,
-                    bias=TINY * TINY,
-                )
-
-            def flip_x2(pair):
-                x2T_bank = dot_banks.tile([P, 2, X2_TILES, P], BF16)
-                for b in range(2):
-                    for m in range(X2_TILES):
-                        nc.tensor.transpose(
-                            x2T_bank[:, b, m, :],
-                            x2[pair][:, b, NU + m * P : NU + (m + 1) * P],
-                            ident_bf[:],
-                        )
-                x2T[pair] = feat.tile([P, 2, X2_TILES, P], BF16, name="x2T")
-                nc.scalar.copy(out=x2T[pair][:], in_=x2T_bank[:])
-
-            def band_products(pair):
-                c = planes_of(pair)[0]
-                for b in range(2):
-                    for h2 in range(PAIR):
-                        sums = dot_banks.tile([P, X2], F32, bufs=2 * PAIR, name="inner_sums")
-                        for m in range(X2_TILES):
-                            nc.tensor.matmul(
-                                out=sums[:, m * P : (m + 1) * P],
-                                lhsT=x2T[pair][:, b, m, :],
-                                rhs=band[:, PAIR * c + h2, m, :],
-                                start=True,
-                                stop=True,
-                            )
-                        inner_sums[(pair, b, h2)] = sums
-
-            def dot_products(pair):
-                c, st0 = planes_of(pair)
-                for b in range(2):
-                    for h2 in range(PAIR):
-                        weighted = feat.tile([P, X2], F32)
-                        nc.vector.scalar_tensor_tensor(
-                            out=weighted[:],
-                            in0=inner_sums[(pair, b, h2)][:],
-                            scalar=1.0,
-                            in1=x2[pair][:, b, NU + 1 : NU + 1 + X2],
-                            op0=ALU.mult,
-                            op1=ALU.mult,
-                            accum_out=dots[:, c, st0 + b, h2 : h2 + 1],
-                        )
-                for h2 in range(PAIR):
+                else:
+                    term = feat.tile([P, PAIR, FULL_TILES, REACH], BF16, tag="weighted")
+                    nc.vector.tensor_tensor(out=term[:], in0=full, in1=full_diagonal, op=ALU.mult)
                     nc.vector.tensor_tensor(
-                        out=edge_terms[:, c, st0 : st0 + 2, h2, :].rearrange(
-                            "p b (m n) -> p b m n", n=2
-                        ),
-                        in0=phi[pair][:, :, X2:F].rearrange("p b (m n) -> p b m n", n=P)[:, :, :, 1:3],
-                        in1=edge_w[:, PAIR * c + h2]
-                        .rearrange("p j m n -> p (j m) n")
-                        .unsqueeze(1)
-                        .to_broadcast([P, 2, EDGES // 2, 2]),
-                        op=ALU.mult,
+                        out=band[:, heads], in0=band[:, heads], in1=term[:], op=ALU.add
+                    )
+                    rest_term = feat.tile([P, PAIR, REST], BF16, bufs=1)
+                    nc.gpsimd.tensor_tensor(
+                        out=rest_term[:], in0=rest, in1=rest_diagonal, op=ALU.mult
+                    )
+                    nc.gpsimd.tensor_tensor(
+                        out=band_rest[:, heads], in0=band_rest[:, heads], in1=rest_term[:], op=ALU.add
                     )
 
-            def round_planes(pair):
-                c, st0 = planes_of(pair)
-                for b in range(2):
-                    nc.vector.tensor_scalar_mul(
-                        out=mk_planes[:, c, st0 + b, :],
-                        in0=phi[pair][:, b, :],
-                        scalar1=inv_norm[:, c, st0 + b : st0 + b + 1],
-                    )
+        bias_rows = keep.tile([P, P], BF16)
 
-            def finish_denominators():
-                edge_sums = feat.tile([P, HKV, S_TILES, PAIR], F32, bufs=1)
-                nc.vector.tensor_reduce(
-                    out=edge_sums[:], in_=edge_terms[:], axis=mybir.AxisListType.X, op=ALU.add
+        def load_biases():
+            nc.gpsimd.memset(bias_rows[:], 0.0)
+            nc.sync.dma_start(out=bias_rows[0:V_TILES, :], in_=bv.rearrange("(m p) -> m p", p=P))
+            nc.sync.dma_start(
+                out=bias_rows[V_TILES:W_TILES, :], in_=bmb.rearrange("(m p) -> m p", p=P)
+            )
+
+        def flip_biases():
+            bias_bank = banks.tile([P, X2_TILES, P], BF16, tag="flipped")
+            nc.tensor.transpose(bias_bank[:, 0, :], bias_rows[:], ident_bf[:])
+            nc.scalar.copy(out=biases[:], in_=bias_bank[:, 0, 0:W_TILES])
+
+        k_rows, half_signs, same_sign, x2, half_phi, scale_up, dots = {}, {}, {}, {}, {}, {}, {}
+        x2T, inner_sums, mk_planes, mkT_grouped, mkT_codes, mkT_scales = {}, {}, {}, {}, {}, {}
+        sum_sq, neg_inv_denom = {}, {}
+        minus_half = keep.tile([P, 2], F32)
+        nc.gpsimd.memset(minus_half[:], -0.5)
+
+        def load_keys(grp):
+            c, sg = divmod(grp, S_PASSES)
+            k_rows[grp] = feat.tile([P, PACK, KEY_PITCH], BF16, name="k_rows")
+            for u in range(2):
+                nc.sync.dma_start(
+                    out=k_rows[grp][:, 2 * u : 2 * u + 2, KEY_FRONT:],
+                    in_=k[c, sg * K_PASS + u * 2 * P : sg * K_PASS + (u + 1) * 2 * P, :].rearrange(
+                        "(p e) d -> p e d", e=2
+                    ),
                 )
-                nc.vector.tensor_tensor(out=dots[:], in0=dots[:], in1=edge_sums[:], op=ALU.add)
+
+        def keys_of(pair):
+            grp, u = divmod(pair, 2)
+            return k_rows[grp][:, 2 * u : 2 * u + 2, :]
+
+        def relu_halves(pair):
+            x = keys_of(pair)[:, :, KEY_FRONT:]
+            x2[pair] = feat.tile([P, 2, NU + X2], BF16, bufs=4, name="x2", tag="x2")
+            nc.vector.tensor_scalar_max(out=x2[pair][:, :, NU : NU + D], in0=x, scalar1=0.0)
+            for start, values in ((NU + D, x), (0, x[:, :, D - NU : D])):
+                nc.vector.tensor_scalar(
+                    out=x2[pair][:, :, start : start + values.shape[2]],
+                    in0=values,
+                    scalar1=-1.0,
+                    scalar2=0.0,
+                    op0=ALU.mult,
+                    op1=ALU.max,
+                )
+
+        def signs(grp):
+            x = k_rows[grp][:, :, KEY_FRONT:]
+            nc.scalar.mul(
+                out=k_rows[grp][:, :, KEY_FRONT - NU : KEY_FRONT], in_=x[:, :, D - NU : D], mul=-1.0
+            )
+            half_signs[grp] = feat.tile([P, PACK, D], BF16, name="half_signs", tag="half_signs")
+            nc.vector.tensor_scalar(
+                out=half_signs[grp][:],
+                in0=x,
+                scalar1=0.0,
+                scalar2=-0.5,
+                op0=ALU.is_ge,
+                op1=ALU.add,
+            )
+
+        def compare_signs(pair):
+            grp, u = divmod(pair, 2)
+            same_sign[pair] = feat.tile([P, 2, NU, D], BF16, name="same_sign")
+            for j in range(1, NU + 1):
                 nc.vector.tensor_tensor(
-                    out=dots[:],
-                    in0=dots[:],
-                    in1=inv_norm[:].unsqueeze(3).to_broadcast([P, HKV, S_TILES, PAIR]),
+                    out=same_sign[pair][:, :, j - 1, :],
+                    in0=keys_of(pair)[:, :, KEY_FRONT - j : KEY_FRONT - j + D],
+                    in1=half_signs[grp][:, 2 * u : 2 * u + 2, :],
                     op=ALU.mult,
                 )
-                nc.vector.tensor_scalar(
-                    out=dots[:], in0=dots[:], scalar1=-1.0, scalar2=-EPS, op0=ALU.mult, op1=ALU.add
+
+        def products(pair, b):
+            if b == 0:
+                half_phi[pair] = feat.tile(
+                    [P, 2, NU, D], F32, bufs=3, name="half_phi", tag="half_phi"
                 )
-                nc.vector.reciprocal(out=neg_inv_denom[:], in_=dots[:])
+            nc.vector.scalar_tensor_tensor(
+                out=half_phi[pair][:, b],
+                in0=same_sign[pair][:, b],
+                scalar=0.0,
+                in1=keys_of(pair)[:, b, KEY_FRONT:].unsqueeze(1).to_broadcast([P, NU, D]),
+                op0=ALU.max,
+                op1=ALU.mult,
+            )
 
-            def transpose_features(grp):
-                c, sg = divmod(grp, S_PASSES)
-                mkT_grouped[grp] = feat.tile(
-                    [P, F_PASSES, K_PASS, PACK], BF16, bufs=1, align_bytes=64, name="mkT_grouped"
-                )
-                mkT_words = mkT_grouped[grp][:].bitcast(F32)
-                for g in range(F_PASSES):
-                    for a in range(PACK // 2):
-                        flipped = flip_banks.tile([P, 2, 2, P], F32, tag="bank")
-                        for b in range(2):
-                            plane_words = mk_planes[:, c, PACK * sg + 2 * a + b, :].bitcast(F32)
-                            for u in range(2):
-                                w0 = (2 * g + u) * P
-                                nc.tensor.transpose(
-                                    flipped[:, b, u, :], plane_words[:, w0 : w0 + P], ident[:]
-                                )
-                        nc.scalar.copy(
-                            out=mkT_words[:, g, 2 * a * P : (2 * a + 2) * P, :].rearrange(
-                                "q (b r) u -> q b r u", b=2
-                            ),
-                            in_=flipped[:].rearrange("q b u r -> q b r u"),
-                        )
+        def square_sums(pair, b):
+            if b == 0:
+                sum_sq[pair] = feat.tile([P, 2], F32, name="sum_sq")
+            squares = feat.tile([P, NU * D], BF16, bufs=1)
+            nc.scalar.activation(
+                out=squares[:],
+                in_=half_phi[pair][:, b].rearrange("p j i -> p (j i)"),
+                func=ACT.Square,
+                accum_out=sum_sq[pair][:, b : b + 1],
+            )
 
-            def quantise_features(grp):
-                c, sg = divmod(grp, S_PASSES)
-                s_cols = slice(sg * K_PASS, (sg + 1) * K_PASS)
-                for g in range(F_PASSES):
-                    quantise(
-                        nc,
-                        mkT_grouped[grp][:, g],
-                        mkT_codes[:, c, g, s_cols],
-                        mkT_scales[:, c, g, s_cols],
-                    )
+        def inverse_norms(pair):
+            grp, u = divmod(pair, 2)
+            if u == 0:
+                scale_up[grp] = feat.tile([P, 2, PACK], F32, name="scale_up")
+            up = scale_up[grp][:, 0, 2 * u : 2 * u + 2]
+            down = scale_up[grp][:, 1, 2 * u : 2 * u + 2]
+            nc.gpsimd.tensor_scalar(
+                out=sum_sq[pair][:],
+                in0=sum_sq[pair][:],
+                scalar1=TINY * TINY / 4.0,
+                scalar2=None,
+                op0=ALU.max,
+            )
+            nc.gpsimd.tensor_tensor(out=up, in0=sum_sq[pair][:], in1=minus_half[:], op=ALU.pow)
+            nc.gpsimd.tensor_scalar(
+                out=down, in0=up, scalar1=-1.0, scalar2=0.0, op0=ALU.mult, op1=ALU.add
+            )
 
-            row_units = []
-            for r0 in range(0, S, ROW_UNIT):
-                r_cols = slice(r0, r0 + ROW_UNIT)
-                row_units.append(
-                    (True, hidden_states[r_cols, :], hs_codes[:, :, r_cols], hs_scales[:, :, r_cols])
-                )
-            for r0 in range(0, HKV * D, ROW_UNIT):
-                r_cols = slice(r0, r0 + ROW_UNIT)
-                row_units.append((True, Wv[r_cols, :], w_codes[:, :, r_cols], w_scales[:, :, r_cols]))
-            for r0 in range(0, HID, ROW_UNIT):
-                o_cols = slice(HKV * D + r0, HKV * D + r0 + ROW_UNIT)
-                row_units.append(
-                    (True, Wmb[r0 : r0 + ROW_UNIT, :], w_codes[:, :, o_cols], w_scales[:, :, o_cols])
-                )
-            mem_units = []
-            for c in range(HKV):
-                for g in range(F_PASSES):
-                    mem_units.append(
-                        (
-                            False,
-                            memory[PAIR * c : PAIR * (c + 1), g * K_PASS : (g + 1) * K_PASS, :],
-                            mem_codes[:, c, g, :],
-                            mem_scales[:, c, g, :],
-                        )
-                    )
-            pairs = HKV * S_TILES // 2
-            share = (len(row_units) + len(mem_units)) // pairs
-            units = []
-            for step in range(pairs):
-                source = mem_units if step % 2 == 0 and len(mem_units) > 0 else row_units
-                units.extend(source[:share])
-                source[:share] = []
-            raw, grouped = {}, {}
+        def flip_x2(pair, b):
+            if b == 0:
+                x2T[pair] = feat.tile([P, 2, X2_TILES, P], BF16, name="x2T")
+            x2T_bank = banks.tile([P, X2_TILES, P], BF16, tag="flipped")
+            for m in range(X2_TILES):
+                start = m * REACH if m < FULL_TILES else NU + X2 - P
+                nc.tensor.transpose(x2T_bank[:, m, :], x2[pair][:, b, start : start + P], ident_bf[:])
+            nc.scalar.copy(out=x2T[pair][:, b], in_=x2T_bank[:])
 
-            def load_unit(n):
-                if units[n][0]:
-                    raw[n] = stage.tile([P, ROW_UNIT // P, HID], BF16, name="raw")
-                    nc.sync.dma_start(
-                        out=raw[n][:], in_=units[n][1].rearrange("(rt p) k -> p rt k", p=P)
-                    )
-                else:
-                    raw[n] = stage.tile([P, PAIR, PACK, D], BF16, name="raw")
-                    for h2 in range(PAIR):
-                        nc.sync.dma_start(
-                            out=raw[n][:, h2].rearrange("q (u e) d -> q u (e d)", u=2),
-                            in_=units[n][1][h2].rearrange("(u q e) d -> q u (e d)", u=2, e=2),
-                        )
-
-            def lay_out_unit(n):
-                if units[n][0]:
-                    grouped[n] = stage.tile(
-                        [P, HID_PASSES, ROW_UNIT, PACK], BF16, align_bytes=64, name="grouped"
-                    )
-                    grouped_words = grouped[n][:].bitcast(F32)
-                    for rt in range(ROW_UNIT // P):
-                        raw_words = raw[n][:, rt, :].bitcast(F32)
-                        flipped = flip_banks.tile([P, HID_PASSES, 2, P], F32, tag="bank")
-                        for g in range(HID_PASSES):
-                            for u in range(2):
-                                w0 = (2 * g + u) * P
-                                nc.tensor.transpose(
-                                    flipped[:, g, u, :], raw_words[:, w0 : w0 + P], ident[:]
-                                )
-                        nc.scalar.copy(
-                            out=grouped_words[:, :, rt * P : (rt + 1) * P, :],
-                            in_=flipped[:].rearrange("q g u r -> q g r u"),
-                        )
-                else:
-                    grouped[n] = stage.tile([P, PAIR, D, PACK], BF16, align_bytes=64, name="grouped")
-                    for h2 in range(PAIR):
-                        interleave(nc.scalar.copy, grouped[n][:, h2], raw[n][:, h2])
-
-            def quantise_unit(n):
-                if units[n][0]:
-                    for g in range(HID_PASSES):
-                        quantise(nc, grouped[n][:, g], units[n][2][:, g, :], units[n][3][:, g, :])
-                else:
-                    quantise(
-                        nc, grouped[n][:].rearrange("q h d t -> q (h d) t"), units[n][2], units[n][3]
-                    )
-
-            with tc.manual_schedule():
-                load_keys(0)
-                load_keys(1)
-                load_norm()
-                for n in range(share):
-                    load_unit(n)
-                nc.sync.dma_start(out=bias_mb[:], in_=bmb.partition_broadcast(P))
-                nc.sync.dma_start(out=bias_v[:], in_=bv.partition_broadcast(P))
-                for pair in range(3):
-                    relu_halves(pair)
-                for pair in range(2):
-                    products(pair)
-                flip_x2(0)
-                build_band()
-                band_products(0)
-                inverse_norms(0)
-                for step in range(pairs + 2):
-                    if step + 1 < pairs:
-                        inverse_norms(step + 1)
-                        flip_x2(step + 1)
-                    if step % 2 == 0 and step + 4 < pairs:
-                        load_keys(step // 2 + 2)
-                    if step + 3 < pairs:
-                        relu_halves(step + 3)
-                    if step % 2 == 1 and step >= 3:
-                        quantise_features((step - 3) // 2)
-                    for n in range(max(step - 1, 0) * share, min(step, pairs) * share):
-                        quantise_unit(n)
-                    if step < pairs:
-                        dot_products(step)
-                        round_planes(step)
-                    if step + 2 < pairs:
-                        products(step + 2)
-                    if step < pairs:
-                        for n in range(step * share, (step + 1) * share):
-                            lay_out_unit(n)
-                    if step + 1 < pairs:
-                        band_products(step + 1)
-                    if step % 2 == 1 and step < pairs:
-                        transpose_features(step // 2)
-                    if step + 1 < pairs:
-                        for n in range((step + 1) * share, (step + 2) * share):
-                            load_unit(n)
-                finish_denominators()
-
-        with tc.tile_pool(name="late", bufs=2, reuse_waits="tile") as late, tc.psum_pool(
-            name="sum_banks", bufs=2, reuse_waits="tile"
-        ) as sum_banks:
-            wmv_codes = late.tile([P, S_PASSES, H * D], U32, bufs=1, align_bytes=64)
-            wmv_scales = late.tile([P, S_PASSES, H * D], U8, bufs=1, align_bytes=64)
-            mkS_codes = late.tile([P, HKV, S_PASSES, F], U32, bufs=1, align_bytes=64)
-            mkS_scales = late.tile([P, HKV, S_PASSES, F], U8, bufs=1, align_bytes=64)
-
-            old = late.tile([P, HKV, F // P, PAIR, D], BF16, bufs=1)
-            for c in range(HKV):
-                for ft in range(F // P):
-                    nc.sync.dma_start(
-                        out=old[:, c, ft],
-                        in_=memory[PAIR * c : PAIR * (c + 1), ft * P : (ft + 1) * P, :].rearrange(
-                            "h f d -> f h d"
-                        ),
-                    )
-
-            for c in range(HKV):
-                c_cols = slice(c * BANK, (c + 1) * BANK)
-
-                for sg in range(S_PASSES):
-                    wmv_planes = late.tile([P, PACK, BANK], BF16)
-                    for t in range(PACK):
-                        st = PACK * sg + t
-                        s_cols = slice(st * P, (st + 1) * P)
-
-                        def project(bank, o0, width):
-                            mx_group(
-                                nc,
-                                bank,
-                                HID_PASSES,
-                                lambda g: hs_codes[:, g, s_cols],
-                                lambda g: hs_scales[:, g, s_cols],
-                                lambda g: w_codes[:, g, o0 : o0 + width],
-                                lambda g: w_scales[:, g, o0 : o0 + width],
-                            )
-
-                        v_bank = sum_banks.tile([P, D], F32)
-                        project(v_bank[:], c * D, D)
-                        mb_bank = sum_banks.tile([P, BANK], F32)
-                        project(mb_bank[:], HKV * D + c * BANK, BANK)
-                        num_bank = sum_banks.tile([P, BANK], F32)
-                        mx_group(
-                            nc,
-                            num_bank[:],
-                            F_PASSES,
-                            lambda g: mkT_codes[:, c, g, s_cols],
-                            lambda g: mkT_scales[:, c, g, s_cols],
-                            lambda g: mem_codes[:, c, g, :],
-                            lambda g: mem_scales[:, c, g, :],
-                        )
-                        gate = late.tile([P, BANK], F32)
-                        nc.vector.tensor_tensor(
-                            out=gate[:], in0=mb_bank[:], in1=bias_mb[:, c_cols], op=ALU.add
-                        )
-                        nc.scalar.activation(out=gate[:], in_=gate[:], func=ACT.Sigmoid)
-                        v_biased = late.tile([P, D], F32)
-                        nc.vector.tensor_tensor(
-                            out=v_biased[:],
-                            in0=v_bank[:],
-                            in1=bias_v[:, c * D : (c + 1) * D],
-                            op=ALU.add,
-                        )
-                        diff = late.tile([P, BANK], F32)
-                        for h2 in range(PAIR):
-                            h_cols = slice(h2 * D, (h2 + 1) * D)
-                            nc.vector.scalar_tensor_tensor(
-                                out=diff[:, h_cols],
-                                in0=num_bank[:, h_cols],
-                                scalar=neg_inv_denom[:, c, st, h2 : h2 + 1],
-                                in1=v_biased[:],
-                                op0=ALU.mult,
-                                op1=ALU.add,
-                            )
-                        nc.gpsimd.tensor_tensor(
-                            out=wmv_planes[:, t, :], in0=diff[:], in1=gate[:], op=ALU.mult
-                        )
-                    wmv_grouped = late.tile([P, BANK, PACK], BF16, bufs=1, align_bytes=64)
-                    interleave(nc.vector.tensor_copy, wmv_grouped[:], wmv_planes[:])
-                    quantise(nc, wmv_grouped[:], wmv_codes[:, sg, c_cols], wmv_scales[:, sg, c_cols])
-
-                for sg in range(S_PASSES):
-                    for g in range(F_PASSES):
-                        f_cols = slice(g * X2, (g + 1) * X2)
-                        mkS_grouped = late.tile([P, X2, PACK], BF16, bufs=3, align_bytes=64)
-                        interleave(
-                            nc.scalar.copy,
-                            mkS_grouped[:],
-                            mk_planes[:, c, PACK * sg : PACK * (sg + 1), f_cols],
-                        )
-                        quantise(
-                            nc, mkS_grouped[:], mkS_codes[:, c, sg, f_cols], mkS_scales[:, c, sg, f_cols]
-                        )
-
-                for ft in range(F // P):
-                    f_cols = slice(ft * P, (ft + 1) * P)
-                    delta = sum_banks.tile([P, BANK], F32)
-                    mx_group(
-                        nc,
-                        delta[:],
-                        S_PASSES,
-                        lambda g: mkS_codes[:, c, g, f_cols],
-                        lambda g: mkS_scales[:, c, g, f_cols],
-                        lambda g: wmv_codes[:, g, c_cols],
-                        lambda g: wmv_scales[:, g, c_cols],
-                    )
-                    new = late.tile([P, PAIR, D], F32, bufs=4)
-                    if ft % 2 == 1:
-                        nc.vector.tensor_tensor(
-                            out=new[:].rearrange("f h d -> f (h d)"),
-                            in0=delta[:],
-                            in1=old[:, c, ft].rearrange("f h d -> f (h d)"),
-                            op=ALU.add,
-                        )
+        def band_products(pair, b):
+            c = pair // (2 * S_PASSES)
+            for h2 in range(PAIR):
+                sums = banks.tile([P, X2], F32, bufs=2, tag="inner_sums")
+                for m in range(X2_TILES):
+                    if m < FULL_TILES:
+                        out_cols = slice(m * REACH, (m + 1) * REACH)
+                        weights = band[:, PAIR * c + h2, m, :]
                     else:
-                        delta_sb = late.tile([P, BANK], F32)
-                        nc.scalar.copy(out=delta_sb[:], in_=delta[:])
-                        nc.gpsimd.tensor_tensor(
-                            out=new[:].rearrange("f h d -> f (h d)"),
-                            in0=delta_sb[:],
-                            in1=old[:, c, ft].rearrange("f h d -> f (h d)"),
-                            op=ALU.add,
-                        )
-                    nc.sync.dma_start(
-                        out=out[PAIR * c : PAIR * (c + 1), f_cols, :].rearrange("h f d -> f h d"),
-                        in_=new[:],
+                        out_cols = slice(X2 - REST, X2)
+                        weights = band_rest[:, PAIR * c + h2, :]
+                    nc.tensor.matmul(
+                        out=sums[:, out_cols],
+                        lhsT=x2T[pair][:, b, m, :],
+                        rhs=weights,
+                        start=True,
+                        stop=True,
                     )
+                inner_sums[(pair, b, h2)] = sums
+
+        def dot_products(pair, b):
+            grp, u = divmod(pair, 2)
+            if u == 0 and b == 0:
+                dots[grp] = feat.tile([P, PACK, PAIR], F32, name="dots")
+            for h2 in range(PAIR):
+                weighted = feat.tile([P, X2], F32, tag="weighted")
+                nc.vector.scalar_tensor_tensor(
+                    out=weighted[:],
+                    in0=inner_sums[(pair, b, h2)][:],
+                    scalar=1.0,
+                    in1=x2[pair][:, b, NU : NU + X2],
+                    op0=ALU.mult,
+                    op1=ALU.mult,
+                    accum_out=dots[grp][:, 2 * u + b, h2 : h2 + 1],
+                )
+
+        def round_plane(pair, b):
+            grp, u = divmod(pair, 2)
+            if u == 0 and b == 0:
+                mk_planes[grp] = feat.tile([P, PACK, F], BF16, name="mk_planes")
+            mk = mk_planes[grp][:, 2 * u + b, :].rearrange("p (j s x i) -> p s x j i", s=2, x=2, j=NU)
+            for sign in range(2):
+                nc.vector.tensor_scalar(
+                    out=mk[:, sign],
+                    in0=half_phi[pair][:, b].rearrange("p j (x i) -> p x j i", x=2),
+                    scalar1=scale_up[grp][:, sign, 2 * u + b : 2 * u + b + 1],
+                    scalar2=0.0,
+                    op0=ALU.mult,
+                    op1=ALU.max,
+                )
+
+        def finish_denominators(grp, part):
+            d = dots[grp][:]
+            if part == 0:
+                nc.vector.tensor_tensor(
+                    out=d,
+                    in0=d,
+                    in1=scale_up[grp][:, 0, :].unsqueeze(2).to_broadcast([P, PACK, PAIR]),
+                    op=ALU.mult,
+                )
+            elif part == 1:
+                nc.vector.tensor_scalar(
+                    out=d, in0=d, scalar1=-0.5, scalar2=-EPS, op0=ALU.mult, op1=ALU.add
+                )
+            else:
+                nc.vector.reciprocal(out=d, in_=d)
+
+        def spread_denominators(grp, h2):
+            if h2 == 0:
+                neg_inv_denom[grp] = late.tile([P, PAIR, K_PASS], F32, name="neg_inv_denom")
+            spread = banks.tile([P, 2, 2, P], F32, tag="flipped")
+            for u in range(2):
+                for e in range(2):
+                    nc.tensor.transpose(
+                        spread[:, u, e, :],
+                        dots[grp][:, 2 * u + e, h2 : h2 + 1].to_broadcast([P, P]),
+                        ident[:],
+                    )
+            nc.scalar.copy(
+                out=neg_inv_denom[grp][:, h2, :].rearrange("q (u p e) -> q u p e", u=2, e=2),
+                in_=spread[:].rearrange("q u e p -> q u p e"),
+            )
+
+        def transpose_features(pair, g):
+            grp, a = divmod(pair, 2)
+            if a == 0:
+                mkT_grouped[(grp, g)] = feat.tile(
+                    [P, K_PASS, PACK], BF16, bufs=F_PASSES, align_bytes=64, name="mkT_grouped"
+                )
+            mkT_words = mkT_grouped[(grp, g)][:].bitcast(F32)
+            flipped = banks.tile([P, 2, 2, P], F32, tag="flipped")
+            for b in range(2):
+                plane_words = mk_planes[grp][:, 2 * a + b, :].bitcast(F32)
+                for u in range(2):
+                    w0 = (2 * g + u) * P
+                    nc.tensor.transpose(flipped[:, b, u, :], plane_words[:, w0 : w0 + P], ident[:])
+            nc.scalar.copy(
+                out=mkT_words[:, 2 * a * P : (2 * a + 2) * P, :].rearrange("q (r b) u -> q r b u", b=2),
+                in_=flipped[:].rearrange("q b u r -> q r b u"),
+            )
+
+        def quantise_features(grp, g):
+            if g == 0:
+                mkT_codes[grp] = late.tile(
+                    [P, F_PASSES, K_PASS], U32, align_bytes=64, name="mkT_codes"
+                )
+                mkT_scales[grp] = late.tile(
+                    [P, F_PASSES, K_PASS], U8, align_bytes=64, name="mkT_scales"
+                )
+            quantise(nc, mkT_grouped[(grp, g)][:], mkT_codes[grp][:, g, :], mkT_scales[grp][:, g, :])
+
+        mkS_grouped = {}
+
+        def interleave_tokens(grp, g, engine_copy):
+            mkS_grouped[(grp, g)] = stage.tile(
+                [P, X2, PACK], BF16, align_bytes=64, name="mkS_grouped"
+            )
+            interleave(
+                engine_copy, mkS_grouped[(grp, g)][:], mk_planes[grp][:, :, g * X2 : (g + 1) * X2]
+            )
+
+        def quantise_tokens(grp, g):
+            c, sg = divmod(grp, S_PASSES)
+            f_cols = slice(g * X2, (g + 1) * X2)
+            quantise(
+                nc, mkS_grouped[(grp, g)][:], mkS_codes[:, c, sg, f_cols], mkS_scales[:, c, sg, f_cols]
+            )
+
+        def row_unit(source, r0, codes, scales, o0):
+            o_cols = slice(o0, o0 + ROW_UNIT)
+            return (True, source[r0 : r0 + ROW_UNIT, :], codes[:, :, o_cols], scales[:, :, o_cols])
+
+        def hs_unit(n):
+            return row_unit(hidden_states, n * ROW_UNIT, hs_codes, hs_scales, n * ROW_UNIT)
+
+        def wv_unit(c):
+            return row_unit(Wv, c * D, w_codes, w_scales, c * D)
+
+        def wmb_unit(h):
+            return row_unit(Wmb, h * D, w_codes, w_scales, HKV * D + h * D)
+
+        def mem_unit(c, g):
+            return (
+                False,
+                memory[PAIR * c : PAIR * (c + 1), g * K_PASS : (g + 1) * K_PASS, :],
+                mem_codes[:, c, g, :],
+                mem_scales[:, c, g, :],
+            )
+
+        units = [hs_unit(0), mem_unit(0, 0), hs_unit(1), mem_unit(0, 1), wv_unit(0), mem_unit(0, 2)]
+        units += [wmb_unit(0), wmb_unit(1), hs_unit(2), hs_unit(3), mem_unit(1, 0), wv_unit(1)]
+        units += [mem_unit(1, 1), wmb_unit(2), mem_unit(1, 2), wmb_unit(3)]
+        raw, grouped = {}, {}
+
+        def load_unit(n):
+            if units[n][0]:
+                raw[n] = stage.tile([P, ROW_UNIT // P, HID], BF16, name="raw")
+                nc.sync.dma_start(
+                    out=raw[n][:], in_=units[n][1].rearrange("(rt p) k -> p rt k", p=P)
+                )
+            else:
+                raw[n] = stage.tile([P, PAIR, PACK, D], BF16, name="raw")
+                for h2 in range(PAIR):
+                    nc.sync.dma_start(
+                        out=raw[n][:, h2].rearrange("q (u e) d -> q u (e d)", u=2),
+                        in_=units[n][1][h2].rearrange("(u q e) d -> q u (e d)", u=2, e=2),
+                    )
+
+        def lay_out_unit(n):
+            if units[n][0]:
+                grouped[n] = stage.tile(
+                    [P, HID_PASSES, ROW_UNIT, PACK], BF16, align_bytes=64, name="grouped"
+                )
+                grouped_words = grouped[n][:].bitcast(F32)
+                for rt in range(ROW_UNIT // P):
+                    raw_words = raw[n][:, rt, :].bitcast(F32)
+                    flipped = banks.tile([P, HID_PASSES, 2, P], F32, tag="flipped")
+                    for g in range(HID_PASSES):
+                        for u in range(2):
+                            w0 = (2 * g + u) * P
+                            nc.tensor.transpose(flipped[:, g, u, :], raw_words[:, w0 : w0 + P], ident[:])
+                    nc.scalar.copy(
+                        out=grouped_words[:, :, rt * P : (rt + 1) * P, :],
+                        in_=flipped[:].rearrange("q g u r -> q g r u"),
+                    )
+            else:
+                grouped[n] = stage.tile([P, PAIR, D, PACK], BF16, align_bytes=64, name="grouped")
+                for h2 in range(PAIR):
+                    interleave(nc.scalar.copy, grouped[n][:, h2], raw[n][:, h2])
+
+        def quantise_unit(n):
+            if units[n][0]:
+                for g in range(HID_PASSES):
+                    quantise(nc, grouped[n][:, g], units[n][2][:, g, :], units[n][3][:, g, :])
+            else:
+                quantise(nc, grouped[n][:].rearrange("q h d t -> q (h d) t"), units[n][2], units[n][3])
+
+        v_bank, mb_bank, num_bank, gate, diff = {}, {}, {}, {}, {}
+        wmv_grouped, wmvT = {}, {}
+
+        def project(bank, grp, m):
+            sg = grp % S_PASSES
+            o_cols = slice(m * P, (m + 1) * P)
+            s_cols = slice(sg * K_PASS, (sg + 1) * K_PASS)
+            mx_group(
+                nc,
+                bank,
+                HID_PASSES,
+                lambda g: w_codes[:, g, o_cols],
+                lambda g: w_scales[:, g, o_cols],
+                lambda g: hs_codes[:, g, s_cols],
+                lambda g: hs_scales[:, g, s_cols],
+            )
+
+        def v_sums(grp, dh):
+            v_bank[(grp, dh)] = banks.tile([P, K_PASS], F32, bufs=1, name="v_bank")
+            project(v_bank[(grp, dh)][:], grp, grp // S_PASSES * (D // P) + dh)
+
+        def head_sums(grp, dh, h2):
+            c = grp // S_PASSES
+            mb_bank[(grp, dh, h2)] = banks.tile([P, K_PASS], F32, bufs=1, name="mb_bank")
+            project(
+                mb_bank[(grp, dh, h2)][:], grp, V_TILES + (PAIR * c + h2) * (D // P) + dh
+            )
+            num_bank[(grp, dh, h2)] = banks.tile([P, K_PASS], F32, bufs=1, name="num_bank")
+            d_cols = slice(h2 * D + dh * P, h2 * D + (dh + 1) * P)
+            mx_group(
+                nc,
+                num_bank[(grp, dh, h2)][:],
+                F_PASSES,
+                lambda g: mem_codes[:, c, g, d_cols],
+                lambda g: mem_scales[:, c, g, d_cols],
+                lambda g: mkT_codes[grp][:, g, :],
+                lambda g: mkT_scales[grp][:, g, :],
+            )
+
+        def gate_values(grp, dh, h2):
+            mb_tile = V_TILES + (PAIR * (grp // S_PASSES) + h2) * (D // P) + dh
+            gate[(grp, dh, h2)] = late.tile([P, K_PASS], F32, name="gate")
+            nc.scalar.activation(
+                out=gate[(grp, dh, h2)][:],
+                in_=mb_bank[(grp, dh, h2)][:],
+                func=ACT.Sigmoid,
+                bias=biases[:, mb_tile : mb_tile + 1],
+            )
+
+        def scale_num(grp, dh, h2):
+            diff[(grp, dh, h2)] = late.tile([P, K_PASS], F32, name="diff")
+            nc.vector.tensor_tensor(
+                out=diff[(grp, dh, h2)][:],
+                in0=num_bank[(grp, dh, h2)][:],
+                in1=neg_inv_denom[grp][:, h2, :],
+                op=ALU.mult,
+            )
+
+        def write_values(grp, dh, h2):
+            v_tile = grp // S_PASSES * (D // P) + dh
+            if h2 == 0:
+                wmvT[(grp, dh)] = late.tile([P, PAIR, K_PASS], BF16, name="wmvT")
+            nc.vector.scalar_tensor_tensor(
+                out=diff[(grp, dh, h2)][:],
+                in0=v_bank[(grp, dh)][:],
+                scalar=biases[:, v_tile : v_tile + 1],
+                in1=diff[(grp, dh, h2)][:],
+                op0=ALU.add,
+                op1=ALU.add,
+            )
+            nc.gpsimd.tensor_tensor(
+                out=wmvT[(grp, dh)][:, h2, :],
+                in0=diff[(grp, dh, h2)][:],
+                in1=gate[(grp, dh, h2)][:],
+                op=ALU.mult,
+            )
+
+        def turn_values(grp, dh):
+            if dh == 0:
+                wmv_grouped[grp] = late.tile(
+                    [P, BANK, PACK], BF16, bufs=1, align_bytes=64, name="wmv_grouped", tag="wmv_grouped"
+                )
+            wmv_words = wmv_grouped[grp][:].bitcast(F32)
+            flipped = banks.tile([P, PAIR, 2, P], F32, tag="flipped")
+            for h2 in range(PAIR):
+                raw_words = wmvT[(grp, dh)][:, h2, :].bitcast(F32)
+                for u in range(2):
+                    nc.tensor.transpose(flipped[:, h2, u, :], raw_words[:, u * P : (u + 1) * P], ident[:])
+            nc.scalar.copy(
+                out=wmv_words.rearrange("p (h m d) u -> p h m d u", h=PAIR, m=D // P)[:, :, dh],
+                in_=flipped[:].rearrange("p h u d -> p h d u"),
+            )
+
+        def quantise_values(grp):
+            c, sg = divmod(grp, S_PASSES)
+            c_cols = slice(c * BANK, (c + 1) * BANK)
+            quantise(nc, wmv_grouped[grp][:], wmv_codes[:, sg, c_cols], wmv_scales[:, sg, c_cols])
+
+        old, new_tiles = {}, {}
+
+        def load_old(n):
+            c, ft = divmod(2 * n, F // P)
+            old[n] = feat.tile([P, 2, PAIR, D], BF16, bufs=4, name="old", tag="x2")
+            for t in range(2):
+                nc.sync.dma_start(
+                    out=old[n][:, t],
+                    in_=memory[PAIR * c : PAIR * (c + 1), (ft + t) * P : (ft + t + 1) * P, :].rearrange(
+                        "h f d -> f h d"
+                    ),
+                )
+
+        def write_memory(n):
+            c, ft = divmod(n, F // P)
+            old_tile = old[n // 2][:, n % 2].rearrange("f h d -> f (h d)")
+            c_cols = slice(c * BANK, (c + 1) * BANK)
+            f_cols = slice(ft * P, (ft + 1) * P)
+            if n % 2 == 0:
+                delta = banks.tile([P, BANK], F32, bufs=2, tag="inner_sums")
+            else:
+                delta = banks.tile([P, BANK], F32, tag="flipped")
+            mx_group(
+                nc,
+                delta[:],
+                S_PASSES,
+                lambda g: mkS_codes[:, c, g, f_cols],
+                lambda g: mkS_scales[:, c, g, f_cols],
+                lambda g: wmv_codes[:, g, c_cols],
+                lambda g: wmv_scales[:, g, c_cols],
+            )
+            if ft % NU == 0:
+                new_tiles[0] = feat.tile(
+                    [P, NU, PAIR, D], F32, bufs=3, name="new_tiles", tag="half_phi"
+                )
+            new = new_tiles[0][:, ft % NU]
+            if ft % 2 == 1:
+                nc.vector.tensor_tensor(
+                    out=new.rearrange("f h d -> f (h d)"),
+                    in0=delta[:],
+                    in1=old_tile,
+                    op=ALU.add,
+                )
+            else:
+                delta_sb = feat.tile([P, BANK], F32, tag="half_signs")
+                nc.scalar.copy(out=delta_sb[:], in_=delta[:])
+                nc.gpsimd.tensor_tensor(
+                    out=new.rearrange("f h d -> f (h d)"),
+                    in0=delta_sb[:],
+                    in1=old_tile,
+                    op=ALU.add,
+                )
+            nc.sync.dma_start(
+                out=out[PAIR * c : PAIR * (c + 1), f_cols, :].rearrange("h f d -> f h d"),
+                in_=new,
+            )
+
+        pairs = 2 * HKV * S_PASSES
+        groups = HKV * S_PASSES
+        tiles = HKV * F // P
+        done = {"units": 0, "quantised": 0, "tiles": 0}
+
+        def advance_unit():
+            n = done["units"]
+            if n < len(units):
+                lay_out_unit(n)
+                if n + 2 < len(units):
+                    load_unit(n + 2)
+                done["units"] = n + 1
+
+        def quantise_next():
+            n = done["quantised"]
+            if n < done["units"]:
+                quantise_unit(n)
+                done["quantised"] = n + 1
+
+        def write_next(step):
+            n = done["tiles"]
+            if step >= pairs and n < tiles:
+                write_memory(n)
+                if n % 2 == 1 and n // 2 + 4 < tiles // 2:
+                    load_old(n // 2 + 4)
+                done["tiles"] = n + 1
+
+        with tc.manual_schedule():
+            load_keys(0)
+            load_norm(0)
+            load_keys(1)
+            load_unit(0)
+            load_unit(1)
+            load_biases()
+            signs(0)
+            relu_halves(0)
+            compare_signs(0)
+            flip_x2(0, 0)
+            products(0, 0)
+            flip_x2(0, 1)
+            products(0, 1)
+            square_sums(0, 0)
+            build_band(0)
+            square_sums(0, 1)
+            inverse_norms(0)
+            load_norm(1)
+            band_products(0, 0)
+            relu_halves(1)
+            compare_signs(1)
+            advance_unit()
+            products(1, 0)
+            products(1, 1)
+            signs(1)
+            flip_biases()
+            relu_halves(2)
+            for step in range(pairs + 4):
+                part = step - 3
+                grp, dh = divmod(part, 2)
+                working = 0 <= part < 2 * groups
+                turning = 0 < part <= 2 * groups
+                ready, second = divmod(step - 2, 2)
+                fresh = 0 <= ready < groups and second == 0
+                if working:
+                    v_sums(grp, dh)
+                    head_sums(grp, dh, 0)
+                if step < pairs:
+                    dot_products(step, 0)
+                    band_products(step, 1)
+                if working:
+                    gate_values(grp, dh, 0)
+                if fresh:
+                    finish_denominators(ready, 0)
+                if step + 1 < pairs:
+                    flip_x2(step + 1, 0)
+                if 0 < step <= pairs:
+                    transpose_features(step - 1, 0)
+                if step + 1 < pairs:
+                    square_sums(step + 1, 0)
+                quantise_next()
+                if fresh:
+                    finish_denominators(ready, 1)
+                if step + 2 < pairs:
+                    compare_signs(step + 2)
+                if working:
+                    scale_num(grp, dh, 0)
+                write_next(step)
+                advance_unit()
+                if 0 < step <= pairs:
+                    transpose_features(step - 1, 1)
+                if 0 <= ready < groups:
+                    if second:
+                        quantise_tokens(ready, 1)
+                    interleave_tokens(ready, 2 if second else 0, nc.scalar.copy)
+                if step + 2 < pairs:
+                    products(step + 2, 0)
+                if fresh:
+                    finish_denominators(ready, 2)
+                if working:
+                    write_values(grp, dh, 0)
+                    head_sums(grp, dh, 1)
+                if step + 3 < pairs:
+                    relu_halves(step + 3)
+                write_next(step)
+                if step < pairs:
+                    dot_products(step, 1)
+                if step + 1 < pairs:
+                    flip_x2(step + 1, 1)
+                if 0 < step <= pairs:
+                    transpose_features(step - 1, 2)
+                if step + 1 < pairs:
+                    square_sums(step + 1, 1)
+                    inverse_norms(step + 1)
+                if working:
+                    gate_values(grp, dh, 1)
+                if step + 2 < pairs:
+                    products(step + 2, 1)
+                quantise_next()
+                write_next(step)
+                if step + 1 < pairs:
+                    band_products(step + 1, 0)
+                advance_unit()
+                if step < 2:
+                    advance_unit()
+                if step < pairs:
+                    round_plane(step, 0)
+                if working:
+                    scale_num(grp, dh, 1)
+                if step < pairs:
+                    round_plane(step, 1)
+                if working:
+                    write_values(grp, dh, 1)
+                if turning:
+                    turn_values(*divmod(part - 1, 2))
+                if fresh:
+                    for h2 in range(PAIR):
+                        spread_denominators(ready, h2)
+                    for g in range(F_PASSES):
+                        quantise_features(ready, g)
+                if fresh:
+                    quantise_tokens(ready, 0)
+                    interleave_tokens(ready, 1, nc.scalar.copy)
+                elif 0 <= ready < groups:
+                    quantise_tokens(ready, 2)
+                if turning and part % 2 == 0:
+                    quantise_values(part // 2 - 1)
+                if step % 2 == 0 and step + 4 < pairs:
+                    load_keys(step // 2 + 2)
+                if step % 2 == 1 and step + 3 < pairs:
+                    signs(step // 2 + 2)
+                if step == 1:
+                    build_band(1)
+                if step < 2:
+                    quantise_next()
+                if step == pairs - 1:
+                    for n in range(4):
+                        load_old(n)
+            while done["tiles"] < tiles:
+                write_next(pairs)

@@ -108,9 +108,7 @@ def tile_armtapproach_pa_kernel(
         norm_w = {}
 
         def load_norm(c):
-            norm_w[c] = late.tile(
-                [P, PAIR, NU, X2], BF16, bufs=1, align_bytes=64, name="norm_w", tag="wmv_grouped"
-            )
+            norm_w[c] = late.tile([P, PAIR, NU, X2], BF16, bufs=1, name="norm_w", tag="neg_inv_denom")
             nc.sync.dma_start(
                 out=norm_w[c][:].rearrange("p h j i -> p (h j) i"),
                 in_=norm[PAIR * c : PAIR * (c + 1), :]
@@ -118,9 +116,9 @@ def tile_armtapproach_pa_kernel(
                 .partition_broadcast(P),
             )
 
-        def build_band(c):
+        def build_band(c, rolls):
             heads = slice(PAIR * c, PAIR * (c + 1))
-            for j in range(1, NU + 1):
+            for j in rolls:
                 full = norm_w[c][:, :, j - 1, 0 : X2 - REST].rearrange(
                     "p h (m n) -> p h m n", n=REACH
                 )
@@ -321,7 +319,7 @@ def tile_armtapproach_pa_kernel(
         def round_plane(pair, b):
             grp, u = divmod(pair, 2)
             if u == 0 and b == 0:
-                mk_planes[grp] = feat.tile([P, PACK, F], BF16, name="mk_planes")
+                mk_planes[grp] = feat.tile([P, PACK, F], BF16, name="mk_planes", tag="mk_planes")
             mk = mk_planes[grp][:, 2 * u + b, :].rearrange("p (j s x i) -> p s x j i", s=2, x=2, j=NU)
             for sign in range(2):
                 nc.vector.tensor_scalar(
@@ -351,7 +349,9 @@ def tile_armtapproach_pa_kernel(
 
         def spread_denominators(grp, h2):
             if h2 == 0:
-                neg_inv_denom[grp] = late.tile([P, PAIR, K_PASS], F32, name="neg_inv_denom")
+                neg_inv_denom[grp] = late.tile(
+                    [P, PAIR, K_PASS], F32, bufs=1, name="neg_inv_denom", tag="neg_inv_denom"
+                )
             spread = banks.tile([P, 2, 2, P], F32, tag="flipped")
             for u in range(2):
                 for e in range(2):
@@ -496,148 +496,131 @@ def tile_armtapproach_pa_kernel(
                 lambda g: hs_scales[:, g, s_cols],
             )
 
-        def v_sums(grp, dh):
-            v_bank[(grp, dh)] = banks.tile([P, K_PASS], F32, bufs=1, name="v_bank")
-            project(v_bank[(grp, dh)][:], grp, grp // S_PASSES * (D // P) + dh)
-
-        def head_sums(grp, dh, h2):
+        def block_sums(block):
+            grp, h2, dh = block
             c = grp // S_PASSES
-            mb_bank[(grp, dh, h2)] = banks.tile([P, K_PASS], F32, bufs=1, name="mb_bank")
-            project(
-                mb_bank[(grp, dh, h2)][:], grp, V_TILES + (PAIR * c + h2) * (D // P) + dh
-            )
-            num_bank[(grp, dh, h2)] = banks.tile([P, K_PASS], F32, bufs=1, name="num_bank")
+            num_bank[block] = banks.tile([P, K_PASS], F32, bufs=1, name="num_bank")
             d_cols = slice(h2 * D + dh * P, h2 * D + (dh + 1) * P)
             mx_group(
                 nc,
-                num_bank[(grp, dh, h2)][:],
+                num_bank[block][:],
                 F_PASSES,
                 lambda g: mem_codes[:, c, g, d_cols],
                 lambda g: mem_scales[:, c, g, d_cols],
                 lambda g: mkT_codes[grp][:, g, :],
                 lambda g: mkT_scales[grp][:, g, :],
             )
+            mb_bank[block] = banks.tile([P, K_PASS], F32, bufs=1, name="mb_bank")
+            project(mb_bank[block][:], grp, V_TILES + (PAIR * c + h2) * (D // P) + dh)
+            v_bank[block] = banks.tile([P, K_PASS], F32, bufs=1, name="v_bank")
+            project(v_bank[block][:], grp, c * (D // P) + dh)
 
-        def gate_values(grp, dh, h2):
+        def gate_values(block):
+            grp, h2, dh = block
             mb_tile = V_TILES + (PAIR * (grp // S_PASSES) + h2) * (D // P) + dh
-            gate[(grp, dh, h2)] = late.tile([P, K_PASS], F32, name="gate")
+            gate[block] = late.tile([P, K_PASS], F32, name="gate")
             nc.scalar.activation(
-                out=gate[(grp, dh, h2)][:],
-                in_=mb_bank[(grp, dh, h2)][:],
+                out=gate[block][:],
+                in_=mb_bank[block][:],
                 func=ACT.Sigmoid,
                 bias=biases[:, mb_tile : mb_tile + 1],
             )
 
-        def scale_num(grp, dh, h2):
-            diff[(grp, dh, h2)] = late.tile([P, K_PASS], F32, name="diff")
+        def scale_num(block):
+            grp, h2, dh = block
+            diff[block] = late.tile([P, K_PASS], F32, name="diff")
             nc.vector.tensor_tensor(
-                out=diff[(grp, dh, h2)][:],
-                in0=num_bank[(grp, dh, h2)][:],
+                out=diff[block][:],
+                in0=num_bank[block][:],
                 in1=neg_inv_denom[grp][:, h2, :],
                 op=ALU.mult,
             )
 
-        def write_values(grp, dh, h2):
+        def write_values(block):
+            grp, h2, dh = block
             v_tile = grp // S_PASSES * (D // P) + dh
-            if h2 == 0:
-                wmvT[(grp, dh)] = late.tile([P, PAIR, K_PASS], BF16, name="wmvT")
+            if dh == 0:
+                wmvT[(grp, h2)] = late.tile([P, D // P, K_PASS], BF16, name="wmvT")
             nc.vector.scalar_tensor_tensor(
-                out=diff[(grp, dh, h2)][:],
-                in0=v_bank[(grp, dh)][:],
+                out=diff[block][:],
+                in0=v_bank[block][:],
                 scalar=biases[:, v_tile : v_tile + 1],
-                in1=diff[(grp, dh, h2)][:],
+                in1=diff[block][:],
                 op0=ALU.add,
                 op1=ALU.add,
             )
             nc.gpsimd.tensor_tensor(
-                out=wmvT[(grp, dh)][:, h2, :],
-                in0=diff[(grp, dh, h2)][:],
-                in1=gate[(grp, dh, h2)][:],
-                op=ALU.mult,
+                out=wmvT[(grp, h2)][:, dh, :], in0=diff[block][:], in1=gate[block][:], op=ALU.mult
             )
 
-        def turn_values(grp, dh):
-            if dh == 0:
-                wmv_grouped[grp] = late.tile(
-                    [P, BANK, PACK], BF16, bufs=1, align_bytes=64, name="wmv_grouped", tag="wmv_grouped"
-                )
-            wmv_words = wmv_grouped[grp][:].bitcast(F32)
-            flipped = banks.tile([P, PAIR, 2, P], F32, tag="flipped")
-            for h2 in range(PAIR):
-                raw_words = wmvT[(grp, dh)][:, h2, :].bitcast(F32)
+        def turn_values(grp, h2):
+            wmv_grouped[(grp, h2)] = late.tile(
+                [P, D, PACK], BF16, align_bytes=64, name="wmv_grouped"
+            )
+            flipped = banks.tile([P, D // P, 2, P], F32, tag="flipped")
+            for dh in range(D // P):
+                raw_words = wmvT[(grp, h2)][:, dh, :].bitcast(F32)
                 for u in range(2):
-                    nc.tensor.transpose(flipped[:, h2, u, :], raw_words[:, u * P : (u + 1) * P], ident[:])
+                    nc.tensor.transpose(flipped[:, dh, u, :], raw_words[:, u * P : (u + 1) * P], ident[:])
             nc.scalar.copy(
-                out=wmv_words.rearrange("p (h m d) u -> p h m d u", h=PAIR, m=D // P)[:, :, dh],
-                in_=flipped[:].rearrange("p h u d -> p h d u"),
+                out=wmv_grouped[(grp, h2)][:].bitcast(F32).rearrange("p (m d) u -> p m d u", m=D // P),
+                in_=flipped[:].rearrange("p m u d -> p m d u"),
             )
 
-        def quantise_values(grp):
+        def quantise_values(grp, h2):
             c, sg = divmod(grp, S_PASSES)
-            c_cols = slice(c * BANK, (c + 1) * BANK)
-            quantise(nc, wmv_grouped[grp][:], wmv_codes[:, sg, c_cols], wmv_scales[:, sg, c_cols])
+            h_cols = slice((PAIR * c + h2) * D, (PAIR * c + h2 + 1) * D)
+            quantise(
+                nc, wmv_grouped[(grp, h2)][:], wmv_codes[:, sg, h_cols], wmv_scales[:, sg, h_cols]
+            )
 
-        old, new_tiles = {}, {}
+        old, delta, new = {}, {}, {}
 
-        def load_old(n):
-            c, ft = divmod(2 * n, F // P)
-            old[n] = feat.tile([P, 2, PAIR, D], BF16, bufs=4, name="old", tag="x2")
-            for t in range(2):
+        def rows_of(tensor, n):
+            h, r = divmod(n, F // (2 * P))
+            return tensor[h, r * 2 * P : (r + 1) * 2 * P, :].rearrange("(t f) d -> f t d", f=P)
+
+        def load_old(c):
+            old[c] = feat.tile([P, PAIR, F // P, D], BF16, name="old", tag="mk_planes")
+            for h2 in range(PAIR):
                 nc.sync.dma_start(
-                    out=old[n][:, t],
-                    in_=memory[PAIR * c : PAIR * (c + 1), (ft + t) * P : (ft + t + 1) * P, :].rearrange(
-                        "h f d -> f h d"
-                    ),
+                    out=old[c][:, h2],
+                    in_=memory[PAIR * c + h2].rearrange("(r f) d -> f r d", f=P),
                 )
 
-        def write_memory(n):
-            c, ft = divmod(n, F // P)
-            old_tile = old[n // 2][:, n % 2].rearrange("f h d -> f (h d)")
-            c_cols = slice(c * BANK, (c + 1) * BANK)
-            f_cols = slice(ft * P, (ft + 1) * P)
+        def write_sums(n):
+            h, r = divmod(n, F // (2 * P))
+            c = h // PAIR
+            h_cols = slice(h * D, (h + 1) * D)
             if n % 2 == 0:
-                delta = banks.tile([P, BANK], F32, bufs=2, tag="inner_sums")
+                delta[n] = banks.tile([P, 2, D], F32, bufs=2, name="delta", tag="inner_sums")
             else:
-                delta = banks.tile([P, BANK], F32, tag="flipped")
-            mx_group(
-                nc,
-                delta[:],
-                S_PASSES,
-                lambda g: mkS_codes[:, c, g, f_cols],
-                lambda g: mkS_scales[:, c, g, f_cols],
-                lambda g: wmv_codes[:, g, c_cols],
-                lambda g: wmv_scales[:, g, c_cols],
-            )
-            if ft % NU == 0:
-                new_tiles[0] = feat.tile(
-                    [P, NU, PAIR, D], F32, bufs=3, name="new_tiles", tag="half_phi"
+                delta[n] = banks.tile([P, 2, D], F32, name="delta", tag="flipped")
+            for t in range(2):
+                f_cols = slice((2 * r + t) * P, (2 * r + t + 1) * P)
+                mx_group(
+                    nc,
+                    delta[n][:, t, :],
+                    S_PASSES,
+                    lambda g: mkS_codes[:, c, g, f_cols],
+                    lambda g: mkS_scales[:, c, g, f_cols],
+                    lambda g: wmv_codes[:, g, h_cols],
+                    lambda g: wmv_scales[:, g, h_cols],
                 )
-            new = new_tiles[0][:, ft % NU]
-            if ft % 2 == 1:
-                nc.vector.tensor_tensor(
-                    out=new.rearrange("f h d -> f (h d)"),
-                    in0=delta[:],
-                    in1=old_tile,
-                    op=ALU.add,
-                )
-            else:
-                delta_sb = feat.tile([P, BANK], F32, tag="half_signs")
-                nc.scalar.copy(out=delta_sb[:], in_=delta[:])
-                nc.gpsimd.tensor_tensor(
-                    out=new.rearrange("f h d -> f (h d)"),
-                    in0=delta_sb[:],
-                    in1=old_tile,
-                    op=ALU.add,
-                )
-            nc.sync.dma_start(
-                out=out[PAIR * c : PAIR * (c + 1), f_cols, :].rearrange("h f d -> f h d"),
-                in_=new,
-            )
+
+        def write_rows(n):
+            h, r = divmod(n, F // (2 * P))
+            c, h2 = divmod(h, PAIR)
+            if n % NU == 0:
+                new[n // NU] = feat.tile([P, NU, 2, D], F32, bufs=3, name="new", tag="half_phi")
+            new_tile = new[n // NU][:, n % NU]
+            old_tile = old[c][:, h2, 2 * r : 2 * r + 2, :]
+            nc.vector.tensor_tensor(out=new_tile, in0=delta[n][:], in1=old_tile, op=ALU.add)
+            nc.sync.dma_start(out=rows_of(out, n), in_=new_tile)
 
         pairs = 2 * HKV * S_PASSES
         groups = HKV * S_PASSES
-        tiles = HKV * F // P
-        done = {"units": 0, "quantised": 0, "tiles": 0}
+        done = {"units": 0, "quantised": 0, "sums": 0, "rows": 0}
 
         def advance_unit():
             n = done["units"]
@@ -653,13 +636,13 @@ def tile_armtapproach_pa_kernel(
                 quantise_unit(n)
                 done["quantised"] = n + 1
 
-        def write_next(step):
-            n = done["tiles"]
-            if step >= pairs and n < tiles:
-                write_memory(n)
-                if n % 2 == 1 and n // 2 + 4 < tiles // 2:
-                    load_old(n // 2 + 4)
-                done["tiles"] = n + 1
+        def write_next(sums, rows):
+            for n in range(done["sums"], done["sums"] + sums):
+                write_sums(n)
+            done["sums"] += sums
+            for n in range(done["rows"], done["rows"] + rows):
+                write_rows(n)
+            done["rows"] += rows
 
         with tc.manual_schedule():
             load_keys(0)
@@ -676,39 +659,41 @@ def tile_armtapproach_pa_kernel(
             flip_x2(0, 1)
             products(0, 1)
             square_sums(0, 0)
-            build_band(0)
+            build_band(0, (1, 2))
             square_sums(0, 1)
             inverse_norms(0)
+            compare_signs(1)
+            build_band(0, (3,))
             load_norm(1)
             band_products(0, 0)
             relu_halves(1)
-            compare_signs(1)
             advance_unit()
             products(1, 0)
             products(1, 1)
             signs(1)
             flip_biases()
             relu_halves(2)
-            for step in range(pairs + 4):
+            for step in range(pairs):
                 part = step - 3
-                grp, dh = divmod(part, 2)
-                working = 0 <= part < 2 * groups
-                turning = 0 < part <= 2 * groups
+                grp, h2 = divmod(part, PAIR)
+                working = part >= 0
                 ready, second = divmod(step - 2, 2)
-                fresh = 0 <= ready < groups and second == 0
+                fresh = ready >= 0 and second == 0
+                if step % 2 == 0 and step + 4 < pairs:
+                    load_keys(step // 2 + 2)
                 if working:
-                    v_sums(grp, dh)
-                    head_sums(grp, dh, 0)
-                if step < pairs:
-                    dot_products(step, 0)
-                    band_products(step, 1)
+                    block_sums((grp, h2, 0))
+                if part > 0:
+                    write_values((*divmod(part - 1, PAIR), 1))
+                dot_products(step, 0)
+                band_products(step, 1)
                 if working:
-                    gate_values(grp, dh, 0)
+                    gate_values((grp, h2, 0))
                 if fresh:
                     finish_denominators(ready, 0)
                 if step + 1 < pairs:
                     flip_x2(step + 1, 0)
-                if 0 < step <= pairs:
+                if step > 0:
                     transpose_features(step - 1, 0)
                 if step + 1 < pairs:
                     square_sums(step + 1, 0)
@@ -717,78 +702,109 @@ def tile_armtapproach_pa_kernel(
                     finish_denominators(ready, 1)
                 if step + 2 < pairs:
                     compare_signs(step + 2)
-                if working:
-                    scale_num(grp, dh, 0)
-                write_next(step)
+                if step < NU:
+                    build_band(1, (step + 1,))
                 advance_unit()
-                if 0 < step <= pairs:
+                if step > 0:
                     transpose_features(step - 1, 1)
-                if 0 <= ready < groups:
+                if ready >= 0:
                     if second:
                         quantise_tokens(ready, 1)
                     interleave_tokens(ready, 2 if second else 0, nc.scalar.copy)
-                if step + 2 < pairs:
-                    products(step + 2, 0)
+                if step + 3 < pairs:
+                    relu_halves(step + 3)
                 if fresh:
                     finish_denominators(ready, 2)
                 if working:
-                    write_values(grp, dh, 0)
-                    head_sums(grp, dh, 1)
-                if step + 3 < pairs:
-                    relu_halves(step + 3)
-                write_next(step)
-                if step < pairs:
-                    dot_products(step, 1)
+                    scale_num((grp, h2, 0))
+                if part > 1:
+                    quantise_values(*divmod(part - 2, PAIR))
+                if step + 2 < pairs:
+                    products(step + 2, 0)
+                if working:
+                    write_values((grp, h2, 0))
+                    block_sums((grp, h2, 1))
+                dot_products(step, 1)
                 if step + 1 < pairs:
                     flip_x2(step + 1, 1)
-                if 0 < step <= pairs:
+                if step > 0:
                     transpose_features(step - 1, 2)
                 if step + 1 < pairs:
                     square_sums(step + 1, 1)
                     inverse_norms(step + 1)
                 if working:
-                    gate_values(grp, dh, 1)
+                    gate_values((grp, h2, 1))
                 if step + 2 < pairs:
                     products(step + 2, 1)
                 quantise_next()
-                write_next(step)
                 if step + 1 < pairs:
                     band_products(step + 1, 0)
                 advance_unit()
                 if step < 2:
                     advance_unit()
-                if step < pairs:
-                    round_plane(step, 0)
-                if working:
-                    scale_num(grp, dh, 1)
-                if step < pairs:
-                    round_plane(step, 1)
-                if working:
-                    write_values(grp, dh, 1)
-                if turning:
-                    turn_values(*divmod(part - 1, 2))
+                round_plane(step, 0)
+                round_plane(step, 1)
+                if part > 0:
+                    turn_values(*divmod(part - 1, PAIR))
                 if fresh:
                     for h2 in range(PAIR):
                         spread_denominators(ready, h2)
                     for g in range(F_PASSES):
                         quantise_features(ready, g)
-                if fresh:
                     quantise_tokens(ready, 0)
                     interleave_tokens(ready, 1, nc.scalar.copy)
-                elif 0 <= ready < groups:
+                elif ready >= 0:
                     quantise_tokens(ready, 2)
-                if turning and part % 2 == 0:
-                    quantise_values(part // 2 - 1)
-                if step % 2 == 0 and step + 4 < pairs:
-                    load_keys(step // 2 + 2)
+                if working:
+                    scale_num((*divmod(part, PAIR), 1))
                 if step % 2 == 1 and step + 3 < pairs:
                     signs(step // 2 + 2)
-                if step == 1:
-                    build_band(1)
                 if step < 2:
                     quantise_next()
-                if step == pairs - 1:
-                    for n in range(4):
-                        load_old(n)
-            while done["tiles"] < tiles:
-                write_next(pairs)
+            load_old(0)
+            last = groups - 1
+            blocks = [(grp, h2, dh) for grp, h2 in ((last - 1, 1), (last, 0), (last, 1)) for dh in range(2)]
+            for g in range(F_PASSES):
+                transpose_features(pairs - 1, g)
+            write_values((last - 1, 0, 1))
+            block_sums(blocks[0])
+            for n, block in enumerate(blocks):
+                if n == 0:
+                    for part3 in range(3):
+                        finish_denominators(last, part3)
+                gate_values(block)
+                scale_num(block)
+                if n == 0:
+                    quantise_values(last - 2, 1)
+                    for g in range(F_PASSES):
+                        quantise_features(last, g)
+                if n == 1:
+                    turn_values(last - 1, 0)
+                    for h2 in range(PAIR):
+                        spread_denominators(last, h2)
+                if n == 3:
+                    turn_values(last - 1, 1)
+                    load_old(1)
+                if n == 5:
+                    turn_values(last, 0)
+                if n + 1 < len(blocks):
+                    block_sums(blocks[n + 1])
+                write_values(block)
+                if n > 0:
+                    write_next(2, 2 if n > 1 else 0)
+                if n in (1, 2, 3):
+                    interleave_tokens(last, n - 1, nc.scalar.copy)
+                if n in (2, 3, 4):
+                    quantise_tokens(last, n - 2)
+                if n == 1:
+                    quantise_values(last - 1, 0)
+                if n == 3:
+                    quantise_values(last - 1, 1)
+                if n == 5:
+                    quantise_values(last, 0)
+            turn_values(last, 1)
+            write_next(3, 4)
+            quantise_values(last, 1)
+            for n in range(11):
+                write_next(1, 1)
+            write_next(0, 1)

@@ -136,7 +136,7 @@ def tile_armtapproach_pa_kernel(
                     nc.vector.tensor_tensor(
                         out=band[:, heads], in0=full, in1=full_diagonal, op=ALU.mult
                     )
-                    nc.gpsimd.tensor_tensor(
+                    nc.vector.tensor_tensor(
                         out=band_rest[:, heads], in0=rest, in1=rest_diagonal, op=ALU.mult
                     )
                 else:
@@ -146,10 +146,10 @@ def tile_armtapproach_pa_kernel(
                         out=band[:, heads], in0=band[:, heads], in1=term[:], op=ALU.add
                     )
                     rest_term = feat.tile([P, PAIR, REST], BF16, bufs=1)
-                    nc.gpsimd.tensor_tensor(
+                    nc.vector.tensor_tensor(
                         out=rest_term[:], in0=rest, in1=rest_diagonal, op=ALU.mult
                     )
-                    nc.gpsimd.tensor_tensor(
+                    nc.vector.tensor_tensor(
                         out=band_rest[:, heads], in0=band_rest[:, heads], in1=rest_term[:], op=ALU.add
                     )
 
@@ -438,12 +438,12 @@ def tile_armtapproach_pa_kernel(
 
         def load_unit(n):
             if units[n][0]:
-                raw[n] = stage.tile([P, ROW_UNIT // P, HID], BF16, name="raw")
+                raw[n] = stage.tile([P, ROW_UNIT // P, HID], BF16, name="raw", tag="raw")
                 nc.sync.dma_start(
                     out=raw[n][:], in_=units[n][1].rearrange("(rt p) k -> p rt k", p=P)
                 )
             else:
-                raw[n] = stage.tile([P, PAIR, PACK, D], BF16, name="raw")
+                raw[n] = stage.tile([P, PAIR, PACK, D], BF16, name="raw", tag="raw")
                 for h2 in range(PAIR):
                     nc.sync.dma_start(
                         out=raw[n][:, h2].rearrange("q (u e) d -> q u (e d)", u=2),
@@ -470,7 +470,16 @@ def tile_armtapproach_pa_kernel(
             else:
                 grouped[n] = stage.tile([P, PAIR, D, PACK], BF16, align_bytes=64, name="grouped")
                 for h2 in range(PAIR):
-                    interleave(nc.scalar.copy, grouped[n][:, h2], raw[n][:, h2])
+                    woven = banks.tile([P, D, PACK], BF16, tag="flipped")
+                    for u in range(2):
+                        nc.tensor.matmul(
+                            out=woven[:, :, 2 * u : 2 * u + 2].rearrange("q d e -> q e d"),
+                            lhsT=ident_bf[:],
+                            rhs=raw[n][:, h2, 2 * u : 2 * u + 2, :],
+                            start=True,
+                            stop=True,
+                        )
+                    nc.scalar.copy(out=grouped[n][:, h2], in_=woven[:])
 
         def quantise_unit(n):
             if units[n][0]:
@@ -581,12 +590,16 @@ def tile_armtapproach_pa_kernel(
             return tensor[h, r * 2 * P : (r + 1) * 2 * P, :].rearrange("(t f) d -> f t d", f=P)
 
         def load_old(c):
-            old[c] = feat.tile([P, PAIR, F // P, D], BF16, name="old", tag="mk_planes")
-            for h2 in range(PAIR):
-                nc.sync.dma_start(
-                    out=old[c][:, h2],
-                    in_=memory[PAIR * c + h2].rearrange("(r f) d -> f r d", f=P),
-                )
+            if c == 0:
+                for h2 in range(PAIR):
+                    head_rows = stage.tile([P, F // P, D], BF16, tag="raw")
+                    old[h2] = head_rows[:]
+            else:
+                last_pair = feat.tile([P, PAIR, F // P, D], BF16, tag="mk_planes")
+                for h2 in range(PAIR):
+                    old[PAIR * c + h2] = last_pair[:, h2]
+            for h in range(PAIR * c, PAIR * (c + 1)):
+                nc.sync.dma_start(out=old[h], in_=memory[h].rearrange("(r f) d -> f r d", f=P))
 
         def write_sums(n):
             h, r = divmod(n, F // (2 * P))
@@ -610,12 +623,10 @@ def tile_armtapproach_pa_kernel(
 
         def write_rows(n):
             h, r = divmod(n, F // (2 * P))
-            c, h2 = divmod(h, PAIR)
             if n % NU == 0:
                 new[n // NU] = feat.tile([P, NU, 2, D], F32, bufs=3, name="new", tag="half_phi")
             new_tile = new[n // NU][:, n % NU]
-            old_tile = old[c][:, h2, 2 * r : 2 * r + 2, :]
-            nc.vector.tensor_tensor(out=new_tile, in0=delta[n][:], in1=old_tile, op=ALU.add)
+            nc.vector.tensor_tensor(out=new_tile, in0=delta[n][:], in1=old[h][:, 2 * r : 2 * r + 2, :], op=ALU.add)
             nc.sync.dma_start(out=rows_of(out, n), in_=new_tile)
 
         pairs = 2 * HKV * S_PASSES
@@ -659,19 +670,21 @@ def tile_armtapproach_pa_kernel(
             flip_x2(0, 1)
             products(0, 1)
             square_sums(0, 0)
+            advance_unit()
             build_band(0, (1, 2))
             square_sums(0, 1)
             inverse_norms(0)
+            advance_unit()
             compare_signs(1)
             build_band(0, (3,))
             load_norm(1)
+            flip_biases()
             band_products(0, 0)
+            quantise_next()
             relu_halves(1)
-            advance_unit()
             products(1, 0)
             products(1, 1)
             signs(1)
-            flip_biases()
             relu_halves(2)
             for step in range(pairs):
                 part = step - 3
@@ -681,20 +694,18 @@ def tile_armtapproach_pa_kernel(
                 fresh = ready >= 0 and second == 0
                 if step % 2 == 0 and step + 4 < pairs:
                     load_keys(step // 2 + 2)
-                if working:
-                    block_sums((grp, h2, 0))
                 if part > 0:
                     write_values((*divmod(part - 1, PAIR), 1))
                 dot_products(step, 0)
-                band_products(step, 1)
-                if working:
-                    gate_values((grp, h2, 0))
                 if fresh:
                     finish_denominators(ready, 0)
                 if step + 1 < pairs:
                     flip_x2(step + 1, 0)
                 if step > 0:
                     transpose_features(step - 1, 0)
+                if working:
+                    block_sums((grp, h2, 0))
+                    gate_values((grp, h2, 0))
                 if step + 1 < pairs:
                     square_sums(step + 1, 0)
                 quantise_next()
@@ -702,14 +713,17 @@ def tile_armtapproach_pa_kernel(
                     finish_denominators(ready, 1)
                 if step + 2 < pairs:
                     compare_signs(step + 2)
+                if step == pairs - 1:
+                    load_old(0)
+                band_products(step, 1)
                 if step < NU:
                     build_band(1, (step + 1,))
                 advance_unit()
                 if step > 0:
                     transpose_features(step - 1, 1)
                 if ready >= 0:
-                    if second:
-                        quantise_tokens(ready, 1)
+                    if not second and ready > 0:
+                        quantise_tokens(ready - 1, 2)
                     interleave_tokens(ready, 2 if second else 0, nc.scalar.copy)
                 if step + 3 < pairs:
                     relu_halves(step + 3)
@@ -740,58 +754,58 @@ def tile_armtapproach_pa_kernel(
                 if step + 1 < pairs:
                     band_products(step + 1, 0)
                 advance_unit()
-                if step < 2:
+                if step < 3:
                     advance_unit()
                 round_plane(step, 0)
+                if working:
+                    scale_num((grp, h2, 1))
                 round_plane(step, 1)
                 if part > 0:
                     turn_values(*divmod(part - 1, PAIR))
                 if fresh:
-                    for h2 in range(PAIR):
-                        spread_denominators(ready, h2)
+                    for h in range(PAIR):
+                        spread_denominators(ready, h)
                     for g in range(F_PASSES):
                         quantise_features(ready, g)
                     quantise_tokens(ready, 0)
                     interleave_tokens(ready, 1, nc.scalar.copy)
                 elif ready >= 0:
-                    quantise_tokens(ready, 2)
-                if working:
-                    scale_num((*divmod(part, PAIR), 1))
+                    quantise_tokens(ready, 1)
                 if step % 2 == 1 and step + 3 < pairs:
                     signs(step // 2 + 2)
-                if step < 2:
+                if step < 4:
                     quantise_next()
-            load_old(0)
+            load_old(1)
             last = groups - 1
             blocks = [(grp, h2, dh) for grp, h2 in ((last - 1, 1), (last, 0), (last, 1)) for dh in range(2)]
+            block_sums(blocks[0])
             for g in range(F_PASSES):
                 transpose_features(pairs - 1, g)
+            finish_denominators(last, 0)
+            quantise_values(last - 2, 1)
+            finish_denominators(last, 1)
             write_values((last - 1, 0, 1))
-            block_sums(blocks[0])
+            gate_values(blocks[0])
             for n, block in enumerate(blocks):
-                if n == 0:
-                    for part3 in range(3):
-                        finish_denominators(last, part3)
-                gate_values(block)
                 scale_num(block)
                 if n == 0:
-                    quantise_values(last - 2, 1)
+                    finish_denominators(last, 2)
                     for g in range(F_PASSES):
                         quantise_features(last, g)
+                    quantise_tokens(last - 1, 2)
                 if n == 1:
                     turn_values(last - 1, 0)
                     for h2 in range(PAIR):
                         spread_denominators(last, h2)
                 if n == 3:
                     turn_values(last - 1, 1)
-                    load_old(1)
                 if n == 5:
                     turn_values(last, 0)
                 if n + 1 < len(blocks):
                     block_sums(blocks[n + 1])
+                    gate_values(blocks[n + 1])
                 write_values(block)
-                if n > 0:
-                    write_next(2, 2 if n > 1 else 0)
+                write_next(2, 2 if n > 0 else 0)
                 if n in (1, 2, 3):
                     interleave_tokens(last, n - 1, nc.scalar.copy)
                 if n in (2, 3, 4):
@@ -805,6 +819,6 @@ def tile_armtapproach_pa_kernel(
             turn_values(last, 1)
             write_next(3, 4)
             quantise_values(last, 1)
-            for n in range(11):
+            for n in range(9):
                 write_next(1, 1)
             write_next(0, 1)

@@ -94,8 +94,8 @@ def tile_armtapproach_pa_kernel(
 
         hs_codes = keep.tile([P, HID_PASSES, S], U32, align_bytes=64)
         hs_scales = keep.tile([P, HID_PASSES, S], U8, align_bytes=64)
-        w_codes = keep.tile([P, HID_PASSES, W_ROWS], U32, align_bytes=64)
-        w_scales = keep.tile([P, HID_PASSES, W_ROWS], U8, align_bytes=64)
+        w_codes = keep.tile([P, W_ROWS // ROW_UNIT, HID_PASSES, ROW_UNIT], U32, align_bytes=64)
+        w_scales = keep.tile([P, W_ROWS // ROW_UNIT, HID_PASSES, ROW_UNIT], U8, align_bytes=64)
         mem_codes = keep.tile([P, HKV, F_PASSES, PAIR * D], U32, align_bytes=64)
         mem_scales = keep.tile([P, HKV, F_PASSES, PAIR * D], U8, align_bytes=64)
         mkS_codes = keep.tile([P, HKV, S_PASSES, F], U32, align_bytes=64)
@@ -105,53 +105,36 @@ def tile_armtapproach_pa_kernel(
 
         band = keep.tile([P, H, FULL_TILES, REACH], BF16)
         band_rest = keep.tile([P, H, REST], BF16)
-        norm_w = {}
+        norm_w = feat.tile([P, H, NU, X2], BF16, tag="mk_planes")
 
-        def load_norm(c):
-            norm_w[c] = late.tile([P, PAIR, NU, X2], BF16, bufs=1, name="norm_w", tag="neg_inv_denom")
+        def load_norm():
             nc.sync.dma_start(
-                out=norm_w[c][:].rearrange("p h j i -> p (h j) i"),
-                in_=norm[PAIR * c : PAIR * (c + 1), :]
-                .rearrange("h (j i) -> (h j) i", j=NU)
-                .partition_broadcast(P),
+                out=norm_w[:].rearrange("p h j i -> p (h j) i"),
+                in_=norm.rearrange("h (j i) -> (h j) i", j=NU).partition_broadcast(P),
             )
 
-        def build_band(c, rolls):
-            heads = slice(PAIR * c, PAIR * (c + 1))
-            for j in rolls:
-                full = norm_w[c][:, :, j - 1, 0 : X2 - REST].rearrange(
-                    "p h (m n) -> p h m n", n=REACH
+        def build_band(j):
+            full = norm_w[:, :, j - 1, 0 : X2 - REST].rearrange("p h (m n) -> p h m n", n=REACH)
+            full_diagonal = (
+                ident_bf[:, NU - j : NU - j + REACH]
+                .unsqueeze(1)
+                .unsqueeze(1)
+                .to_broadcast([P, H, FULL_TILES, REACH])
+            )
+            rest = norm_w[:, :, j - 1, X2 - REST : X2]
+            rest_diagonal = ident_bf[:, P - REST - j : P - j].unsqueeze(1).to_broadcast([P, H, REST])
+            if j == 1:
+                nc.vector.tensor_tensor(out=band[:], in0=full, in1=full_diagonal, op=ALU.mult)
+                nc.vector.tensor_tensor(out=band_rest[:], in0=rest, in1=rest_diagonal, op=ALU.mult)
+            else:
+                term = feat.tile([P, H, FULL_TILES, REACH], BF16, bufs=1, tag="mkT_grouped", align_bytes=64)
+                rest_term = feat.tile([P, H, REST], BF16, bufs=1)
+                nc.vector.tensor_tensor(out=term[:], in0=full, in1=full_diagonal, op=ALU.mult)
+                nc.vector.tensor_tensor(out=rest_term[:], in0=rest, in1=rest_diagonal, op=ALU.mult)
+                nc.vector.tensor_tensor(out=band[:], in0=band[:], in1=term[:], op=ALU.add)
+                nc.vector.tensor_tensor(
+                    out=band_rest[:], in0=band_rest[:], in1=rest_term[:], op=ALU.add
                 )
-                full_diagonal = (
-                    ident_bf[:, NU - j : NU - j + REACH]
-                    .unsqueeze(1)
-                    .unsqueeze(1)
-                    .to_broadcast([P, PAIR, FULL_TILES, REACH])
-                )
-                rest = norm_w[c][:, :, j - 1, X2 - REST : X2]
-                rest_diagonal = (
-                    ident_bf[:, P - REST - j : P - j].unsqueeze(1).to_broadcast([P, PAIR, REST])
-                )
-                if j == 1:
-                    nc.vector.tensor_tensor(
-                        out=band[:, heads], in0=full, in1=full_diagonal, op=ALU.mult
-                    )
-                    nc.vector.tensor_tensor(
-                        out=band_rest[:, heads], in0=rest, in1=rest_diagonal, op=ALU.mult
-                    )
-                else:
-                    term = feat.tile([P, PAIR, FULL_TILES, REACH], BF16, tag="weighted")
-                    nc.vector.tensor_tensor(out=term[:], in0=full, in1=full_diagonal, op=ALU.mult)
-                    nc.vector.tensor_tensor(
-                        out=band[:, heads], in0=band[:, heads], in1=term[:], op=ALU.add
-                    )
-                    rest_term = feat.tile([P, PAIR, REST], BF16, bufs=1)
-                    nc.vector.tensor_tensor(
-                        out=rest_term[:], in0=rest, in1=rest_diagonal, op=ALU.mult
-                    )
-                    nc.vector.tensor_tensor(
-                        out=band_rest[:, heads], in0=band_rest[:, heads], in1=rest_term[:], op=ALU.add
-                    )
 
         bias_rows = keep.tile([P, P], BF16)
 
@@ -184,17 +167,13 @@ def tile_armtapproach_pa_kernel(
                     ),
                 )
 
-        def keys_of(pair):
-            grp, u = divmod(pair, 2)
-            return k_rows[grp][:, 2 * u : 2 * u + 2, :]
-
-        def relu_halves(pair):
-            x = keys_of(pair)[:, :, KEY_FRONT:]
-            x2[pair] = feat.tile([P, 2, NU + X2], BF16, bufs=4, name="x2", tag="x2")
-            nc.vector.tensor_scalar_max(out=x2[pair][:, :, NU : NU + D], in0=x, scalar1=0.0)
+        def relu_halves(grp):
+            x = k_rows[grp][:, :, KEY_FRONT:]
+            x2[grp] = feat.tile([P, PACK, NU + X2], BF16, name="x2")
+            nc.vector.tensor_scalar_max(out=x2[grp][:, :, NU : NU + D], in0=x, scalar1=0.0)
             for start, values in ((NU + D, x), (0, x[:, :, D - NU : D])):
                 nc.vector.tensor_scalar(
-                    out=x2[pair][:, :, start : start + values.shape[2]],
+                    out=x2[grp][:, :, start : start + values.shape[2]],
                     in0=values,
                     scalar1=-1.0,
                     scalar2=0.0,
@@ -217,27 +196,27 @@ def tile_armtapproach_pa_kernel(
                 op1=ALU.add,
             )
 
-        def compare_signs(pair):
-            grp, u = divmod(pair, 2)
-            same_sign[pair] = feat.tile([P, 2, NU, D], BF16, name="same_sign")
+        def compare_signs(grp):
+            same_sign[grp] = feat.tile([P, PACK, NU, D], BF16, bufs=1, name="same_sign")
             for j in range(1, NU + 1):
                 nc.vector.tensor_tensor(
-                    out=same_sign[pair][:, :, j - 1, :],
-                    in0=keys_of(pair)[:, :, KEY_FRONT - j : KEY_FRONT - j + D],
-                    in1=half_signs[grp][:, 2 * u : 2 * u + 2, :],
+                    out=same_sign[grp][:, :, j - 1, :],
+                    in0=k_rows[grp][:, :, KEY_FRONT - j : KEY_FRONT - j + D],
+                    in1=half_signs[grp][:],
                     op=ALU.mult,
                 )
 
         def products(pair, b):
+            grp, u = divmod(pair, 2)
             if b == 0:
                 half_phi[pair] = feat.tile(
                     [P, 2, NU, D], F32, bufs=3, name="half_phi", tag="half_phi"
                 )
             nc.vector.scalar_tensor_tensor(
                 out=half_phi[pair][:, b],
-                in0=same_sign[pair][:, b],
+                in0=same_sign[grp][:, 2 * u + b],
                 scalar=0.0,
-                in1=keys_of(pair)[:, b, KEY_FRONT:].unsqueeze(1).to_broadcast([P, NU, D]),
+                in1=k_rows[grp][:, 2 * u + b, KEY_FRONT:].unsqueeze(1).to_broadcast([P, NU, D]),
                 op0=ALU.max,
                 op1=ALU.mult,
             )
@@ -272,12 +251,15 @@ def tile_armtapproach_pa_kernel(
             )
 
         def flip_x2(pair, b):
+            grp, u = divmod(pair, 2)
             if b == 0:
                 x2T[pair] = feat.tile([P, 2, X2_TILES, P], BF16, name="x2T")
             x2T_bank = banks.tile([P, X2_TILES, P], BF16, tag="flipped")
             for m in range(X2_TILES):
                 start = m * REACH if m < FULL_TILES else NU + X2 - P
-                nc.tensor.transpose(x2T_bank[:, m, :], x2[pair][:, b, start : start + P], ident_bf[:])
+                nc.tensor.transpose(
+                    x2T_bank[:, m, :], x2[grp][:, 2 * u + b, start : start + P], ident_bf[:]
+                )
             nc.scalar.copy(out=x2T[pair][:, b], in_=x2T_bank[:])
 
         def band_products(pair, b):
@@ -310,7 +292,7 @@ def tile_armtapproach_pa_kernel(
                     out=weighted[:],
                     in0=inner_sums[(pair, b, h2)][:],
                     scalar=1.0,
-                    in1=x2[pair][:, b, NU : NU + X2],
+                    in1=x2[grp][:, 2 * u + b, NU : NU + X2],
                     op0=ALU.mult,
                     op1=ALU.mult,
                     accum_out=dots[grp][:, 2 * u + b, h2 : h2 + 1],
@@ -349,9 +331,7 @@ def tile_armtapproach_pa_kernel(
 
         def spread_denominators(grp, h2):
             if h2 == 0:
-                neg_inv_denom[grp] = late.tile(
-                    [P, PAIR, K_PASS], F32, bufs=1, name="neg_inv_denom", tag="neg_inv_denom"
-                )
+                neg_inv_denom[grp] = late.tile([P, PAIR, K_PASS], F32, bufs=1, name="neg_inv_denom")
             spread = banks.tile([P, 2, 2, P], F32, tag="flipped")
             for u in range(2):
                 for e in range(2):
@@ -367,11 +347,16 @@ def tile_armtapproach_pa_kernel(
 
         def transpose_features(pair, g):
             grp, a = divmod(pair, 2)
-            if a == 0:
-                mkT_grouped[(grp, g)] = feat.tile(
-                    [P, K_PASS, PACK], BF16, bufs=F_PASSES, align_bytes=64, name="mkT_grouped"
+            if a == 0 and g == 0:
+                mkT_grouped[grp] = feat.tile(
+                    [P, F_PASSES, K_PASS, PACK],
+                    BF16,
+                    bufs=1,
+                    align_bytes=64,
+                    name="mkT_grouped",
+                    tag="mkT_grouped",
                 )
-            mkT_words = mkT_grouped[(grp, g)][:].bitcast(F32)
+            mkT_words = mkT_grouped[grp][:, g].bitcast(F32)
             flipped = banks.tile([P, 2, 2, P], F32, tag="flipped")
             for b in range(2):
                 plane_words = mk_planes[grp][:, 2 * a + b, :].bitcast(F32)
@@ -383,15 +368,20 @@ def tile_armtapproach_pa_kernel(
                 in_=flipped[:].rearrange("q b u r -> q r b u"),
             )
 
-        def quantise_features(grp, g):
-            if g == 0:
+        def quantise_features(grp, passes):
+            if grp not in mkT_codes:
                 mkT_codes[grp] = late.tile(
                     [P, F_PASSES, K_PASS], U32, align_bytes=64, name="mkT_codes"
                 )
                 mkT_scales[grp] = late.tile(
                     [P, F_PASSES, K_PASS], U8, align_bytes=64, name="mkT_scales"
                 )
-            quantise(nc, mkT_grouped[(grp, g)][:], mkT_codes[grp][:, g, :], mkT_scales[grp][:, g, :])
+            quantise(
+                nc,
+                mkT_grouped[grp][:, passes].rearrange("p g c t -> p (g c) t"),
+                mkT_codes[grp][:, passes].rearrange("p g c -> p (g c)"),
+                mkT_scales[grp][:, passes].rearrange("p g c -> p (g c)"),
+            )
 
         mkS_grouped = {}
 
@@ -410,18 +400,19 @@ def tile_armtapproach_pa_kernel(
                 nc, mkS_grouped[(grp, g)][:], mkS_codes[:, c, sg, f_cols], mkS_scales[:, c, sg, f_cols]
             )
 
-        def row_unit(source, r0, codes, scales, o0):
-            o_cols = slice(o0, o0 + ROW_UNIT)
-            return (True, source[r0 : r0 + ROW_UNIT, :], codes[:, :, o_cols], scales[:, :, o_cols])
-
         def hs_unit(n):
-            return row_unit(hidden_states, n * ROW_UNIT, hs_codes, hs_scales, n * ROW_UNIT)
+            r_cols = slice(n * ROW_UNIT, (n + 1) * ROW_UNIT)
+            return (True, hidden_states[r_cols, :], hs_codes[:, :, r_cols], hs_scales[:, :, r_cols])
+
+        def w_unit(source, n, unit):
+            r_rows = slice(n * ROW_UNIT, (n + 1) * ROW_UNIT)
+            return (True, source[r_rows, :], w_codes[:, unit], w_scales[:, unit])
 
         def wv_unit(c):
-            return row_unit(Wv, c * D, w_codes, w_scales, c * D)
+            return w_unit(Wv, c, c)
 
         def wmb_unit(h):
-            return row_unit(Wmb, h * D, w_codes, w_scales, HKV * D + h * D)
+            return w_unit(Wmb, h, HKV + h)
 
         def mem_unit(c, g):
             return (
@@ -482,25 +473,34 @@ def tile_armtapproach_pa_kernel(
                     nc.scalar.copy(out=grouped[n][:, h2], in_=woven[:])
 
         def quantise_unit(n):
-            if units[n][0]:
+            rows, source, codes, scales = units[n]
+            if not rows:
+                quantise(nc, grouped[n][:].rearrange("q h d t -> q (h d) t"), codes, scales)
+            elif source.shape[1] == HID and n in (0, 2, 8, 9):
                 for g in range(HID_PASSES):
-                    quantise(nc, grouped[n][:, g], units[n][2][:, g, :], units[n][3][:, g, :])
+                    quantise(nc, grouped[n][:, g], codes[:, g, :], scales[:, g, :])
             else:
-                quantise(nc, grouped[n][:].rearrange("q h d t -> q (h d) t"), units[n][2], units[n][3])
+                quantise(
+                    nc,
+                    grouped[n][:].rearrange("q g r t -> q (g r) t"),
+                    codes.rearrange("q g r -> q (g r)"),
+                    scales.rearrange("q g r -> q (g r)"),
+                )
 
         v_bank, mb_bank, num_bank, gate, diff = {}, {}, {}, {}, {}
         wmv_grouped, wmvT = {}, {}
 
         def project(bank, grp, m):
             sg = grp % S_PASSES
-            o_cols = slice(m * P, (m + 1) * P)
+            unit, part = divmod(m, ROW_UNIT // P)
+            o_cols = slice(part * P, (part + 1) * P)
             s_cols = slice(sg * K_PASS, (sg + 1) * K_PASS)
             mx_group(
                 nc,
                 bank,
                 HID_PASSES,
-                lambda g: w_codes[:, g, o_cols],
-                lambda g: w_scales[:, g, o_cols],
+                lambda g: w_codes[:, unit, g, o_cols],
+                lambda g: w_scales[:, unit, g, o_cols],
                 lambda g: hs_codes[:, g, s_cols],
                 lambda g: hs_scales[:, g, s_cols],
             )
@@ -657,10 +657,10 @@ def tile_armtapproach_pa_kernel(
 
         with tc.manual_schedule():
             load_keys(0)
-            load_norm(0)
-            load_keys(1)
+            load_norm()
             load_unit(0)
             load_unit(1)
+            load_keys(1)
             load_biases()
             signs(0)
             relu_halves(0)
@@ -668,24 +668,21 @@ def tile_armtapproach_pa_kernel(
             flip_x2(0, 0)
             products(0, 0)
             flip_x2(0, 1)
+            build_band(1)
             products(0, 1)
             square_sums(0, 0)
             advance_unit()
-            build_band(0, (1, 2))
+            build_band(2)
             square_sums(0, 1)
             inverse_norms(0)
             advance_unit()
-            compare_signs(1)
-            build_band(0, (3,))
-            load_norm(1)
+            build_band(3)
             flip_biases()
             band_products(0, 0)
             quantise_next()
-            relu_halves(1)
             products(1, 0)
             products(1, 1)
             signs(1)
-            relu_halves(2)
             for step in range(pairs):
                 part = step - 3
                 grp, h2 = divmod(part, PAIR)
@@ -711,13 +708,11 @@ def tile_armtapproach_pa_kernel(
                 quantise_next()
                 if fresh:
                     finish_denominators(ready, 1)
-                if step + 2 < pairs:
-                    compare_signs(step + 2)
+                if step % 2 == 0 and step + 2 < pairs:
+                    compare_signs(step // 2 + 1)
                 if step == pairs - 1:
                     load_old(0)
                 band_products(step, 1)
-                if step < NU:
-                    build_band(1, (step + 1,))
                 advance_unit()
                 if step > 0:
                     transpose_features(step - 1, 1)
@@ -725,8 +720,8 @@ def tile_armtapproach_pa_kernel(
                     if not second and ready > 0:
                         quantise_tokens(ready - 1, 2)
                     interleave_tokens(ready, 2 if second else 0, nc.scalar.copy)
-                if step + 3 < pairs:
-                    relu_halves(step + 3)
+                if step % 2 == 0 and step + 2 < pairs:
+                    relu_halves(step // 2 + 1)
                 if fresh:
                     finish_denominators(ready, 2)
                 if working:
@@ -765,8 +760,8 @@ def tile_armtapproach_pa_kernel(
                 if fresh:
                     for h in range(PAIR):
                         spread_denominators(ready, h)
-                    for g in range(F_PASSES):
-                        quantise_features(ready, g)
+                    for passes in (slice(0, 2), slice(2, 3)):
+                        quantise_features(ready, passes)
                     quantise_tokens(ready, 0)
                     interleave_tokens(ready, 1, nc.scalar.copy)
                 elif ready >= 0:
@@ -790,8 +785,8 @@ def tile_armtapproach_pa_kernel(
                 scale_num(block)
                 if n == 0:
                     finish_denominators(last, 2)
-                    for g in range(F_PASSES):
-                        quantise_features(last, g)
+                    for passes in (slice(0, 2), slice(2, 3)):
+                        quantise_features(last, passes)
                     quantise_tokens(last - 1, 2)
                 if n == 1:
                     turn_values(last - 1, 0)

@@ -107,33 +107,42 @@ def tile_armtapproach_pa_kernel(
         band_rest = keep.tile([P, H, REST], BF16)
         norm_w = feat.tile([P, H, NU, X2], BF16, tag="mk_planes")
 
-        def load_norm():
+        def load_norm(c):
+            heads = slice(PAIR * c, PAIR * (c + 1))
             nc.sync.dma_start(
-                out=norm_w[:].rearrange("p h j i -> p (h j) i"),
-                in_=norm.rearrange("h (j i) -> (h j) i", j=NU).partition_broadcast(P),
+                out=norm_w[:, heads].rearrange("p h j i -> p (h j) i"),
+                in_=norm[heads, :].rearrange("h (j i) -> (h j) i", j=NU).partition_broadcast(P),
             )
 
-        def build_band(j):
-            full = norm_w[:, :, j - 1, 0 : X2 - REST].rearrange("p h (m n) -> p h m n", n=REACH)
+        def build_band(c, j):
+            heads = slice(PAIR * c, PAIR * (c + 1))
+            full = norm_w[:, heads, j - 1, 0 : X2 - REST].rearrange("p h (m n) -> p h m n", n=REACH)
             full_diagonal = (
                 ident_bf[:, NU - j : NU - j + REACH]
                 .unsqueeze(1)
                 .unsqueeze(1)
-                .to_broadcast([P, H, FULL_TILES, REACH])
+                .to_broadcast([P, PAIR, FULL_TILES, REACH])
             )
-            rest = norm_w[:, :, j - 1, X2 - REST : X2]
-            rest_diagonal = ident_bf[:, P - REST - j : P - j].unsqueeze(1).to_broadcast([P, H, REST])
             if j == 1:
-                nc.vector.tensor_tensor(out=band[:], in0=full, in1=full_diagonal, op=ALU.mult)
-                nc.vector.tensor_tensor(out=band_rest[:], in0=rest, in1=rest_diagonal, op=ALU.mult)
+                nc.vector.tensor_tensor(out=band[:, heads], in0=full, in1=full_diagonal, op=ALU.mult)
             else:
-                term = feat.tile([P, H, FULL_TILES, REACH], BF16, bufs=1, tag="mkT_grouped", align_bytes=64)
-                rest_term = feat.tile([P, H, REST], BF16, bufs=1)
+                term = feat.tile([P, PAIR, FULL_TILES, REACH], BF16, bufs=1)
                 nc.vector.tensor_tensor(out=term[:], in0=full, in1=full_diagonal, op=ALU.mult)
-                nc.vector.tensor_tensor(out=rest_term[:], in0=rest, in1=rest_diagonal, op=ALU.mult)
-                nc.vector.tensor_tensor(out=band[:], in0=band[:], in1=term[:], op=ALU.add)
+                nc.vector.tensor_tensor(out=band[:, heads], in0=band[:, heads], in1=term[:], op=ALU.add)
+
+        def build_rest(c, j):
+            heads = slice(PAIR * c, PAIR * (c + 1))
+            rest = norm_w[:, heads, j - 1, X2 - REST : X2]
+            rest_diagonal = ident_bf[:, P - REST - j : P - j].unsqueeze(1).to_broadcast([P, PAIR, REST])
+            if j == 1:
                 nc.vector.tensor_tensor(
-                    out=band_rest[:], in0=band_rest[:], in1=rest_term[:], op=ALU.add
+                    out=band_rest[:, heads], in0=rest, in1=rest_diagonal, op=ALU.mult
+                )
+            else:
+                rest_term = feat.tile([P, PAIR, REST], BF16, bufs=1)
+                nc.vector.tensor_tensor(out=rest_term[:], in0=rest, in1=rest_diagonal, op=ALU.mult)
+                nc.vector.tensor_tensor(
+                    out=band_rest[:, heads], in0=band_rest[:, heads], in1=rest_term[:], op=ALU.add
                 )
 
         bias_rows = keep.tile([P, P], BF16)
@@ -505,10 +514,10 @@ def tile_armtapproach_pa_kernel(
                 lambda g: hs_scales[:, g, s_cols],
             )
 
-        def block_sums(block):
+        def num_sums(block):
             grp, h2, dh = block
             c = grp // S_PASSES
-            num_bank[block] = banks.tile([P, K_PASS], F32, bufs=1, name="num_bank")
+            num_bank[block] = banks.tile([P, K_PASS], F32, bufs=1, name="num_bank", tag="num_bank")
             d_cols = slice(h2 * D + dh * P, h2 * D + (dh + 1) * P)
             mx_group(
                 nc,
@@ -519,10 +528,18 @@ def tile_armtapproach_pa_kernel(
                 lambda g: mkT_codes[grp][:, g, :],
                 lambda g: mkT_scales[grp][:, g, :],
             )
-            mb_bank[block] = banks.tile([P, K_PASS], F32, bufs=1, name="mb_bank")
-            project(mb_bank[block][:], grp, V_TILES + (PAIR * c + h2) * (D // P) + dh)
-            v_bank[block] = banks.tile([P, K_PASS], F32, bufs=1, name="v_bank")
-            project(v_bank[block][:], grp, c * (D // P) + dh)
+
+        def mb_sums(block):
+            grp, h2, dh = block
+            mb_bank[block] = banks.tile([P, K_PASS], F32, bufs=1, name="mb_bank", tag="mb_bank")
+            project(
+                mb_bank[block][:], grp, V_TILES + (PAIR * (grp // S_PASSES) + h2) * (D // P) + dh
+            )
+
+        def v_sums(block):
+            grp, h2, dh = block
+            v_bank[block] = banks.tile([P, K_PASS], F32, bufs=1, name="v_bank", tag="v_bank")
+            project(v_bank[block][:], grp, grp // S_PASSES * (D // P) + dh)
 
         def gate_values(block):
             grp, h2, dh = block
@@ -647,6 +664,11 @@ def tile_armtapproach_pa_kernel(
                 quantise_unit(n)
                 done["quantised"] = n + 1
 
+        def block_sums(block):
+            num_sums(block)
+            mb_sums(block)
+            v_sums(block)
+
         def write_next(sums, rows):
             for n in range(done["sums"], done["sums"] + sums):
                 write_sums(n)
@@ -657,10 +679,11 @@ def tile_armtapproach_pa_kernel(
 
         with tc.manual_schedule():
             load_keys(0)
-            load_norm()
+            load_norm(0)
             load_unit(0)
             load_unit(1)
             load_keys(1)
+            load_norm(1)
             load_biases()
             signs(0)
             relu_halves(0)
@@ -668,15 +691,15 @@ def tile_armtapproach_pa_kernel(
             flip_x2(0, 0)
             products(0, 0)
             flip_x2(0, 1)
-            build_band(1)
             products(0, 1)
             square_sums(0, 0)
             advance_unit()
-            build_band(2)
+            for j in range(1, NU + 1):
+                build_band(0, j)
+                build_rest(0, j)
             square_sums(0, 1)
             inverse_norms(0)
             advance_unit()
-            build_band(3)
             flip_biases()
             band_products(0, 0)
             quantise_next()
@@ -698,10 +721,12 @@ def tile_armtapproach_pa_kernel(
                     finish_denominators(ready, 0)
                 if step + 1 < pairs:
                     flip_x2(step + 1, 0)
+                if working:
+                    num_sums((grp, h2, 0))
                 if step > 0:
                     transpose_features(step - 1, 0)
                 if working:
-                    block_sums((grp, h2, 0))
+                    mb_sums((grp, h2, 0))
                     gate_values((grp, h2, 0))
                 if step + 1 < pairs:
                     square_sums(step + 1, 0)
@@ -712,8 +737,13 @@ def tile_armtapproach_pa_kernel(
                     compare_signs(step // 2 + 1)
                 if step == pairs - 1:
                     load_old(0)
+                if step < NU:
+                    build_band(1, step + 1)
+                    build_rest(1, step + 1)
                 band_products(step, 1)
                 advance_unit()
+                if working:
+                    v_sums((grp, h2, 0))
                 if step > 0:
                     transpose_features(step - 1, 1)
                 if ready >= 0:
@@ -732,10 +762,12 @@ def tile_armtapproach_pa_kernel(
                     products(step + 2, 0)
                 if working:
                     write_values((grp, h2, 0))
-                    block_sums((grp, h2, 1))
+                    num_sums((grp, h2, 1))
                 dot_products(step, 1)
                 if step + 1 < pairs:
                     flip_x2(step + 1, 1)
+                if working:
+                    mb_sums((grp, h2, 1))
                 if step > 0:
                     transpose_features(step - 1, 2)
                 if step + 1 < pairs:
@@ -749,6 +781,8 @@ def tile_armtapproach_pa_kernel(
                 if step + 1 < pairs:
                     band_products(step + 1, 0)
                 advance_unit()
+                if working:
+                    v_sums((grp, h2, 1))
                 if step < 3:
                     advance_unit()
                 round_plane(step, 0)

@@ -340,7 +340,13 @@ def tile_armtapproach_pa_kernel(
 
         def spread_denominators(grp, h2):
             if h2 == 0:
-                neg_inv_denom[grp] = late.tile([P, PAIR, K_PASS], F32, bufs=1, name="neg_inv_denom")
+                if grp + 1 < HKV * S_PASSES:
+                    spread_tile = late.tile([P, PAIR, K_PASS], F32, bufs=1)
+                else:
+                    spread_tile = stage.tile(
+                        [P, PAIR, K_PASS], F32, align_bytes=64, name="spread_last", tag="grouped"
+                    )
+                neg_inv_denom[grp] = spread_tile
             spread = banks.tile([P, 2, 2, P], F32, tag="flipped")
             for u in range(2):
                 for e in range(2):
@@ -453,7 +459,11 @@ def tile_armtapproach_pa_kernel(
         def lay_out_unit(n):
             if units[n][0]:
                 grouped[n] = stage.tile(
-                    [P, HID_PASSES, ROW_UNIT, PACK], BF16, align_bytes=64, name="grouped"
+                    [P, HID_PASSES, ROW_UNIT, PACK],
+                    BF16,
+                    align_bytes=64,
+                    name="grouped",
+                    tag="grouped",
                 )
                 grouped_words = grouped[n][:].bitcast(F32)
                 for rt in range(ROW_UNIT // P):
@@ -468,7 +478,7 @@ def tile_armtapproach_pa_kernel(
                         in_=flipped[:].rearrange("q g u r -> q g r u"),
                     )
             else:
-                grouped[n] = stage.tile([P, PAIR, D, PACK], BF16, align_bytes=64, name="grouped")
+                grouped[n] = stage.tile([P, PAIR, D, PACK], BF16, align_bytes=64, name="grouped", tag="grouped")
                 for h2 in range(PAIR):
                     woven = banks.tile([P, D, PACK], BF16, tag="flipped")
                     for u in range(2):
@@ -717,8 +727,6 @@ def tile_armtapproach_pa_kernel(
                 if part > 0:
                     write_values((*divmod(part - 1, PAIR), 1))
                 dot_products(step, 0)
-                if fresh:
-                    finish_denominators(ready, 0)
                 if step + 1 < pairs:
                     flip_x2(step + 1, 0)
                 if working:
@@ -731,8 +739,6 @@ def tile_armtapproach_pa_kernel(
                 if step + 1 < pairs:
                     square_sums(step + 1, 0)
                 quantise_next()
-                if fresh:
-                    finish_denominators(ready, 1)
                 if step % 2 == 0 and step + 2 < pairs:
                     compare_signs(step // 2 + 1)
                 if step == pairs - 1:
@@ -744,16 +750,14 @@ def tile_armtapproach_pa_kernel(
                 advance_unit()
                 if working:
                     v_sums((grp, h2, 0))
-                if step > 0:
-                    transpose_features(step - 1, 1)
                 if ready >= 0:
                     if not second and ready > 0:
                         quantise_tokens(ready - 1, 2)
                     interleave_tokens(ready, 2 if second else 0, nc.scalar.copy)
+                if step > 0:
+                    transpose_features(step - 1, 1)
                 if step % 2 == 0 and step + 2 < pairs:
                     relu_halves(step // 2 + 1)
-                if fresh:
-                    finish_denominators(ready, 2)
                 if working:
                     scale_num((grp, h2, 0))
                 if part > 1:
@@ -785,9 +789,15 @@ def tile_armtapproach_pa_kernel(
                     v_sums((grp, h2, 1))
                 if step < 3:
                     advance_unit()
+                if second:
+                    finish_denominators(step // 2, 0)
                 round_plane(step, 0)
+                if second:
+                    finish_denominators(step // 2, 1)
                 if working:
                     scale_num((grp, h2, 1))
+                if second:
+                    finish_denominators(step // 2, 2)
                 round_plane(step, 1)
                 if part > 0:
                     turn_values(*divmod(part - 1, PAIR))
@@ -798,7 +808,7 @@ def tile_armtapproach_pa_kernel(
                         quantise_features(ready, passes)
                     quantise_tokens(ready, 0)
                     interleave_tokens(ready, 1, nc.scalar.copy)
-                elif ready >= 0:
+                elif ready >= 0 and step + 1 < pairs:
                     quantise_tokens(ready, 1)
                 if step % 2 == 1 and step + 3 < pairs:
                     signs(step // 2 + 2)
@@ -807,25 +817,25 @@ def tile_armtapproach_pa_kernel(
             load_old(1)
             last = groups - 1
             blocks = [(grp, h2, dh) for grp, h2 in ((last - 1, 1), (last, 0), (last, 1)) for dh in range(2)]
-            block_sums(blocks[0])
+            num_sums(blocks[0])
             for g in range(F_PASSES):
                 transpose_features(pairs - 1, g)
-            finish_denominators(last, 0)
-            quantise_values(last - 2, 1)
-            finish_denominators(last, 1)
+            mb_sums(blocks[0])
+            v_sums(blocks[0])
             write_values((last - 1, 0, 1))
+            quantise_values(last - 2, 1)
+            for h2 in range(PAIR):
+                spread_denominators(last, h2)
             gate_values(blocks[0])
             for n, block in enumerate(blocks):
                 scale_num(block)
                 if n == 0:
-                    finish_denominators(last, 2)
+                    quantise_tokens(last - 1, 1)
+                    quantise_tokens(last - 1, 2)
                     for passes in (slice(0, 2), slice(2, 3)):
                         quantise_features(last, passes)
-                    quantise_tokens(last - 1, 2)
                 if n == 1:
                     turn_values(last - 1, 0)
-                    for h2 in range(PAIR):
-                        spread_denominators(last, h2)
                 if n == 3:
                     turn_values(last - 1, 1)
                 if n == 5:
@@ -835,10 +845,10 @@ def tile_armtapproach_pa_kernel(
                     gate_values(blocks[n + 1])
                 write_values(block)
                 write_next(2, 2 if n > 0 else 0)
-                if n in (1, 2, 3):
-                    interleave_tokens(last, n - 1, nc.scalar.copy)
-                if n in (2, 3, 4):
-                    quantise_tokens(last, n - 2)
+                if n < F_PASSES:
+                    interleave_tokens(last, n, nc.scalar.copy)
+                if 0 < n <= F_PASSES:
+                    quantise_tokens(last, n - 1)
                 if n == 1:
                     quantise_values(last - 1, 0)
                 if n == 3:

@@ -753,7 +753,11 @@ def tile_armtapproach_pa_kernel(
                 if ready >= 0:
                     if not second and ready > 0:
                         quantise_tokens(ready - 1, 2)
-                    interleave_tokens(ready, 2 if second else 0, nc.scalar.copy)
+                    interleave_tokens(
+                        ready,
+                        2 if second else 0,
+                        nc.vector.tensor_copy if second and ready == 0 else nc.scalar.copy,
+                    )
                 if step > 0:
                     transpose_features(step - 1, 1)
                 if step % 2 == 0 and step + 2 < pairs:

@@ -69,8 +69,8 @@ def mx_group(nc, bank, passes, lhs_codes, lhs_scales, rhs_codes, rhs_scales):
 
 def interleave(engine_copy, grouped, planes):
     engine_copy(
-        out=grouped.rearrange("p (n i) t -> p n t i", i=4),
-        in_=planes.rearrange("p t (n i) -> p n t i", i=4),
+        out=grouped.rearrange("p (n i) t -> p n t i", i=8),
+        in_=planes.rearrange("p t (n i) -> p n t i", i=8),
     )
 
 

@@ -179,16 +179,26 @@ def tile_armtapproach_pa_kernel(
         def relu_halves(grp):
             x = k_rows[grp][:, :, KEY_FRONT:]
             x2[grp] = feat.tile([P, PACK, NU + X2], BF16, name="x2")
-            nc.vector.tensor_scalar_max(out=x2[grp][:, :, NU : NU + D], in0=x, scalar1=0.0)
-            for start, values in ((NU + D, x), (0, x[:, :, D - NU : D])):
-                nc.vector.tensor_scalar(
-                    out=x2[grp][:, :, start : start + values.shape[2]],
-                    in0=values,
-                    scalar1=-1.0,
-                    scalar2=0.0,
-                    op0=ALU.mult,
-                    op1=ALU.max,
-                )
+            if grp < 2:
+                nc.scalar.activation(out=x2[grp][:, :, NU : NU + D], in_=x, func=ACT.Relu)
+                for start, values in ((NU + D, x), (0, x[:, :, D - NU : D])):
+                    nc.scalar.activation(
+                        out=x2[grp][:, :, start : start + values.shape[2]],
+                        in_=values,
+                        func=ACT.Relu,
+                        scale=-1.0,
+                    )
+            else:
+                nc.vector.tensor_scalar_max(out=x2[grp][:, :, NU : NU + D], in0=x, scalar1=0.0)
+                for start, values in ((NU + D, x), (0, x[:, :, D - NU : D])):
+                    nc.vector.tensor_scalar(
+                        out=x2[grp][:, :, start : start + values.shape[2]],
+                        in0=values,
+                        scalar1=-1.0,
+                        scalar2=0.0,
+                        op0=ALU.mult,
+                        op1=ALU.max,
+                    )
 
         def signs(grp):
             x = k_rows[grp][:, :, KEY_FRONT:]
@@ -786,11 +796,11 @@ def tile_armtapproach_pa_kernel(
                 if step + 2 < pairs:
                     products(step + 2, 1)
                 quantise_next()
-                if step + 1 < pairs:
-                    band_products(step + 1, 0)
                 advance_unit()
                 if working:
                     v_sums((grp, h2, 1))
+                if step + 1 < pairs:
+                    band_products(step + 1, 0)
                 if step < 3:
                     advance_unit()
                 if second:

@@ -165,6 +165,10 @@ def tile_armtapproach_pa_kernel(
         minus_half = keep.tile([P, 2], F32)
         nc.gpsimd.memset(minus_half[:], -0.5)
 
+        def load_table():
+            first = keep.tile([P, 1], F32)
+            nc.scalar.activation(out=first[:], in_=minus_half[:, 0:1], func=ACT.Sigmoid)
+
         def load_keys(grp):
             c, sg = divmod(grp, S_PASSES)
             k_rows[grp] = feat.tile([P, PACK, KEY_PITCH], BF16, name="k_rows")
@@ -698,6 +702,7 @@ def tile_armtapproach_pa_kernel(
             done["rows"] += rows
 
         with tc.manual_schedule():
+            load_table()
             load_keys(0)
             load_norm(0)
             load_unit(0)

from contextlib import ExitStack

import concourse.mybir as mybir
from concourse.masks import make_identity

F32 = mybir.dt.float32
BF16 = mybir.dt.bfloat16
U32 = mybir.dt.uint32
U8 = mybir.dt.uint8
FP8X4 = mybir.dt.float8_e4m3fn_x4
ACT = mybir.ActivationFunctionType
ALU = mybir.AluOpType

P = 128
PACK = 4
K_PASS = P * PACK
BANK = 512

S = 1024
HID = 1024
D = 256
H = 4
HKV = 2
PAIR = H // HKV
NU = 3
X2 = 2 * D
F = NU * X2
EPS = 1e-8
TINY = 1e-12

S_TILES = S // P
S_PASSES = S // K_PASS
HID_PASSES = HID // K_PASS
F_PASSES = F // K_PASS
REACH = P - NU
FULL_TILES = X2 // REACH
REST = X2 - FULL_TILES * REACH
X2_TILES = FULL_TILES + 1
W_ROWS = HKV * D + HID
W_TILES = W_ROWS // P
V_TILES = HKV * D // P
ROW_UNIT = 256
KEY_FRONT = 16
KEY_PITCH = KEY_FRONT + D

FLOPS = 2 * S * HID * W_ROWS + 2 * 2 * H * S * F * D


def quantise(nc, grouped, codes, scales):
    nc.vector.quantize_mx(
        out=codes.bitcast(FP8X4),
        scales=scales,
        in_=grouped.rearrange("p c t -> p (c t)"),
    )


def mx_group(nc, bank, passes, lhs_codes, lhs_scales, rhs_codes, rhs_scales):
    for g in range(passes):
        nc.tensor.matmul_mx(
            out=bank,
            lhsT=lhs_codes(g).bitcast(FP8X4),
            lhsT_scale=lhs_scales(g),
            rhs=rhs_codes(g).bitcast(FP8X4),
            rhs_scale=rhs_scales(g),
            start=(g == 0),
            stop=(g == passes - 1),
        )


def interleave(engine_copy, grouped, planes):
    engine_copy(
        out=grouped.rearrange("p (n i) t -> p n t i", i=8),
        in_=planes.rearrange("p t (n i) -> p n t i", i=8),
    )


def tile_armtapproach_pa_kernel(
    tc, hidden_states, k, Wv, bv, Wmb, bmb, memory, norm, out
):
    nc = tc.nc
    with ExitStack() as whole:
        keep = whole.enter_context(tc.tile_pool(name="keep", bufs=1))
        feat = whole.enter_context(tc.tile_pool(name="feat", bufs=2))
        stage = whole.enter_context(tc.tile_pool(name="stage", bufs=2))
        late = whole.enter_context(tc.tile_pool(name="late", bufs=2))
        banks = whole.enter_context(tc.psum_pool(name="banks", bufs=3))

        ident = keep.tile([P, P], F32)
        make_identity(nc, ident[:])
        ident_bf = keep.tile([P, P], BF16)
        make_identity(nc, ident_bf[:])

        biases = keep.tile([P, W_TILES], F32)

        hs_codes = keep.tile([P, HID_PASSES, S], U32, align_bytes=64)
        hs_scales = keep.tile([P, HID_PASSES, S], U8, align_bytes=64)
        w_codes = keep.tile([P, W_ROWS // ROW_UNIT, HID_PASSES, ROW_UNIT], U32, align_bytes=64)
        w_scales = keep.tile([P, W_ROWS // ROW_UNIT, HID_PASSES, ROW_UNIT], U8, align_bytes=64)
        mem_codes = keep.tile([P, HKV, F_PASSES, PAIR * D], U32, align_bytes=64)
        mem_scales = keep.tile([P, HKV, F_PASSES, PAIR * D], U8, align_bytes=64)
        mkS_codes = keep.tile([P, HKV, S_PASSES, F], U32, align_bytes=64)
        mkS_scales = keep.tile([P, HKV, S_PASSES, F], U8, align_bytes=64)
        wmv_codes = keep.tile([P, S_PASSES, H * D], U32, align_bytes=64)
        wmv_scales = keep.tile([P, S_PASSES, H * D], U8, align_bytes=64)

        band = keep.tile([P, H, FULL_TILES, REACH], BF16)
        band_rest = keep.tile([P, H, REST], BF16)
        norm_w = feat.tile([P, H, NU, X2], BF16, tag="mk_planes")

        def load_norm(c):
            heads = slice(PAIR * c, PAIR * (c + 1))
            nc.sync.dma_start(
                out=norm_w[:, heads].rearrange("p h j i -> p (h j) i"),
                in_=norm[heads, :].rearrange("h (j i) -> (h j) i", j=NU).partition_broadcast(P),
            )

        def build_band(c, j):
            heads = slice(PAIR * c, PAIR * (c + 1))
            full = norm_w[:, heads, j - 1, 0 : X2 - REST].rearrange("p h (m n) -> p h m n", n=REACH)
            full_diagonal = (
                ident_bf[:, NU - j : NU - j + REACH]
                .unsqueeze(1)
                .unsqueeze(1)
                .to_broadcast([P, PAIR, FULL_TILES, REACH])
            )
            if j == 1:
                nc.vector.tensor_tensor(out=band[:, heads], in0=full, in1=full_diagonal, op=ALU.mult)
            else:
                term = feat.tile([P, PAIR, FULL_TILES, REACH], BF16, bufs=1)
                nc.vector.tensor_tensor(out=term[:], in0=full, in1=full_diagonal, op=ALU.mult)
                nc.vector.tensor_tensor(out=band[:, heads], in0=band[:, heads], in1=term[:], op=ALU.add)

        def build_rest(c, j):
            heads = slice(PAIR * c, PAIR * (c + 1))
            rest = norm_w[:, heads, j - 1, X2 - REST : X2]
            rest_diagonal = ident_bf[:, P - REST - j : P - j].unsqueeze(1).to_broadcast([P, PAIR, REST])
            if j == 1:
                nc.vector.tensor_tensor(
                    out=band_rest[:, heads], in0=rest, in1=rest_diagonal, op=ALU.mult
                )
            else:
                rest_term = feat.tile([P, PAIR, REST], BF16, bufs=1)
                nc.vector.tensor_tensor(out=rest_term[:], in0=rest, in1=rest_diagonal, op=ALU.mult)
                nc.vector.tensor_tensor(
                    out=band_rest[:, heads], in0=band_rest[:, heads], in1=rest_term[:], op=ALU.add
                )

        bias_rows = keep.tile([P, P], BF16)

        def load_biases():
            nc.gpsimd.memset(bias_rows[:], 0.0)
            nc.sync.dma_start(out=bias_rows[0:V_TILES, :], in_=bv.rearrange("(m p) -> m p", p=P))
            nc.sync.dma_start(
                out=bias_rows[V_TILES:W_TILES, :], in_=bmb.rearrange("(m p) -> m p", p=P)
            )

        def flip_biases():
            bias_bank = banks.tile([P, X2_TILES, P], BF16, tag="flipped")
            nc.tensor.transpose(bias_bank[:, 0, :], bias_rows[:], ident_bf[:])
            nc.scalar.copy(out=biases[:], in_=bias_bank[:, 0, 0:W_TILES])

        k_rows, half_signs, same_sign, x2, half_phi, scale_up, dots = {}, {}, {}, {}, {}, {}, {}
        x2T, inner_sums, mk_planes, mkT_grouped, mkT_codes, mkT_scales = {}, {}, {}, {}, {}, {}
        sum_sq, neg_inv_denom = {}, {}
        minus_half = keep.tile([P, 2], F32)
        nc.gpsimd.memset(minus_half[:], -0.5)

        def load_table():
            first = keep.tile([P, 1], F32)
            nc.scalar.activation(out=first[:], in_=minus_half[:, 0:1], func=ACT.Sigmoid)

        def load_keys(grp):
            c, sg = divmod(grp, S_PASSES)
            k_rows[grp] = feat.tile([P, PACK, KEY_PITCH], BF16, name="k_rows")
            for u in range(2):
                nc.sync.dma_start(
                    out=k_rows[grp][:, 2 * u : 2 * u + 2, KEY_FRONT:],
                    in_=k[c, sg * K_PASS + u * 2 * P : sg * K_PASS + (u + 1) * 2 * P, :].rearrange(
                        "(p e) d -> p e d", e=2
                    ),
                )

        def relu_halves(grp):
            x = k_rows[grp][:, :, KEY_FRONT:]
            x2[grp] = feat.tile([P, PACK, NU + X2], BF16, name="x2")
            if grp < 2:
                nc.scalar.activation(out=x2[grp][:, :, NU : NU + D], in_=x, func=ACT.Relu)
                for start, values in ((NU + D, x), (0, x[:, :, D - NU : D])):
                    nc.scalar.activation(
                        out=x2[grp][:, :, start : start + values.shape[2]],
                        in_=values,
                        func=ACT.Relu,
                        scale=-1.0,
                    )
            else:
                nc.vector.tensor_scalar_max(out=x2[grp][:, :, NU : NU + D], in0=x, scalar1=0.0)
                for start, values in ((NU + D, x), (0, x[:, :, D - NU : D])):
                    nc.vector.tensor_scalar(
                        out=x2[grp][:, :, start : start + values.shape[2]],
                        in0=values,
                        scalar1=-1.0,
                        scalar2=0.0,
                        op0=ALU.mult,
                        op1=ALU.max,
                    )

        def signs(grp):
            x = k_rows[grp][:, :, KEY_FRONT:]
            nc.scalar.mul(
                out=k_rows[grp][:, :, KEY_FRONT - NU : KEY_FRONT], in_=x[:, :, D - NU : D], mul=-1.0
            )
            half_signs[grp] = feat.tile([P, PACK, D], BF16, name="half_signs", tag="half_signs")
            nc.vector.tensor_scalar(
                out=half_signs[grp][:],
                in0=x,
                scalar1=0.0,
                scalar2=-0.5,
                op0=ALU.is_ge,
                op1=ALU.add,
            )

        def compare_signs(grp):
            same_sign[grp] = feat.tile([P, PACK, NU, D], BF16, bufs=1, name="same_sign")
            for j in range(1, NU + 1):
                nc.vector.tensor_tensor(
                    out=same_sign[grp][:, :, j - 1, :],
                    in0=k_rows[grp][:, :, KEY_FRONT - j : KEY_FRONT - j + D],
                    in1=half_signs[grp][:],
                    op=ALU.mult,
                )

        def products(pair, b):
            grp, u = divmod(pair, 2)
            if b == 0:
                half_phi[pair] = feat.tile(
                    [P, 2, NU, D], F32, bufs=3, name="half_phi", tag="half_phi"
                )
            nc.vector.scalar_tensor_tensor(
                out=half_phi[pair][:, b],
                in0=same_sign[grp][:, 2 * u + b],
                scalar=0.0,
                in1=k_rows[grp][:, 2 * u + b, KEY_FRONT:].unsqueeze(1).to_broadcast([P, NU, D]),
                op0=ALU.max,
                op1=ALU.mult,
            )

        def square_sums(pair, b):
            if b == 0:
                sum_sq[pair] = feat.tile([P, 2], F32, name="sum_sq")
            squares = feat.tile([P, NU * D], BF16, bufs=1)
            nc.scalar.activation(
                out=squares[:],
                in_=half_phi[pair][:, b].rearrange("p j i -> p (j i)"),
                func=ACT.Square,
                accum_out=sum_sq[pair][:, b : b + 1],
            )

        def inverse_norms(pair):
            grp, u = divmod(pair, 2)
            if u == 0:
                scale_up[grp] = feat.tile([P, 2, PACK], F32, name="scale_up")
            up = scale_up[grp][:, 0, 2 * u : 2 * u + 2]
            down = scale_up[grp][:, 1, 2 * u : 2 * u + 2]
            nc.gpsimd.tensor_scalar(
                out=sum_sq[pair][:],
                in0=sum_sq[pair][:],
                scalar1=TINY * TINY / 4.0,
                scalar2=None,
                op0=ALU.max,
            )
            nc.gpsimd.tensor_tensor(out=up, in0=sum_sq[pair][:], in1=minus_half[:], op=ALU.pow)
            nc.gpsimd.tensor_scalar(
                out=down, in0=up, scalar1=-1.0, scalar2=0.0, op0=ALU.mult, op1=ALU.add
            )

        def flip_x2(pair, b):
            grp, u = divmod(pair, 2)
            if b == 0:
                x2T[pair] = feat.tile([P, 2, X2_TILES, P], BF16, name="x2T")
            x2T_bank = banks.tile([P, X2_TILES, P], BF16, tag="flipped")
            for m in range(X2_TILES):
                start = m * REACH if m < FULL_TILES else NU + X2 - P
                nc.tensor.transpose(
                    x2T_bank[:, m, :], x2[grp][:, 2 * u + b, start : start + P], ident_bf[:]
                )
            nc.scalar.copy(out=x2T[pair][:, b], in_=x2T_bank[:])

        def band_products(pair, b):
            c = pair // (2 * S_PASSES)
            for h2 in range(PAIR):
                sums = banks.tile([P, X2], F32, bufs=2, tag="inner_sums")
                for m in range(X2_TILES):
                    if m < FULL_TILES:
                        out_cols = slice(m * REACH, (m + 1) * REACH)
                        weights = band[:, PAIR * c + h2, m, :]
                    else:
                        out_cols = slice(X2 - REST, X2)
                        weights = band_rest[:, PAIR * c + h2, :]
                    nc.tensor.matmul(
                        out=sums[:, out_cols],
                        lhsT=x2T[pair][:, b, m, :],
                        rhs=weights,
                        start=True,
                        stop=True,
                    )
                inner_sums[(pair, b, h2)] = sums

        def dot_products(pair, b):
            grp, u = divmod(pair, 2)
            if u == 0 and b == 0:
                dots[grp] = feat.tile([P, PACK, PAIR], F32, name="dots")
            for h2 in range(PAIR):
                weighted = feat.tile([P, X2], F32, tag="weighted")
                nc.vector.scalar_tensor_tensor(
                    out=weighted[:],
                    in0=inner_sums[(pair, b, h2)][:],
                    scalar=1.0,
                    in1=x2[grp][:, 2 * u + b, NU : NU + X2],
                    op0=ALU.mult,
                    op1=ALU.mult,
                    accum_out=dots[grp][:, 2 * u + b, h2 : h2 + 1],
                )

        def round_plane(pair, b):
            grp, u = divmod(pair, 2)
            if u == 0 and b == 0:
                mk_planes[grp] = feat.tile([P, PACK, F], BF16, name="mk_planes", tag="mk_planes")
            mk = mk_planes[grp][:, 2 * u + b, :].rearrange("p (j s x i) -> p s x j i", s=2, x=2, j=NU)
            for sign in range(2):
                nc.vector.tensor_scalar(
                    out=mk[:, sign],
                    in0=half_phi[pair][:, b].rearrange("p j (x i) -> p x j i", x=2),
                    scalar1=scale_up[grp][:, sign, 2 * u + b : 2 * u + b + 1],
                    scalar2=0.0,
                    op0=ALU.mult,
                    op1=ALU.max,
                )

        def finish_denominators(grp, part):
            d = dots[grp][:]
            if part == 0:
                nc.vector.tensor_tensor(
                    out=d,
                    in0=d,
                    in1=scale_up[grp][:, 0, :].unsqueeze(2).to_broadcast([P, PACK, PAIR]),
                    op=ALU.mult,
                )
            elif part == 1:
                nc.vector.tensor_scalar(
                    out=d, in0=d, scalar1=-0.5, scalar2=-EPS, op0=ALU.mult, op1=ALU.add
                )
            else:
                nc.vector.reciprocal(out=d, in_=d)

        def spread_denominators(grp, h2):
            if h2 == 0:
                if grp + 1 < HKV * S_PASSES:
                    spread_tile = late.tile([P, PAIR, K_PASS], F32, bufs=1)
                else:
                    spread_tile = stage.tile(
                        [P, PAIR, K_PASS], F32, align_bytes=64, name="spread_last", tag="grouped"
                    )
                neg_inv_denom[grp] = spread_tile
            spread = banks.tile([P, 2, 2, P], F32, tag="flipped")
            for u in range(2):
                for e in range(2):
                    nc.tensor.transpose(
                        spread[:, u, e, :],
                        dots[grp][:, 2 * u + e, h2 : h2 + 1].to_broadcast([P, P]),
                        ident[:],
                    )
            nc.scalar.copy(
                out=neg_inv_denom[grp][:, h2, :].rearrange("q (u p e) -> q u p e", u=2, e=2),
                in_=spread[:].rearrange("q u e p -> q u p e"),
            )

        def transpose_features(pair, g):
            grp, a = divmod(pair, 2)
            if a == 0 and g == 0:
                mkT_grouped[grp] = feat.tile(
                    [P, F_PASSES, K_PASS, PACK],
                    BF16,
                    bufs=1,
                    align_bytes=64,
                    name="mkT_grouped",
                    tag="mkT_grouped",
                )
            mkT_words = mkT_grouped[grp][:, g].bitcast(F32)
            flipped = banks.tile([P, 2, 2, P], F32, tag="flipped")
            for b in range(2):
                plane_words = mk_planes[grp][:, 2 * a + b, :].bitcast(F32)
                for u in range(2):
                    w0 = (2 * g + u) * P
                    nc.tensor.transpose(flipped[:, b, u, :], plane_words[:, w0 : w0 + P], ident[:])
            nc.scalar.copy(
                out=mkT_words[:, 2 * a * P : (2 * a + 2) * P, :].rearrange("q (r b) u -> q r b u", b=2),
                in_=flipped[:].rearrange("q b u r -> q r b u"),
            )

        def quantise_features(grp, passes):
            if grp not in mkT_codes:
                mkT_codes[grp] = late.tile(
                    [P, F_PASSES, K_PASS], U32, align_bytes=64, name="mkT_codes"
                )
                mkT_scales[grp] = late.tile(
                    [P, F_PASSES, K_PASS], U8, align_bytes=64, name="mkT_scales"
                )
            quantise(
                nc,
                mkT_grouped[grp][:, passes].rearrange("p g c t -> p (g c) t"),
                mkT_codes[grp][:, passes].rearrange("p g c -> p (g c)"),
                mkT_scales[grp][:, passes].rearrange("p g c -> p (g c)"),
            )

        mkS_grouped = {}

        def interleave_tokens(grp, g, engine_copy):
            mkS_grouped[(grp, g)] = stage.tile(
                [P, X2, PACK], BF16, align_bytes=64, name="mkS_grouped"
            )
            interleave(
                engine_copy, mkS_grouped[(grp, g)][:], mk_planes[grp][:, :, g * X2 : (g + 1) * X2]
            )

        def quantise_tokens(grp, g):
            c, sg = divmod(grp, S_PASSES)
            f_cols = slice(g * X2, (g + 1) * X2)
            quantise(
                nc, mkS_grouped[(grp, g)][:], mkS_codes[:, c, sg, f_cols], mkS_scales[:, c, sg, f_cols]
            )

        def hs_unit(n):
            r_cols = slice(n * ROW_UNIT, (n + 1) * ROW_UNIT)
            return (True, hidden_states[r_cols, :], hs_codes[:, :, r_cols], hs_scales[:, :, r_cols])

        def w_unit(source, n, unit):
            r_rows = slice(n * ROW_UNIT, (n + 1) * ROW_UNIT)
            return (True, source[r_rows, :], w_codes[:, unit], w_scales[:, unit])

        def wv_unit(c):
            return w_unit(Wv, c, c)

        def wmb_unit(h):
            return w_unit(Wmb, h, HKV + h)

        def mem_unit(c, g):
            return (
                False,
                memory[PAIR * c : PAIR * (c + 1), g * K_PASS : (g + 1) * K_PASS, :],
                mem_codes[:, c, g, :],
                mem_scales[:, c, g, :],
            )

        units = [hs_unit(0), mem_unit(0, 0), hs_unit(1), mem_unit(0, 1), wv_unit(0), mem_unit(0, 2)]
        units += [wmb_unit(0), wmb_unit(1), hs_unit(2), hs_unit(3), mem_unit(1, 0), wv_unit(1)]
        units += [mem_unit(1, 1), wmb_unit(2), mem_unit(1, 2), wmb_unit(3)]
        raw, grouped = {}, {}

        def load_unit(n):
            if units[n][0]:
                raw[n] = stage.tile([P, ROW_UNIT // P, HID], BF16, name="raw", tag="raw")
                nc.sync.dma_start(
                    out=raw[n][:], in_=units[n][1].rearrange("(rt p) k -> p rt k", p=P)
                )
            else:
                raw[n] = stage.tile([P, PAIR, PACK, D], BF16, name="raw", tag="raw")
                for h2 in range(PAIR):
                    nc.sync.dma_start(
                        out=raw[n][:, h2].rearrange("q (u e) d -> q u (e d)", u=2),
                        in_=units[n][1][h2].rearrange("(u q e) d -> q u (e d)", u=2, e=2),
                    )

        def lay_out_unit(n):
            if units[n][0]:
                grouped[n] = stage.tile(
                    [P, HID_PASSES, ROW_UNIT, PACK],
                    BF16,
                    align_bytes=64,
                    name="grouped",
                    tag="grouped",
                )
                grouped_words = grouped[n][:].bitcast(F32)
                for rt in range(ROW_UNIT // P):
                    raw_words = raw[n][:, rt, :].bitcast(F32)
                    flipped = banks.tile([P, HID_PASSES, 2, P], F32, tag="flipped")
                    for g in range(HID_PASSES):
                        for u in range(2):
                            w0 = (2 * g + u) * P
                            nc.tensor.transpose(flipped[:, g, u, :], raw_words[:, w0 : w0 + P], ident[:])
                    nc.scalar.copy(
                        out=grouped_words[:, :, rt * P : (rt + 1) * P, :],
                        in_=flipped[:].rearrange("q g u r -> q g r u"),
                    )
            else:
                grouped[n] = stage.tile([P, PAIR, D, PACK], BF16, align_bytes=64, name="grouped", tag="grouped")
                for h2 in range(PAIR):
                    woven = banks.tile([P, D, PACK], BF16, tag="flipped")
                    for u in range(2):
                        nc.tensor.matmul(
                            out=woven[:, :, 2 * u : 2 * u + 2].rearrange("q d e -> q e d"),
                            lhsT=ident_bf[:],
                            rhs=raw[n][:, h2, 2 * u : 2 * u + 2, :],
                            start=True,
                            stop=True,
                        )
                    nc.scalar.copy(out=grouped[n][:, h2], in_=woven[:])

        def quantise_unit(n):
            rows, source, codes, scales = units[n]
            if not rows:
                quantise(nc, grouped[n][:].rearrange("q h d t -> q (h d) t"), codes, scales)
            elif source.shape[1] == HID and n in (0, 2, 8, 9):
                for g in range(HID_PASSES):
                    quantise(nc, grouped[n][:, g], codes[:, g, :], scales[:, g, :])
            else:
                quantise(
                    nc,
                    grouped[n][:].rearrange("q g r t -> q (g r) t"),
                    codes.rearrange("q g r -> q (g r)"),
                    scales.rearrange("q g r -> q (g r)"),
                )

        v_bank, mb_bank, num_bank, gate, diff = {}, {}, {}, {}, {}
        wmv_grouped, wmvT = {}, {}

        def project(bank, grp, m):
            sg = grp % S_PASSES
            unit, part = divmod(m, ROW_UNIT // P)
            o_cols = slice(part * P, (part + 1) * P)
            s_cols = slice(sg * K_PASS, (sg + 1) * K_PASS)
            mx_group(
                nc,
                bank,
                HID_PASSES,
                lambda g: w_codes[:, unit, g, o_cols],
                lambda g: w_scales[:, unit, g, o_cols],
                lambda g: hs_codes[:, g, s_cols],
                lambda g: hs_scales[:, g, s_cols],
            )

        def num_sums(block):
            grp, h2, dh = block
            c = grp // S_PASSES
            num_bank[block] = banks.tile([P, K_PASS], F32, bufs=1, name="num_bank", tag="num_bank")
            d_cols = slice(h2 * D + dh * P, h2 * D + (dh + 1) * P)
            mx_group(
                nc,
                num_bank[block][:],
                F_PASSES,
                lambda g: mem_codes[:, c, g, d_cols],
                lambda g: mem_scales[:, c, g, d_cols],
                lambda g: mkT_codes[grp][:, g, :],
                lambda g: mkT_scales[grp][:, g, :],
            )

        def mb_sums(block):
            grp, h2, dh = block
            mb_bank[block] = banks.tile([P, K_PASS], F32, bufs=1, name="mb_bank", tag="mb_bank")
            project(
                mb_bank[block][:], grp, V_TILES + (PAIR * (grp // S_PASSES) + h2) * (D // P) + dh
            )

        def v_sums(block):
            grp, h2, dh = block
            v_bank[block] = banks.tile([P, K_PASS], F32, bufs=1, name="v_bank", tag="v_bank")
            project(v_bank[block][:], grp, grp // S_PASSES * (D // P) + dh)

        def gate_values(block):
            grp, h2, dh = block
            mb_tile = V_TILES + (PAIR * (grp // S_PASSES) + h2) * (D // P) + dh
            gate[block] = late.tile([P, K_PASS], F32, name="gate")
            nc.scalar.activation(
                out=gate[block][:],
                in_=mb_bank[block][:],
                func=ACT.Sigmoid,
                bias=biases[:, mb_tile : mb_tile + 1],
            )

        def scale_num(block):
            grp, h2, dh = block
            diff[block] = late.tile([P, K_PASS], F32, name="diff")
            nc.vector.tensor_tensor(
                out=diff[block][:],
                in0=num_bank[block][:],
                in1=neg_inv_denom[grp][:, h2, :],
                op=ALU.mult,
            )

        def write_values(block):
            grp, h2, dh = block
            v_tile = grp // S_PASSES * (D // P) + dh
            if dh == 0:
                wmvT[(grp, h2)] = late.tile([P, D // P, K_PASS], BF16, name="wmvT")
            nc.vector.scalar_tensor_tensor(
                out=diff[block][:],
                in0=v_bank[block][:],
                scalar=biases[:, v_tile : v_tile + 1],
                in1=diff[block][:],
                op0=ALU.add,
                op1=ALU.add,
            )
            nc.gpsimd.tensor_tensor(
                out=wmvT[(grp, h2)][:, dh, :], in0=diff[block][:], in1=gate[block][:], op=ALU.mult
            )

        def turn_values(grp, h2):
            wmv_grouped[(grp, h2)] = late.tile(
                [P, D, PACK], BF16, align_bytes=64, name="wmv_grouped"
            )
            flipped = banks.tile([P, D // P, 2, P], F32, tag="flipped")
            for dh in range(D // P):
                raw_words = wmvT[(grp, h2)][:, dh, :].bitcast(F32)
                for u in range(2):
                    nc.tensor.transpose(flipped[:, dh, u, :], raw_words[:, u * P : (u + 1) * P], ident[:])
            nc.scalar.copy(
                out=wmv_grouped[(grp, h2)][:].bitcast(F32).rearrange("p (m d) u -> p m d u", m=D // P),
                in_=flipped[:].rearrange("p m u d -> p m d u"),
            )

        def quantise_values(grp, h2):
            c, sg = divmod(grp, S_PASSES)
            h_cols = slice((PAIR * c + h2) * D, (PAIR * c + h2 + 1) * D)
            quantise(
                nc, wmv_grouped[(grp, h2)][:], wmv_codes[:, sg, h_cols], wmv_scales[:, sg, h_cols]
            )

        old, delta, new = {}, {}, {}

        def rows_of(tensor, n):
            h, r = divmod(n, F // (2 * P))
            return tensor[h, r * 2 * P : (r + 1) * 2 * P, :].rearrange("(t f) d -> f t d", f=P)

        def load_old(c):
            if c == 0:
                for h2 in range(PAIR):
                    head_rows = stage.tile([P, F // P, D], BF16, tag="raw")
                    old[h2] = head_rows[:]
            else:
                last_pair = feat.tile([P, PAIR, F // P, D], BF16, tag="mk_planes")
                for h2 in range(PAIR):
                    old[PAIR * c + h2] = last_pair[:, h2]
            for h in range(PAIR * c, PAIR * (c + 1)):
                nc.sync.dma_start(out=old[h], in_=memory[h].rearrange("(r f) d -> f r d", f=P))

        def write_sums(n):
            h, r = divmod(n, F // (2 * P))
            c = h // PAIR
            h_cols = slice(h * D, (h + 1) * D)
            if n % 2 == 0:
                delta[n] = banks.tile([P, 2, D], F32, bufs=2, name="delta", tag="inner_sums")
            else:
                delta[n] = banks.tile([P, 2, D], F32, name="delta", tag="flipped")
            for t in range(2):
                f_cols = slice((2 * r + t) * P, (2 * r + t + 1) * P)
                mx_group(
                    nc,
                    delta[n][:, t, :],
                    S_PASSES,
                    lambda g: mkS_codes[:, c, g, f_cols],
                    lambda g: mkS_scales[:, c, g, f_cols],
                    lambda g: wmv_codes[:, g, h_cols],
                    lambda g: wmv_scales[:, g, h_cols],
                )

        def write_rows(n):
            h, r = divmod(n, F // (2 * P))
            if n % NU == 0:
                new[n // NU] = feat.tile([P, NU, 2, D], F32, bufs=3, name="new", tag="half_phi")
            new_tile = new[n // NU][:, n % NU]
            nc.vector.tensor_tensor(out=new_tile, in0=delta[n][:], in1=old[h][:, 2 * r : 2 * r + 2, :], op=ALU.add)
            nc.sync.dma_start(out=rows_of(out, n), in_=new_tile)

        pairs = 2 * HKV * S_PASSES
        groups = HKV * S_PASSES
        done = {"units": 0, "quantised": 0, "sums": 0, "rows": 0}

        def advance_unit():
            n = done["units"]
            if n < len(units):
                lay_out_unit(n)
                if n + 2 < len(units):
                    load_unit(n + 2)
                done["units"] = n + 1

        def quantise_next():
            n = done["quantised"]
            if n < done["units"]:
                quantise_unit(n)
                done["quantised"] = n + 1

        def block_sums(block):
            num_sums(block)
            mb_sums(block)
            v_sums(block)

        def write_next(sums, rows):
            for n in range(done["sums"], done["sums"] + sums):
                write_sums(n)
            done["sums"] += sums
            for n in range(done["rows"], done["rows"] + rows):
                write_rows(n)
            done["rows"] += rows

        with tc.manual_schedule():
            load_table()
            load_keys(0)
            load_norm(0)
            load_unit(0)
            load_unit(1)
            load_keys(1)
            load_norm(1)
            load_biases()
            signs(0)
            relu_halves(0)
            compare_signs(0)
            flip_x2(0, 0)
            products(0, 0)
            flip_x2(0, 1)
            products(0, 1)
            square_sums(0, 0)
            advance_unit()
            for j in range(1, NU + 1):
                build_band(0, j)
                build_rest(0, j)
            square_sums(0, 1)
            inverse_norms(0)
            advance_unit()
            flip_biases()
            band_products(0, 0)
            quantise_next()
            products(1, 0)
            products(1, 1)
            signs(1)
            for step in range(pairs):
                part = step - 3
                grp, h2 = divmod(part, PAIR)
                working = part >= 0
                ready, second = divmod(step - 2, 2)
                fresh = ready >= 0 and second == 0
                if step % 2 == 0 and step + 4 < pairs:
                    load_keys(step // 2 + 2)
                if part > 0:
                    write_values((*divmod(part - 1, PAIR), 1))
                dot_products(step, 0)
                if step + 1 < pairs:
                    flip_x2(step + 1, 0)
                if working:
                    num_sums((grp, h2, 0))
                if step > 0:
                    transpose_features(step - 1, 0)
                if working:
                    mb_sums((grp, h2, 0))
                    gate_values((grp, h2, 0))
                if step + 1 < pairs:
                    square_sums(step + 1, 0)
                quantise_next()
                if step % 2 == 0 and step + 2 < pairs:
                    compare_signs(step // 2 + 1)
                if step == pairs - 1:
                    load_old(0)
                if step < NU:
                    build_band(1, step + 1)
                    build_rest(1, step + 1)
                band_products(step, 1)
                advance_unit()
                if working:
                    v_sums((grp, h2, 0))
                if ready >= 0:
                    if not second and ready > 0:
                        quantise_tokens(ready - 1, 2)
                    interleave_tokens(
                        ready,
                        2 if second else 0,
                        nc.vector.tensor_copy if second and ready == 0 else nc.scalar.copy,
                    )
                if step > 0:
                    transpose_features(step - 1, 1)
                if step % 2 == 0 and step + 2 < pairs:
                    relu_halves(step // 2 + 1)
                if working:
                    scale_num((grp, h2, 0))
                if part > 1:
                    quantise_values(*divmod(part - 2, PAIR))
                if step + 2 < pairs:
                    products(step + 2, 0)
                if working:
                    write_values((grp, h2, 0))
                    num_sums((grp, h2, 1))
                dot_products(step, 1)
                if step + 1 < pairs:
                    flip_x2(step + 1, 1)
                if working:
                    mb_sums((grp, h2, 1))
                if step > 0:
                    transpose_features(step - 1, 2)
                if step + 1 < pairs:
                    square_sums(step + 1, 1)
                    inverse_norms(step + 1)
                if working:
                    gate_values((grp, h2, 1))
                if step + 2 < pairs:
                    products(step + 2, 1)
                quantise_next()
                advance_unit()
                if working:
                    v_sums((grp, h2, 1))
                if step + 1 < pairs:
                    band_products(step + 1, 0)
                if step < 3:
                    advance_unit()
                if second:
                    finish_denominators(step // 2, 0)
                round_plane(step, 0)
                if second:
                    finish_denominators(step // 2, 1)
                if working:
                    scale_num((grp, h2, 1))
                if second:
                    finish_denominators(step // 2, 2)
                round_plane(step, 1)
                if part > 0:
                    turn_values(*divmod(part - 1, PAIR))
                if fresh:
                    for h in range(PAIR):
                        spread_denominators(ready, h)
                    for passes in (slice(0, 2), slice(2, 3)):
                        quantise_features(ready, passes)
                    quantise_tokens(ready, 0)
                    interleave_tokens(ready, 1, nc.scalar.copy)
                elif ready >= 0 and step + 1 < pairs:
                    quantise_tokens(ready, 1)
                if step % 2 == 1 and step + 3 < pairs:
                    signs(step // 2 + 2)
                if step < 4:
                    quantise_next()
            load_old(1)
            last = groups - 1
            blocks = [(grp, h2, dh) for grp, h2 in ((last - 1, 1), (last, 0), (last, 1)) for dh in range(2)]
            num_sums(blocks[0])
            for g in range(F_PASSES):
                transpose_features(pairs - 1, g)
            mb_sums(blocks[0])
            v_sums(blocks[0])
            write_values((last - 1, 0, 1))
            quantise_values(last - 2, 1)
            for h2 in range(PAIR):
                spread_denominators(last, h2)
            gate_values(blocks[0])
            for n, block in enumerate(blocks):
                scale_num(block)
                if n == 0:
                    quantise_tokens(last - 1, 1)
                    quantise_tokens(last - 1, 2)
                    for passes in (slice(0, 2), slice(2, 3)):
                        quantise_features(last, passes)
                if n == 1:
                    turn_values(last - 1, 0)
                if n == 3:
                    turn_values(last - 1, 1)
                if n == 5:
                    turn_values(last, 0)
                if n + 1 < len(blocks):
                    block_sums(blocks[n + 1])
                    gate_values(blocks[n + 1])
                write_values(block)
                write_next(2, 2 if n > 0 else 0)
                if n < F_PASSES:
                    interleave_tokens(last, n, nc.scalar.copy)
                if 0 < n <= F_PASSES:
                    quantise_tokens(last, n - 1)
                if n == 1:
                    quantise_values(last - 1, 0)
                if n == 3:
                    quantise_values(last - 1, 1)
                if n == 5:
                    quantise_values(last, 0)
            turn_values(last, 1)
            write_next(3, 4)
            quantise_values(last, 1)
            for n in range(9):
                write_next(1, 1)
            write_next(0, 1)
